import numpy as np
import ml_dtypes


def mxq(x, axis, fmt="e4m3"):
    dtype, down = {"e4m3": (ml_dtypes.float8_e4m3fn, 7), "e5m2": (ml_dtypes.float8_e5m2, 14)}[fmt]
    v = np.moveaxis(np.asarray(x, np.float32).astype(ml_dtypes.bfloat16).astype(np.float64), axis, -1)
    blocks = v.reshape(v.shape[:-1] + (-1, 32))
    amax = np.abs(blocks).max(-1, keepdims=True)
    byte = np.maximum(np.where(amax > 0, np.frexp(amax)[1] - 1 + 127, 0) - down, 1)
    scale = np.exp2(byte - 127.0)
    codes = (blocks / scale).astype(np.float32).astype(dtype).astype(np.float64)
    return np.moveaxis((codes * scale).reshape(v.shape), -1, axis)


WIDE = False


def mx_kscale(k):
    if not WIDE:
        return np.ones(k)
    levels = np.array([10, -10, 5, -5, 0])
    a = np.random.permutation(np.resize(levels, k // 512 * 4)).reshape(k // 512, 4)
    idx = np.arange(k)
    return np.exp2(a[idx // 512, idx % 128 // 32])


BF16 = ml_dtypes.bfloat16


def bf(x):
    return np.asarray(x, np.float32).astype(BF16)


def f64(x):
    return np.asarray(x).astype(np.float64)


N, B, C, E, D, R = 1024, 16384, 512, 128, 128, 8
SPREAD = 2.0


def spread(z, lat):
    return (z[:, :, None] * lat[None, :, :]).sum(1)


def setup_inputs():
    s = mx_kscale(C)
    lat = np.random.standard_normal((R, E)) * SPREAD
    return {
        "source": bf(np.random.standard_normal((N, C)) * s),
        "target": bf(spread(np.random.standard_normal((B, R)), lat)),
        "k_right": bf(spread(np.random.standard_normal((N, R)), lat)),
        "WF_right": bf(np.random.standard_normal((D, C)) * 3.0 / np.sqrt(C) / s),
    }


def reference(source, target, k_right, WF_right):
    t, k = f64(target), f64(k_right)
    f = mxq(f64(source), 1, "e4m3") @ mxq(f64(WF_right).T, 0, "e4m3")
    d2 = (t * t).sum(-1, keepdims=True) + (k * k).sum(-1)[None, :] - 2.0 * (f64(target) @ f64(k_right).T)
    dist = np.sqrt(np.maximum(d2, 0.0))
    l = -dist * E ** (-0.5)
    e = np.exp(l - l.max(-1, keepdims=True))
    return (mxq(e, 1, "e4m3") @ mxq(f, 0, "e4m3")) / e.sum(-1, keepdims=True)

@@ -1,0 +1,321 @@
+from contextlib import ExitStack
+
+import concourse.bass as bass
+import concourse.mybir as mybir
+import concourse.tile as tile
+from concourse.masks import make_identity
+
+FLOPS = 2 * 1024 * 512 * 128 + 2 * 2 * 16384 * 1024 * 128
+
+BF16 = mybir.dt.bfloat16
+F32 = mybir.dt.float32
+U32 = mybir.dt.uint32
+U8 = mybir.dt.uint8
+FP8X4 = mybir.dt.float8_e4m3fn_x4
+ALU = mybir.AluOpType
+ACTF = mybir.ActivationFunctionType
+AX = mybir.AxisListType
+
+P = 128
+NKEY = 1024
+NB = 128
+NO = 16
+GROUPS = [6, 10, 16, 24, 24, 24, 16, 8]
+R = 28
+RE = 16
+MARGIN = 2
+DIRECT = True
+ALT = True
+NTN, NTT, NET, NG, NC, NOS = 4, 2, 2, 1, 2, 2
+
+
+def tile_kanadjunction_pa_t_kernel(tc, source, target, k_right, WF_right, out):
+    nc = tc.nc
+    with ExitStack() as ctx:
+        keep = ctx.enter_context(tc.tile_pool(name="keep", bufs=1))
+        psum = ctx.enter_context(tc.psum_pool(name="psum", bufs=1))
+        ctx.enter_context(tc.manual_schedule())
+
+        ident_f = keep.tile([P, P], F32, name="ident_f")
+        ident_b = keep.tile([P, P], BF16, name="ident_b")
+        kr = keep.tile([P, 1024], BF16, name="kr")
+        kT = keep.tile([P, 1024], BF16, name="kT")
+        k2 = keep.tile([P, 8], F32, name="k2")
+        negk = keep.tile([P, 8, P], F32, name="negk")
+        src = keep.tile([P, 4096], BF16, name="src")
+        src_g = keep.tile([P, 4096], BF16, name="src_g", align_bytes=64)
+        src_c = keep.tile([P, 1024], U32, name="src_c", align_bytes=64)
+        src_s = keep.tile([P, 1024], U8, name="src_s", align_bytes=64)
+        wf = keep.tile([P, 512], BF16, name="wf")
+        wf_g = keep.tile([P, 512], BF16, name="wf_g", align_bytes=64)
+        wf_c = keep.tile([P, 128], U32, name="wf_c", align_bytes=64)
+        wf_s = keep.tile([P, 128], U8, name="wf_s", align_bytes=64)
+        f_g = keep.tile([P, 1024], BF16, name="f_g", align_bytes=64)
+        f_c = keep.tile([P, 256], U32, name="f_c", align_bytes=64)
+        f_s = keep.tile([P, 256], U8, name="f_s", align_bytes=64)
+        t2 = keep.tile([P, NB], F32, name="t2")
+        t2s = keep.tile([P, NB], F32, name="t2s")
+        ymax2 = keep.tile([P, 2 * NB], F32, name="ymax2")
+        ymx = keep.tile([P, NB], F32, name="ymx")
+        arg = keep.tile([P, NB], F32, name="arg")
+        lmin = keep.tile([P, NB], F32, name="lmin")
+        rs = keep.tile([P, NB], F32, name="rs")
+        rcp = keep.tile([P, NB], F32, name="rcp")
+        sq = [keep.tile([P, 1024], F32, name="sq%d" % i) for i in range(2)]
+        grd = keep.tile([P, NKEY], BF16, name="grd", align_bytes=64)
+        tn = [keep.tile([P, 1024], BF16, name="tn%d" % i) for i in range(NTN)]
+        tT = [keep.tile([P, 1024], BF16, name="tT%d" % i) for i in range(NTT)]
+        y = [keep.tile([P, NKEY], F32, name="y%d" % i) for i in range(R)]
+        e = [keep.tile([P, NKEY], BF16, name="e%d" % i) for i in range(RE)]
+        eT = [keep.tile([P, NKEY], BF16, name="eT%d" % i) for i in range(NET)]
+        grp = [keep.tile([P, NKEY], BF16, name="grp%d" % i, align_bytes=64) for i in range(NG)]
+        codes = [keep.tile([P, 1024], U32, name="codes%d" % i, align_bytes=64) for i in range(NC)]
+        scl = [keep.tile([P, 1024], U8, name="scl%d" % i, align_bytes=64) for i in range(NC)]
+        osb = [keep.tile([P, 512], F32, name="osb%d" % i) for i in range(NOS)]
+        bank = {}
+
+        def load_octet(o):
+            nc.sync.dma_start(out=tn[o % NTN][:], in_=target[o * 1024:(o + 1) * 1024, :].rearrange("(p i) e -> p (i e)", i=8))
+
+        def transpose8(tag, src_tile):
+            pb = psum.tile([P, 1024], BF16, name="pb_" + tag, tag=tag)
+            for i in range(8):
+                nc.tensor.transpose(pb[:, i * P:(i + 1) * P], src_tile[:, i * P:(i + 1) * P], ident_b[:])
+            return pb
+
+        def prep_pe(o):
+            bank["x", o] = transpose8("X", tn[o % NTN])
+
+        def prep_cp(o):
+            nc.vector.tensor_copy(out=tT[o % NTT][:], in_=bank["x", o][:])
+
+        def prep_sq(eng, o, lo, hi):
+            eng.tensor_tensor(out=sq[o % 2][:, lo:hi], in0=tn[o % NTN][:, lo:hi], in1=tn[o % NTN][:, lo:hi], op=ALU.mult)
+
+        def prep_red(o):
+            nc.vector.tensor_reduce(out=t2[:, 8 * o:8 * o + 8], in_=sq[o % 2][:].rearrange("p (i e) -> p i e", i=8), axis=AX.X, op=ALU.add)
+            nc.vector.tensor_scalar(out=t2s[:, 8 * o:8 * o + 8], in0=t2[:, 8 * o:8 * o + 8], scalar1=2.0 ** -7, scalar2=None, op0=ALU.mult)
+
+        def front_pe(a):
+            o, i = divmod(a, 8)
+            for g in range(2):
+                yb = psum.tile([P, 512], F32, name="yb", tag="Y%d" % (2 * (a % 2) + g))
+                nc.tensor.matmul(yb[:], lhsT=tT[o % NTT][:, i * P:(i + 1) * P], rhs=kT[:, g * 512:(g + 1) * 512], start=True, stop=False)
+                for t in range(4):
+                    nc.tensor.matmul(yb[:, t * P:(t + 1) * P], lhsT=negk[:, 4 * g + t, :], rhs=ident_f[:], is_transpose=True, start=False, stop=(t == 3))
+                bank["y", a, g] = yb
+
+        def front_v(a):
+            for g in range(2):
+                nc.vector.tensor_scalar(out=y[a % R][:, g * 512:(g + 1) * 512], in0=bank["y", a, g][:], scalar1=t2s[:, a:a + 1], scalar2=None,
+                                        op0=ALU.min, op1=ALU.max, accum_out=ymax2[:, 2 * a + g:2 * a + g + 1])
+
+        def v_tiny(a0, a1):
+            nc.vector.tensor_reduce(out=ymx[:, a0:a1], in_=ymax2[:, 2 * a0:2 * a1].rearrange("p (a h) -> p a h", h=2), axis=AX.X, op=ALU.max)
+            nc.vector.tensor_tensor(out=arg[:, a0:a1], in0=t2s[:, a0:a1], in1=ymx[:, a0:a1], op=ALU.subtract)
+
+        def act_sqrt(a):
+            nc.scalar.activation(out=y[a % R][:], in_=y[a % R][:], func=ACTF.Sqrt, bias=t2s[:, a:a + 1], scale=-1.0)
+
+        def act_tiny(a0, a1):
+            nc.scalar.activation(out=lmin[:, a0:a1], in_=arg[:, a0:a1], func=ACTF.Sqrt)
+
+        def act_exp(a):
+            nc.scalar.activation(out=e[a % RE][:], in_=y[a % R][:], func=ACTF.Exp, bias=lmin[:, a:a + 1], scale=-1.0, accum_out=rs[:, a:a + 1])
+
+        def back_pe(b):
+            bank["t", b] = transpose8("T%d" % (b % 2), e[b % RE])
+
+        def back_cp(b):
+            nc.vector.tensor_copy(out=eT[b % NET][:], in_=bank["t", b][:])
+
+        def back_rg(b):
+            nc.gpsimd.tensor_scalar(out=grp[b % NG][:].rearrange("p (g b t) -> p g b t", g=2, t=4),
+                                    in0=eT[b % NET][:].rearrange("p (g t b) -> p g b t", g=2, t=4),
+                                    scalar1=1.0, scalar2=0.0, op0=ALU.mult, op1=ALU.add)
+
+        def back_cd(b):
+            nc.vector.tensor_copy(out=grd[:].rearrange("p (g b t) -> p g b t", g=2, t=4), in_=bank["t", b][:].rearrange("p (g t b) -> p g b t", g=2, t=4))
+
+        def back_q(b):
+            q, i = divmod(b, 4)
+            nc.vector.quantize_mx(out=codes[q % NC][:, i * 256:(i + 1) * 256].bitcast(FP8X4), scales=scl[q % NC][:, i * 256:(i + 1) * 256],
+                                  in_=(grd[:] if direct[b] else grp[b % NG][:]))
+
+        def mx(q):
+            ob = psum.tile([P, 512], F32, name="ob", tag="O")
+            for i in range(4):
+                for g in range(2):
+                    c0 = i * 256 + g * P
+                    nc.tensor.matmul_mx(out=ob[:, i * P:(i + 1) * P], lhsT=codes[q % NC][:, c0:c0 + P].bitcast(FP8X4), lhsT_scale=scl[q % NC][:, c0:c0 + P],
+                                        rhs=f_c[:, g * P:(g + 1) * P].bitcast(FP8X4), rhs_scale=f_s[:, g * P:(g + 1) * P], start=(g == 0), stop=(g == 1))
+            bank["o", q] = ob
+
+        def fin(q):
+            nc.vector.reciprocal(out=rcp[:, 4 * q:4 * q + 4], in_=rs[:, 4 * q:4 * q + 4])
+            nc.vector.tensor_tensor(out=osb[q % NOS][:].rearrange("p (i d) -> p i d", i=4), in0=bank["o", q][:].rearrange("p (i d) -> p i d", i=4),
+                                    in1=rcp[:, 4 * q:4 * q + 4].unsqueeze(2).to_broadcast([P, 4, P]), op=ALU.mult)
+            o, h = divmod(q, 2)
+            nc.sync.dma_start(out=out[o * 1024:(o + 1) * 1024, :].rearrange("(p i) d -> p (i d)", i=8)[:, h * 512:(h + 1) * 512], in_=osb[q % NOS][:])
+
+        def words_pe(tag, rows, nchunk):
+            pw = psum.tile([P, 2 * nchunk * P], F32, name="pw_" + tag, tag=tag)
+            for c in range(nchunk):
+                for u in range(2):
+                    nc.tensor.transpose(pw[:, (2 * c + u) * P:(2 * c + u + 1) * P], rows[:, c * 512:(c + 1) * 512].bitcast(F32)[:, u * P:(u + 1) * P], ident_f[:])
+            return pw
+
+        def words_cp(pw, dst, nchunk):
+            nc.vector.tensor_copy(out=dst.bitcast(F32).rearrange("w (c n u) -> w c n u", c=nchunk, u=2), in_=pw[:].rearrange("w (c u n) -> w c n u", c=nchunk, u=2))
+
+        def src_pe(j):
+            bank["s", j] = words_pe(["O", "T1"][j % 2], src[:, j * 1024:(j + 1) * 1024], 2)
+
+        def src_cp(j):
+            words_cp(bank["s", j], src_g[:, j * 1024:(j + 1) * 1024], 2)
+
+        def wf_pe():
+            bank["w"] = words_pe("T0", wf[:], 1)
+
+        def f_mx():
+            for g in range(2):
+                fb = psum.tile([P, 512], F32, name="fb", tag=["O", "T1"][g])
+                for t in range(4):
+                    c = 4 * g + t
+                    nc.tensor.matmul_mx(out=fb[:, t * P:(t + 1) * P], lhsT=src_c[:, c * P:(c + 1) * P].bitcast(FP8X4), lhsT_scale=src_s[:, c * P:(c + 1) * P],
+                                        rhs=wf_c[:].bitcast(FP8X4), rhs_scale=wf_s[:], start=True, stop=True)
+                bank["f", g] = fb
+
+        def f_cp(g):
+            nc.vector.tensor_copy(out=f_g[:, g * 512:(g + 1) * 512].rearrange("p (d t) -> p d t", t=4), in_=bank["f", g][:].rearrange("p (t d) -> p d t", t=4))
+
+        def x0():
+            wf_pe(); src_pe(0)
+        def x1():
+            words_cp(bank["w"], wf_g[:], 1); src_pe(1)
+        def x2():
+            src_cp(0); src_pe(2)
+        def x3():
+            src_cp(1); src_pe(3)
+        def x4():
+            src_cp(2)
+            nc.vector.quantize_mx(out=wf_c[:].bitcast(FP8X4), scales=wf_s[:], in_=wf_g[:])
+        def x5():
+            src_cp(3)
+        def x6():
+            nc.vector.quantize_mx(out=src_c[:].bitcast(FP8X4), scales=src_s[:], in_=src_g[:])
+            f_mx()
+        def x7():
+            f_cp(0); f_cp(1)
+        def x8():
+            nc.vector.quantize_mx(out=f_c[:].bitcast(FP8X4), scales=f_s[:], in_=f_g[:])
+        extra = [x0, x1, x2, x3, x4, x5, x6, x7, x8]
+
+        nc.sync.dma_start(out=kr[:].rearrange("p (g x) -> p g x", g=2), in_=k_right.rearrange("(g p t) e -> p g (t e)", g=2, t=4))
+        load_octet(0)
+        nc.sync.dma_start(out=wf[:], in_=WF_right)
+        nc.sync.dma_start(out=src[:].rearrange("p (g x) -> p g x", g=2), in_=source.rearrange("(g p t) c -> p g (t c)", g=2, t=4))
+        load_octet(1)
+        load_octet(2)
+        make_identity(nc, ident_b[:])
+        make_identity(nc, ident_f[:])
+        kb = transpose8("T0", kr)
+        prep_pe(0)
+        nc.vector.tensor_scalar(out=kT[:], in0=kb[:], scalar1=2.0 ** -6, scalar2=None, op0=ALU.mult)
+        prep_cp(0)
+        nc.vector.tensor_tensor(out=sq[1][:], in0=kr[:], in1=kr[:], op=ALU.mult)
+        nc.vector.tensor_reduce(out=k2[:], in_=sq[1][:].rearrange("p (i e) -> p i e", i=8), axis=AX.X, op=ALU.add)
+        nc.vector.tensor_scalar(out=negk[:], in0=k2[:].unsqueeze(2).to_broadcast([P, 8, P]), scalar1=-(2.0 ** -7), scalar2=None, op0=ALU.mult)
+        prep_sq(nc.vector, 0, 0, 1024)
+        prep_red(0)
+        front_pe(0)
+        prep_sq(nc.gpsimd, 1, 0, 1024)
+
+        bounds = []
+        a0 = 0
+        for gsz in GROUPS:
+            bounds.append((a0, a0 + gsz))
+            a0 += gsz
+        assert a0 == NB
+        acts = []
+        for (b0, b1) in bounds:
+            acts += [("s", a) for a in range(b0, b1)] + [("t", (b0, b1))] + [("e", a) for a in range(b0, b1)]
+        need = [0.0] * (len(acts) + 1)
+        for s in range(len(acts) - 1, -1, -1):
+            need[s] = need[s + 1] - 0.5
+            if acts[s][0] == "s":
+                need[s] = max(need[s], acts[s][1] + 1 + MARGIN)
+        last_of = dict((b1 - 1, (b0, b1)) for (b0, b1) in bounds)
+        st = {"F": 0, "B": 0, "E": 0, "last": "F"}
+        direct = {}
+
+        def can_f():
+            return st["F"] < NB and st["F"] - R < st["E"]
+
+        def unit_f():
+            a = st["F"]
+            oc, r = divmod(a, 8)
+            if r == 0 and oc + 3 < NO:
+                load_octet(oc + 3)
+            if oc + 2 < NO:
+                prep_sq(nc.gpsimd, oc + 2, r * P, (r + 1) * P)
+            if r == 2 and oc + 1 < NO:
+                prep_pe(oc + 1)
+            if a + 1 < NB:
+                front_pe(a + 1)
+            front_v(a)
+            if r == 1 and oc + 1 < NO:
+                prep_red(oc + 1)
+            if r == 3 and oc + 1 < NO:
+                prep_cp(oc + 1)
+            if a in last_of:
+                v_tiny(*last_of[a])
+            st["F"] += 1
+            st["last"] = "F"
+
+        def unit_b():
+            n = st["B"]
+            if n >= 6 and (n - 6) % 4 == 0 and (n - 6) // 4 < NB // 4:
+                while extra:
+                    extra.pop(0)()
+                mx((n - 6) // 4)
+            if n < NB:
+                back_pe(n)
+            if 0 <= n - 1 < NB:
+                direct[n - 1] = DIRECT and st["last"] == "B" and not direct.get(n - 2, False)
+            if 0 <= n - 1 < NB and not direct[n - 1]:
+                back_cp(n - 1)
+            if 0 <= n - 2 < NB:
+                back_q(n - 2)
+            if 0 <= n - 1 < NB:
+                if direct[n - 1]:
+                    back_cd(n - 1)
+                else:
+                    back_rg(n - 1)
+            if n >= 7 and (n - 7) % 4 == 0 and (n - 7) // 4 < NB // 4:
+                fin((n - 7) // 4)
+            st["B"] += 1
+            st["last"] = "B"
+
+        for s, (kind, x) in enumerate(acts):
+            if kind == "s":
+                while st["F"] <= x:
+                    unit_f()
+                act_sqrt(x)
+            elif kind == "t":
+                act_tiny(*x)
+            else:
+                while st["B"] <= x - RE:
+                    unit_b()
+                act_exp(x)
+                st["E"] += 1
+            if can_f() and st["F"] < need[s + 1]:
+                unit_f()
+            elif extra:
+                extra.pop(0)()
+            elif st["B"] < st["E"] and (st["last"] != "B" or not can_f() or not ALT):
+                unit_b()
+            elif can_f():
+                unit_f()
+        while st["B"] < NB + 8:
+            unit_b()

@@ -24,9 +24,16 @@ GROUPS = [6, 10, 16, 24, 24, 24, 16, 8]
 R = 28
 RE = 16
 MARGIN = 2
-DIRECT = True
 ALT = True
-NTN, NTT, NET, NG, NC, NOS = 4, 2, 2, 1, 2, 2
+AB = 2
+TT_ON_ACT = False
+NQ = 32
+QA = 24
+SLOPE = 0.55
+QD = 30
+LM = 1
+LQ = 3
+NTN, NTT, NET, NG, NC, NOS = 4, 3, 2, 1, 2, 2
 
 
 def tile_kanadjunction_pa_t_kernel(tc, source, target, k_right, WF_right, out):
@@ -42,9 +49,9 @@ def tile_kanadjunction_pa_t_kernel(tc, source, target, k_right, WF_right, out):
         kT = keep.tile([P, 1024], BF16, name="kT")
         k2 = keep.tile([P, 8], F32, name="k2")
         negk = keep.tile([P, 8, P], F32, name="negk")
-        src = keep.tile([P, 4096], BF16, name="src")
-        src_g = keep.tile([P, 4096], BF16, name="src_g", align_bytes=64)
-        src_c = keep.tile([P, 1024], U32, name="src_c", align_bytes=64)
+        src = [keep.tile([P, 2048], BF16, name="src%d" % g, tag="y%d" % (R - 1 - g), align_bytes=64) for g in range(2)]
+        src_g = [keep.tile([P, 2048], BF16, name="src_g%d" % g, tag="y%d" % (R - 3 - g), align_bytes=64) for g in range(2)]
+        src_c = keep.tile([P, 1024], U32, name="src_c", tag="y%d" % (R - 5), align_bytes=64)
         src_s = keep.tile([P, 1024], U8, name="src_s", align_bytes=64)
         wf = keep.tile([P, 512], BF16, name="wf")
         wf_g = keep.tile([P, 512], BF16, name="wf_g", align_bytes=64)
@@ -53,7 +60,9 @@ def tile_kanadjunction_pa_t_kernel(tc, source, target, k_right, WF_right, out):
         f_g = keep.tile([P, 1024], BF16, name="f_g", align_bytes=64)
         f_c = keep.tile([P, 256], U32, name="f_c", align_bytes=64)
         f_s = keep.tile([P, 256], U8, name="f_s", align_bytes=64)
-        t2 = keep.tile([P, NB], F32, name="t2")
+        ones2 = keep.tile([P, 2], F32, name="ones2")
+        junk = keep.tile([P, P], F32, name="junk")
+        t20 = keep.tile([P, 8], F32, name="t20")
         t2s = keep.tile([P, NB], F32, name="t2s")
         ymax2 = keep.tile([P, 2 * NB], F32, name="ymax2")
         ymx = keep.tile([P, NB], F32, name="ymx")
@@ -62,13 +71,13 @@ def tile_kanadjunction_pa_t_kernel(tc, source, target, k_right, WF_right, out):
         rs = keep.tile([P, NB], F32, name="rs")
         rcp = keep.tile([P, NB], F32, name="rcp")
         sq = [keep.tile([P, 1024], F32, name="sq%d" % i) for i in range(2)]
-        grd = keep.tile([P, NKEY], BF16, name="grd", align_bytes=64)
         tn = [keep.tile([P, 1024], BF16, name="tn%d" % i) for i in range(NTN)]
         tT = [keep.tile([P, 1024], BF16, name="tT%d" % i) for i in range(NTT)]
-        y = [keep.tile([P, NKEY], F32, name="y%d" % i) for i in range(R)]
+        y = [keep.tile([P, NKEY], F32, name="y%d" % i, align_bytes=64) for i in range(R - 5)]
         e = [keep.tile([P, NKEY], BF16, name="e%d" % i) for i in range(RE)]
-        eT = [keep.tile([P, NKEY], BF16, name="eT%d" % i) for i in range(NET)]
-        grp = [keep.tile([P, NKEY], BF16, name="grp%d" % i, align_bytes=64) for i in range(NG)]
+        eT = [keep.tile([P, 4 * NKEY], BF16, name="eT%d" % i) for i in range(NET)]
+        grp = keep.tile([P, 4 * NKEY], BF16, name="grp", align_bytes=64)
+        grd = [keep.tile([P, NKEY], BF16, name="grd%d" % i, align_bytes=64) for i in range(2)]
         codes = [keep.tile([P, 1024], U32, name="codes%d" % i, align_bytes=64) for i in range(NC)]
         scl = [keep.tile([P, 1024], U8, name="scl%d" % i, align_bytes=64) for i in range(NC)]
         osb = [keep.tile([P, 512], F32, name="osb%d" % i) for i in range(NOS)]
@@ -87,14 +96,22 @@ def tile_kanadjunction_pa_t_kernel(tc, source, target, k_right, WF_right, out):
             bank["x", o] = transpose8("X", tn[o % NTN])
 
         def prep_cp(o):
-            nc.vector.tensor_copy(out=tT[o % NTT][:], in_=bank["x", o][:])
+            if TT_ON_ACT and o > 1:
+                nc.scalar.copy(out=tT[o % NTT][:], in_=bank["x", o][:])
+            else:
+                nc.vector.tensor_copy(out=tT[o % NTT][:], in_=bank["x", o][:])
 
         def prep_sq(eng, o, lo, hi):
-            eng.tensor_tensor(out=sq[o % 2][:, lo:hi], in0=tn[o % NTN][:, lo:hi], in1=tn[o % NTN][:, lo:hi], op=ALU.mult)
+            eng.tensor_tensor(out=sq[o % 2][:, lo:hi], in0=tT[o % NTT][:, lo:hi], in1=tT[o % NTT][:, lo:hi], op=ALU.mult)
+
+        def prep_sum(o):
+            xs = psum.tile([P, 16], F32, name="xs", tag="X")
+            for i in range(8):
+                nc.tensor.matmul(xs[:, 2 * i:2 * i + 2], lhsT=sq[o % 2][:, i * P:(i + 1) * P], rhs=ones2[:], start=True, stop=True)
+            bank["xs", o] = xs
 
         def prep_red(o):
-            nc.vector.tensor_reduce(out=t2[:, 8 * o:8 * o + 8], in_=sq[o % 2][:].rearrange("p (i e) -> p i e", i=8), axis=AX.X, op=ALU.add)
-            nc.vector.tensor_scalar(out=t2s[:, 8 * o:8 * o + 8], in0=t2[:, 8 * o:8 * o + 8], scalar1=2.0 ** -7, scalar2=None, op0=ALU.mult)
+            nc.vector.tensor_scalar(out=t2s[:, 8 * o:8 * o + 8], in0=bank["xs", o][:].rearrange("p (i w) -> p i w", w=2)[:, :, 0], scalar1=2.0 ** -7, scalar2=None, op0=ALU.mult)
 
         def front_pe(a):
             o, i = divmod(a, 8)
@@ -106,7 +123,7 @@ def tile_kanadjunction_pa_t_kernel(tc, source, target, k_right, WF_right, out):
                 bank["y", a, g] = yb
 
         def front_v(a):
-            for g in range(2):
+            for g in (1, 0):
                 nc.vector.tensor_scalar(out=y[a % R][:, g * 512:(g + 1) * 512], in0=bank["y", a, g][:], scalar1=t2s[:, a:a + 1], scalar2=None,
                                         op0=ALU.min, op1=ALU.max, accum_out=ymax2[:, 2 * a + g:2 * a + g + 1])
 
@@ -127,20 +144,24 @@ def tile_kanadjunction_pa_t_kernel(tc, source, target, k_right, WF_right, out):
             bank["t", b] = transpose8("T%d" % (b % 2), e[b % RE])
 
         def back_cp(b):
-            nc.vector.tensor_copy(out=eT[b % NET][:], in_=bank["t", b][:])
+            q, i = divmod(b, 4)
+            nc.vector.tensor_copy(out=eT[q % NET][:, i * NKEY:(i + 1) * NKEY], in_=bank["t", b][:])
 
-        def back_rg(b):
-            nc.gpsimd.tensor_scalar(out=grp[b % NG][:].rearrange("p (g b t) -> p g b t", g=2, t=4),
-                                    in0=eT[b % NET][:].rearrange("p (g t b) -> p g b t", g=2, t=4),
+        def back_rg(q):
+            nc.gpsimd.tensor_scalar(out=grp[:].rearrange("p (g b t) -> p g b t", g=8, t=4),
+                                    in0=eT[q % NET][:].rearrange("p (g t b) -> p g b t", g=8, t=4),
                                     scalar1=1.0, scalar2=0.0, op0=ALU.mult, op1=ALU.add)
 
         def back_cd(b):
-            nc.vector.tensor_copy(out=grd[:].rearrange("p (g b t) -> p g b t", g=2, t=4), in_=bank["t", b][:].rearrange("p (g t b) -> p g b t", g=2, t=4))
+            nc.vector.tensor_copy(out=grd[b % 2][:].rearrange("p (g b t) -> p g b t", g=2, t=4),
+                                  in_=bank["t", b][:].rearrange("p (g t b) -> p g b t", g=2, t=4))
 
-        def back_q(b):
+        def back_q4(q):
+            nc.vector.quantize_mx(out=codes[q % NC][:].bitcast(FP8X4), scales=scl[q % NC][:], in_=grp[:])
+
+        def back_q1(b):
             q, i = divmod(b, 4)
-            nc.vector.quantize_mx(out=codes[q % NC][:, i * 256:(i + 1) * 256].bitcast(FP8X4), scales=scl[q % NC][:, i * 256:(i + 1) * 256],
-                                  in_=(grd[:] if direct[b] else grp[b % NG][:]))
+            nc.vector.quantize_mx(out=codes[q % NC][:, i * 256:(i + 1) * 256].bitcast(FP8X4), scales=scl[q % NC][:, i * 256:(i + 1) * 256], in_=grd[b % 2][:])
 
         def mx(q):
             ob = psum.tile([P, 512], F32, name="ob", tag="O")
@@ -169,10 +190,10 @@ def tile_kanadjunction_pa_t_kernel(tc, source, target, k_right, WF_right, out):
             nc.vector.tensor_copy(out=dst.bitcast(F32).rearrange("w (c n u) -> w c n u", c=nchunk, u=2), in_=pw[:].rearrange("w (c u n) -> w c n u", c=nchunk, u=2))
 
         def src_pe(j):
-            bank["s", j] = words_pe(["O", "T1"][j % 2], src[:, j * 1024:(j + 1) * 1024], 2)
+            bank["s", j] = words_pe(["O", "T1"][j % 2], src[j // 2][:, (j % 2) * 1024:(j % 2 + 1) * 1024], 2)
 
         def src_cp(j):
-            words_cp(bank["s", j], src_g[:, j * 1024:(j + 1) * 1024], 2)
+            words_cp(bank["s", j], src_g[j // 2][:, (j % 2) * 1024:(j % 2 + 1) * 1024], 2)
 
         def wf_pe():
             bank["w"] = words_pe("T0", wf[:], 1)
@@ -203,7 +224,8 @@ def tile_kanadjunction_pa_t_kernel(tc, source, target, k_right, WF_right, out):
         def x5():
             src_cp(3)
         def x6():
-            nc.vector.quantize_mx(out=src_c[:].bitcast(FP8X4), scales=src_s[:], in_=src_g[:])
+            for g in range(2):
+                nc.vector.quantize_mx(out=src_c[:, g * 512:(g + 1) * 512].bitcast(FP8X4), scales=src_s[:, g * 512:(g + 1) * 512], in_=src_g[g][:])
             f_mx()
         def x7():
             f_cp(0); f_cp(1)
@@ -214,22 +236,27 @@ def tile_kanadjunction_pa_t_kernel(tc, source, target, k_right, WF_right, out):
         nc.sync.dma_start(out=kr[:].rearrange("p (g x) -> p g x", g=2), in_=k_right.rearrange("(g p t) e -> p g (t e)", g=2, t=4))
         load_octet(0)
         nc.sync.dma_start(out=wf[:], in_=WF_right)
-        nc.sync.dma_start(out=src[:].rearrange("p (g x) -> p g x", g=2), in_=source.rearrange("(g p t) c -> p g (t c)", g=2, t=4))
+        for g in range(2):
+            nc.sync.dma_start(out=src[g][:], in_=source[g * 512:(g + 1) * 512, :].rearrange("(p t) c -> p (t c)", t=4))
         load_octet(1)
         load_octet(2)
+        load_octet(3)
         make_identity(nc, ident_b[:])
         make_identity(nc, ident_f[:])
+        nc.gpsimd.memset(ones2[:], 1.0)
+        nc.vector.memset(junk[:, 0:1], 1.0)
+        nc.scalar.activation(out=junk[:, 1:2], in_=junk[:, 0:1], func=ACTF.Sqrt)
         kb = transpose8("T0", kr)
         prep_pe(0)
+        for c in range(8):
+            nc.scalar.activation(out=junk[:], in_=kr[:, c * P:(c + 1) * P], func=ACTF.Square, accum_out=k2[:, c:c + 1])
+        for c in range(8):
+            nc.scalar.activation(out=junk[:], in_=tn[0][:, c * P:(c + 1) * P], func=ACTF.Square, accum_out=t20[:, c:c + 1])
         nc.vector.tensor_scalar(out=kT[:], in0=kb[:], scalar1=2.0 ** -6, scalar2=None, op0=ALU.mult)
         prep_cp(0)
-        nc.vector.tensor_tensor(out=sq[1][:], in0=kr[:], in1=kr[:], op=ALU.mult)
-        nc.vector.tensor_reduce(out=k2[:], in_=sq[1][:].rearrange("p (i e) -> p i e", i=8), axis=AX.X, op=ALU.add)
         nc.vector.tensor_scalar(out=negk[:], in0=k2[:].unsqueeze(2).to_broadcast([P, 8, P]), scalar1=-(2.0 ** -7), scalar2=None, op0=ALU.mult)
-        prep_sq(nc.vector, 0, 0, 1024)
-        prep_red(0)
+        nc.vector.tensor_scalar(out=t2s[:, 0:8], in0=t20[:], scalar1=2.0 ** -7, scalar2=None, op0=ALU.mult)
         front_pe(0)
-        prep_sq(nc.gpsimd, 1, 0, 1024)
 
         bounds = []
         a0 = 0
@@ -239,35 +266,62 @@ def tile_kanadjunction_pa_t_kernel(tc, source, target, k_right, WF_right, out):
         assert a0 == NB
         acts = []
         for (b0, b1) in bounds:
-            acts += [("s", a) for a in range(b0, b1)] + [("t", (b0, b1))] + [("e", a) for a in range(b0, b1)]
+            order = []
+            for c0 in range(b0, b1, AB):
+                order += list(reversed(range(c0, min(c0 + AB, b1))))
+            acts += [("s", a) for a in order] + [("t", (b0, b1))] + [("e", a) for a in order]
         need = [0.0] * (len(acts) + 1)
         for s in range(len(acts) - 1, -1, -1):
-            need[s] = need[s + 1] - 0.5
+            need[s] = need[s + 1] - SLOPE
             if acts[s][0] == "s":
                 need[s] = max(need[s], acts[s][1] + 1 + MARGIN)
         last_of = dict((b1 - 1, (b0, b1)) for (b0, b1) in bounds)
         st = {"F": 0, "B": 0, "E": 0, "last": "F"}
-        direct = {}
+
+        def is_direct(q):
+            return q >= QD or (q >= QA and q % 2 == 1)
+
+        mx_at = [(4 * q + 6 if is_direct(q) else 4 * q + 4 + LQ + LM) for q in range(NQ)]
+
+        exp_done = [False] * NB
 
         def can_f():
-            return st["F"] < NB and st["F"] - R < st["E"]
+            return st["F"] < NB and (st["F"] < R or exp_done[st["F"] - R])
+
+        def can_b():
+            return st["B"] < NB and exp_done[st["B"]]
 
         def unit_f():
             a = st["F"]
             oc, r = divmod(a, 8)
-            if r == 0 and oc + 3 < NO:
-                load_octet(oc + 3)
-            if oc + 2 < NO:
-                prep_sq(nc.gpsimd, oc + 2, r * P, (r + 1) * P)
-            if r == 2 and oc + 1 < NO:
-                prep_pe(oc + 1)
+            if len(y) <= a < R:
+                while extra:
+                    extra.pop(0)()
+                y.append(keep.tile([P, NKEY], F32, name="y%d" % a, align_bytes=64))
+            if oc == 0:
+                if r == 0:
+                    prep_pe(1)
+                if 1 <= r <= 4:
+                    prep_sq(nc.gpsimd, 1, (r - 1) * 256, r * 256)
+            if r == 4 and oc + 4 < NO:
+                load_octet(oc + 4)
+            if r >= 4 and oc + 2 < NO:
+                prep_sq(nc.gpsimd, oc + 2, (r - 4) * P, (r - 3) * P)
+            if r < 4 and 2 <= oc + 1 < NO:
+                prep_sq(nc.gpsimd, oc + 1, (r + 4) * P, (r + 5) * P)
+            if r == 2 and oc + 2 < NO:
+                prep_pe(oc + 2)
+            if r == 5 and oc + 1 < NO:
+                prep_sum(oc + 1)
             if a + 1 < NB:
                 front_pe(a + 1)
             front_v(a)
-            if r == 1 and oc + 1 < NO:
+            if r == 6 and oc + 1 < NO:
                 prep_red(oc + 1)
-            if r == 3 and oc + 1 < NO:
-                prep_cp(oc + 1)
+            if oc == 0 and r == 0:
+                prep_cp(1)
+            if r == 3 and oc + 2 < NO:
+                prep_cp(oc + 2)
             if a in last_of:
                 v_tiny(*last_of[a])
             st["F"] += 1
@@ -275,25 +329,29 @@ def tile_kanadjunction_pa_t_kernel(tc, source, target, k_right, WF_right, out):
 
         def unit_b():
             n = st["B"]
-            if n >= 6 and (n - 6) % 4 == 0 and (n - 6) // 4 < NB // 4:
-                while extra:
-                    extra.pop(0)()
-                mx((n - 6) // 4)
+            for q in range(NQ):
+                if n == mx_at[q]:
+                    while extra:
+                        extra.pop(0)()
+                    mx(q)
             if n < NB:
                 back_pe(n)
-            if 0 <= n - 1 < NB:
-                direct[n - 1] = DIRECT and st["last"] == "B" and not direct.get(n - 2, False)
-            if 0 <= n - 1 < NB and not direct[n - 1]:
-                back_cp(n - 1)
-            if 0 <= n - 2 < NB:
-                back_q(n - 2)
-            if 0 <= n - 1 < NB:
-                if direct[n - 1]:
-                    back_cd(n - 1)
+            b = n - 1
+            if 0 <= b < NB:
+                if not is_direct(b // 4):
+                    back_cp(b)
+                    if b % 4 == 3:
+                        back_rg(b // 4)
                 else:
-                    back_rg(n - 1)
-            if n >= 7 and (n - 7) % 4 == 0 and (n - 7) // 4 < NB // 4:
-                fin((n - 7) // 4)
+                    back_cd(b)
+            for q in range(NQ):
+                if not is_direct(q) and n == 4 * q + 4 + LQ:
+                    back_q4(q)
+            if 0 <= n - 2 < NB and is_direct((n - 2) // 4):
+                back_q1(n - 2)
+            for q in range(NQ):
+                if n == mx_at[q] + 1:
+                    fin(q)
             st["B"] += 1
             st["last"] = "B"
 
@@ -308,14 +366,14 @@ def tile_kanadjunction_pa_t_kernel(tc, source, target, k_right, WF_right, out):
                 while st["B"] <= x - RE:
                     unit_b()
                 act_exp(x)
-                st["E"] += 1
+                exp_done[x] = True
             if can_f() and st["F"] < need[s + 1]:
                 unit_f()
             elif extra:
                 extra.pop(0)()
-            elif st["B"] < st["E"] and (st["last"] != "B" or not can_f() or not ALT):
+            elif can_b() and (st["last"] != "B" or not can_f() or not ALT):
                 unit_b()
             elif can_f():
                 unit_f()
-        while st["B"] < NB + 8:
+        while st["B"] < NB + 8 + LQ + LM:
             unit_b()

@@ -17,6 +17,7 @@ ACTF = mybir.ActivationFunctionType
 AX = mybir.AxisListType
 
 P = 128
+CSC = 128.0 ** -0.5
 NKEY = 1024
 NB = 128
 NO = 16
@@ -25,8 +26,11 @@ R = 28
 RE = 16
 MARGIN = 2
 ALT = True
+LAZY = True
+L1 = True
+T2PE = False
 AB = 2
-TT_ON_ACT = False
+TT_ON_ACT = True
 NQ = 32
 QA = 24
 SLOPE = 0.55
@@ -61,13 +65,14 @@ def tile_kanadjunction_pa_t_kernel(tc, source, target, k_right, WF_right, out):
         f_c = keep.tile([P, 256], U32, name="f_c", align_bytes=64)
         f_s = keep.tile([P, 256], U8, name="f_s", align_bytes=64)
         ones2 = keep.tile([P, 2], F32, name="ones2")
+        sqh = keep.tile([P, 512], F32, name="sqh")
         junk = keep.tile([P, P], F32, name="junk")
-        t20 = keep.tile([P, 8], F32, name="t20")
         t2s = keep.tile([P, NB], F32, name="t2s")
         ymax2 = keep.tile([P, 2 * NB], F32, name="ymax2")
         ymx = keep.tile([P, NB], F32, name="ymx")
         arg = keep.tile([P, NB], F32, name="arg")
         lmin = keep.tile([P, NB], F32, name="lmin")
+        dmin = keep.tile([P, NB], F32, name="dmin")
         rs = keep.tile([P, NB], F32, name="rs")
         rcp = keep.tile([P, NB], F32, name="rcp")
         sq = [keep.tile([P, 1024], F32, name="sq%d" % i) for i in range(2)]
@@ -102,7 +107,12 @@ def tile_kanadjunction_pa_t_kernel(tc, source, target, k_right, WF_right, out):
                 nc.vector.tensor_copy(out=tT[o % NTT][:], in_=bank["x", o][:])
 
         def prep_sq(eng, o, lo, hi):
-            eng.tensor_tensor(out=sq[o % 2][:, lo:hi], in0=tT[o % NTT][:, lo:hi], in1=tT[o % NTT][:, lo:hi], op=ALU.mult)
+            rows = tT[o % NTT] if T2PE else tn[o % NTN]
+            eng.tensor_tensor(out=sq[o % 2][:, lo:hi], in0=rows[:, lo:hi], in1=rows[:, lo:hi], op=ALU.mult)
+
+        def prep_half(o):
+            v = sq[o % 2][:].rearrange("p (i h e) -> p i h e", i=8, h=2)
+            nc.gpsimd.tensor_tensor(out=sqh[:].rearrange("p (i e) -> p i e", i=8), in0=v[:, :, 0, :], in1=v[:, :, 1, :], op=ALU.add)
 
         def prep_sum(o):
             xs = psum.tile([P, 16], F32, name="xs", tag="X")
@@ -111,7 +121,13 @@ def tile_kanadjunction_pa_t_kernel(tc, source, target, k_right, WF_right, out):
             bank["xs", o] = xs
 
         def prep_red(o):
-            nc.vector.tensor_scalar(out=t2s[:, 8 * o:8 * o + 8], in0=bank["xs", o][:].rearrange("p (i w) -> p i w", w=2)[:, :, 0], scalar1=2.0 ** -7, scalar2=None, op0=ALU.mult)
+            if not T2PE:
+                if L1:
+                    nc.vector.tensor_reduce(out=t2s[:, 8 * o:8 * o + 8], in_=sqh[:].rearrange("p (i e) -> p i e", i=8), axis=AX.X, op=ALU.add)
+                else:
+                    nc.vector.tensor_reduce(out=t2s[:, 8 * o:8 * o + 8], in_=sq[o % 2][:].rearrange("p (i e) -> p i e", i=8), axis=AX.X, op=ALU.add)
+                return
+            nc.vector.tensor_copy(out=t2s[:, 8 * o:8 * o + 8], in_=bank["xs", o][:].rearrange("p (i w) -> p i w", w=2)[:, :, 0])
 
         def front_pe(a):
             o, i = divmod(a, 8)
@@ -129,16 +145,17 @@ def tile_kanadjunction_pa_t_kernel(tc, source, target, k_right, WF_right, out):
 
         def v_tiny(a0, a1):
             nc.vector.tensor_reduce(out=ymx[:, a0:a1], in_=ymax2[:, 2 * a0:2 * a1].rearrange("p (a h) -> p a h", h=2), axis=AX.X, op=ALU.max)
-            nc.vector.tensor_tensor(out=arg[:, a0:a1], in0=t2s[:, a0:a1], in1=ymx[:, a0:a1], op=ALU.subtract)
+            nc.gpsimd.tensor_tensor(out=arg[:, a0:a1], in0=t2s[:, a0:a1], in1=ymx[:, a0:a1], op=ALU.subtract)
 
         def act_sqrt(a):
             nc.scalar.activation(out=y[a % R][:], in_=y[a % R][:], func=ACTF.Sqrt, bias=t2s[:, a:a + 1], scale=-1.0)
 
         def act_tiny(a0, a1):
-            nc.scalar.activation(out=lmin[:, a0:a1], in_=arg[:, a0:a1], func=ACTF.Sqrt)
+            nc.scalar.activation(out=dmin[:, a0:a1], in_=arg[:, a0:a1], func=ACTF.Sqrt)
+            nc.scalar.activation(out=lmin[:, a0:a1], in_=dmin[:, a0:a1], func=ACTF.Copy, scale=CSC)
 
         def act_exp(a):
-            nc.scalar.activation(out=e[a % RE][:], in_=y[a % R][:], func=ACTF.Exp, bias=lmin[:, a:a + 1], scale=-1.0, accum_out=rs[:, a:a + 1])
+            nc.scalar.activation(out=e[a % RE][:], in_=y[a % R][:], func=ACTF.Exp, bias=lmin[:, a:a + 1], scale=-CSC, accum_out=rs[:, a:a + 1])
 
         def back_pe(b):
             bank["t", b] = transpose8("T%d" % (b % 2), e[b % RE])
@@ -173,7 +190,12 @@ def tile_kanadjunction_pa_t_kernel(tc, source, target, k_right, WF_right, out):
             bank["o", q] = ob
 
         def fin(q):
-            nc.vector.reciprocal(out=rcp[:, 4 * q:4 * q + 4], in_=rs[:, 4 * q:4 * q + 4])
+            if st["rcp"] < 4 * q + 4:
+                hi = 4 * q + 4
+                while LAZY and hi + 4 <= NB and all(exp_old[hi:hi + 4]):
+                    hi += 4
+                nc.vector.reciprocal(out=rcp[:, st["rcp"]:hi], in_=rs[:, st["rcp"]:hi])
+                st["rcp"] = hi
             nc.vector.tensor_tensor(out=osb[q % NOS][:].rearrange("p (i d) -> p i d", i=4), in0=bank["o", q][:].rearrange("p (i d) -> p i d", i=4),
                                     in1=rcp[:, 4 * q:4 * q + 4].unsqueeze(2).to_broadcast([P, 4, P]), op=ALU.mult)
             o, h = divmod(q, 2)
@@ -251,11 +273,10 @@ def tile_kanadjunction_pa_t_kernel(tc, source, target, k_right, WF_right, out):
         for c in range(8):
             nc.scalar.activation(out=junk[:], in_=kr[:, c * P:(c + 1) * P], func=ACTF.Square, accum_out=k2[:, c:c + 1])
         for c in range(8):
-            nc.scalar.activation(out=junk[:], in_=tn[0][:, c * P:(c + 1) * P], func=ACTF.Square, accum_out=t20[:, c:c + 1])
-        nc.vector.tensor_scalar(out=kT[:], in0=kb[:], scalar1=2.0 ** -6, scalar2=None, op0=ALU.mult)
+            nc.scalar.activation(out=junk[:], in_=tn[0][:, c * P:(c + 1) * P], func=ACTF.Square, accum_out=t2s[:, c:c + 1])
+        nc.vector.tensor_scalar(out=kT[:], in0=kb[:], scalar1=2.0, scalar2=None, op0=ALU.mult)
         prep_cp(0)
-        nc.vector.tensor_scalar(out=negk[:], in0=k2[:].unsqueeze(2).to_broadcast([P, 8, P]), scalar1=-(2.0 ** -7), scalar2=None, op0=ALU.mult)
-        nc.vector.tensor_scalar(out=t2s[:, 0:8], in0=t20[:], scalar1=2.0 ** -7, scalar2=None, op0=ALU.mult)
+        nc.vector.tensor_scalar(out=negk[:], in0=k2[:].unsqueeze(2).to_broadcast([P, 8, P]), scalar1=-1.0, scalar2=None, op0=ALU.mult)
         front_pe(0)
 
         bounds = []
@@ -276,7 +297,9 @@ def tile_kanadjunction_pa_t_kernel(tc, source, target, k_right, WF_right, out):
             if acts[s][0] == "s":
                 need[s] = max(need[s], acts[s][1] + 1 + MARGIN)
         last_of = dict((b1 - 1, (b0, b1)) for (b0, b1) in bounds)
-        st = {"F": 0, "B": 0, "E": 0, "last": "F"}
+        st = {"F": 0, "B": 0, "E": 0, "last": "F", "rcp": 0}
+        exp_old = [False] * NB
+        recent = []
 
         def is_direct(q):
             return q >= QD or (q >= QA and q % 2 == 1)
@@ -311,8 +334,10 @@ def tile_kanadjunction_pa_t_kernel(tc, source, target, k_right, WF_right, out):
                 prep_sq(nc.gpsimd, oc + 1, (r + 4) * P, (r + 5) * P)
             if r == 2 and oc + 2 < NO:
                 prep_pe(oc + 2)
-            if r == 5 and oc + 1 < NO:
+            if r == 5 and oc + 1 < NO and T2PE:
                 prep_sum(oc + 1)
+            if r == 4 and oc + 1 < NO and L1:
+                prep_half(oc + 1)
             if a + 1 < NB:
                 front_pe(a + 1)
             front_v(a)
@@ -367,6 +392,9 @@ def tile_kanadjunction_pa_t_kernel(tc, source, target, k_right, WF_right, out):
                     unit_b()
                 act_exp(x)
                 exp_done[x] = True
+                recent.append(x)
+                if len(recent) > 6:
+                    exp_old[recent.pop(0)] = True
             if can_f() and st["F"] < need[s + 1]:
                 unit_f()
             elif extra:

@@ -26,15 +26,18 @@ R = 28
 RE = 16
 MARGIN = 2
 ALT = True
+RCP = 5
+CDA = 1000
+AB1 = 1
 LAZY = True
 L1 = True
 T2PE = False
 AB = 2
 TT_ON_ACT = True
 NQ = 32
-QA = 24
+QA = 32
 SLOPE = 0.55
-QD = 30
+QD = 25
 LM = 1
 LQ = 3
 NTN, NTT, NET, NG, NC, NOS = 4, 3, 2, 1, 2, 2
@@ -133,10 +136,11 @@ def tile_kanadjunction_pa_t_kernel(tc, source, target, k_right, WF_right, out):
             o, i = divmod(a, 8)
             for g in range(2):
                 yb = psum.tile([P, 512], F32, name="yb", tag="Y%d" % (2 * (a % 2) + g))
-                nc.tensor.matmul(yb[:], lhsT=tT[o % NTT][:, i * P:(i + 1) * P], rhs=kT[:, g * 512:(g + 1) * 512], start=True, stop=False)
                 for t in range(4):
-                    nc.tensor.matmul(yb[:, t * P:(t + 1) * P], lhsT=negk[:, 4 * g + t, :], rhs=ident_f[:], is_transpose=True, start=False, stop=(t == 3))
+                    nc.tensor.matmul(yb[:, t * P:(t + 1) * P], lhsT=negk[:, 4 * g + t, :], rhs=ident_f[:], is_transpose=True, start=(t == 0), stop=False)
                 bank["y", a, g] = yb
+            for g in range(2):
+                nc.tensor.matmul(bank["y", a, g][:], lhsT=tT[o % NTT][:, i * P:(i + 1) * P], rhs=kT[:, g * 512:(g + 1) * 512], start=False, stop=True)
 
         def front_v(a):
             for g in (1, 0):
@@ -170,8 +174,12 @@ def tile_kanadjunction_pa_t_kernel(tc, source, target, k_right, WF_right, out):
                                     scalar1=1.0, scalar2=0.0, op0=ALU.mult, op1=ALU.add)
 
         def back_cd(b):
-            nc.vector.tensor_copy(out=grd[b % 2][:].rearrange("p (g b t) -> p g b t", g=2, t=4),
-                                  in_=bank["t", b][:].rearrange("p (g t b) -> p g b t", g=2, t=4))
+            if b % CDA == CDA - 1:
+                nc.scalar.copy(out=grd[b % 2][:].rearrange("p (g b t) -> p g b t", g=2, t=4),
+                               in_=bank["t", b][:].rearrange("p (g t b) -> p g b t", g=2, t=4))
+            else:
+                nc.vector.tensor_copy(out=grd[b % 2][:].rearrange("p (g b t) -> p g b t", g=2, t=4),
+                                      in_=bank["t", b][:].rearrange("p (g t b) -> p g b t", g=2, t=4))
 
         def back_q4(q):
             nc.vector.quantize_mx(out=codes[q % NC][:].bitcast(FP8X4), scales=scl[q % NC][:], in_=grp[:])
@@ -288,8 +296,9 @@ def tile_kanadjunction_pa_t_kernel(tc, source, target, k_right, WF_right, out):
         acts = []
         for (b0, b1) in bounds:
             order = []
-            for c0 in range(b0, b1, AB):
-                order += list(reversed(range(c0, min(c0 + AB, b1))))
+            ab = AB1 if b0 == 0 else AB
+            for c0 in range(b0, b1, ab):
+                order += list(reversed(range(c0, min(c0 + ab, b1))))
             acts += [("s", a) for a in order] + [("t", (b0, b1))] + [("e", a) for a in order]
         need = [0.0] * (len(acts) + 1)
         for s in range(len(acts) - 1, -1, -1):
@@ -345,7 +354,7 @@ def tile_kanadjunction_pa_t_kernel(tc, source, target, k_right, WF_right, out):
                 prep_red(oc + 1)
             if oc == 0 and r == 0:
                 prep_cp(1)
-            if r == 3 and oc + 2 < NO:
+            if r == RCP and oc + 2 < NO:
                 prep_cp(oc + 2)
             if a in last_of:
                 v_tiny(*last_of[a])

@@ -1,8 +1,6 @@
 from contextlib import ExitStack
 
-import concourse.bass as bass
 import concourse.mybir as mybir
-import concourse.tile as tile
 from concourse.masks import make_identity
 
 FLOPS = 2 * 1024 * 512 * 128 + 2 * 2 * 16384 * 1024 * 128
@@ -13,34 +11,23 @@ U32 = mybir.dt.uint32
 U8 = mybir.dt.uint8
 FP8X4 = mybir.dt.float8_e4m3fn_x4
 ALU = mybir.AluOpType
-ACTF = mybir.ActivationFunctionType
+ACT = mybir.ActivationFunctionType
 AX = mybir.AxisListType
 
 P = 128
-CSC = 128.0 ** -0.5
-NKEY = 1024
-NB = 128
-NO = 16
+KEYS = 1024
+BLOCKS = 128
+OCTETS = BLOCKS // 8
+QUADS = BLOCKS // 4
+INV_ROOT = 128.0 ** -0.5
+
 GROUPS = [6, 10, 16, 24, 24, 24, 16, 8]
-R = 28
-RE = 16
-MARGIN = 2
-ALT = True
-RCP = 5
-CDA = 1000
-AB1 = 1
-LAZY = True
-L1 = True
-T2PE = False
-AB = 2
-TT_ON_ACT = True
-NQ = 32
-QA = 32
-SLOPE = 0.55
-QD = 25
-LM = 1
-LQ = 3
-NTN, NTT, NET, NG, NC, NOS = 4, 3, 2, 1, 2, 2
+DIST_SLOTS = 28
+E_SLOTS = 16
+LEAD = 2
+FRONT_PACE = 0.55
+VECTOR_QUADS = 25
+SRC_SLOTS = 5
 
 
 def tile_kanadjunction_pa_t_kernel(tc, source, target, k_right, WF_right, out):
@@ -52,365 +39,333 @@ def tile_kanadjunction_pa_t_kernel(tc, source, target, k_right, WF_right, out):
 
         ident_f = keep.tile([P, P], F32, name="ident_f")
         ident_b = keep.tile([P, P], BF16, name="ident_b")
-        kr = keep.tile([P, 1024], BF16, name="kr")
-        kT = keep.tile([P, 1024], BF16, name="kT")
-        k2 = keep.tile([P, 8], F32, name="k2")
-        negk = keep.tile([P, 8, P], F32, name="negk")
-        src = [keep.tile([P, 2048], BF16, name="src%d" % g, tag="y%d" % (R - 1 - g), align_bytes=64) for g in range(2)]
-        src_g = [keep.tile([P, 2048], BF16, name="src_g%d" % g, tag="y%d" % (R - 3 - g), align_bytes=64) for g in range(2)]
-        src_c = keep.tile([P, 1024], U32, name="src_c", tag="y%d" % (R - 5), align_bytes=64)
-        src_s = keep.tile([P, 1024], U8, name="src_s", align_bytes=64)
-        wf = keep.tile([P, 512], BF16, name="wf")
-        wf_g = keep.tile([P, 512], BF16, name="wf_g", align_bytes=64)
-        wf_c = keep.tile([P, 128], U32, name="wf_c", align_bytes=64)
-        wf_s = keep.tile([P, 128], U8, name="wf_s", align_bytes=64)
-        f_g = keep.tile([P, 1024], BF16, name="f_g", align_bytes=64)
-        f_c = keep.tile([P, 256], U32, name="f_c", align_bytes=64)
-        f_s = keep.tile([P, 256], U8, name="f_s", align_bytes=64)
-        ones2 = keep.tile([P, 2], F32, name="ones2")
-        sqh = keep.tile([P, 512], F32, name="sqh")
-        junk = keep.tile([P, P], F32, name="junk")
-        t2s = keep.tile([P, NB], F32, name="t2s")
-        ymax2 = keep.tile([P, 2 * NB], F32, name="ymax2")
-        ymx = keep.tile([P, NB], F32, name="ymx")
-        arg = keep.tile([P, NB], F32, name="arg")
-        lmin = keep.tile([P, NB], F32, name="lmin")
-        dmin = keep.tile([P, NB], F32, name="dmin")
-        rs = keep.tile([P, NB], F32, name="rs")
-        rcp = keep.tile([P, NB], F32, name="rcp")
-        sq = [keep.tile([P, 1024], F32, name="sq%d" % i) for i in range(2)]
-        tn = [keep.tile([P, 1024], BF16, name="tn%d" % i) for i in range(NTN)]
-        tT = [keep.tile([P, 1024], BF16, name="tT%d" % i) for i in range(NTT)]
-        y = [keep.tile([P, NKEY], F32, name="y%d" % i, align_bytes=64) for i in range(R - 5)]
-        e = [keep.tile([P, NKEY], BF16, name="e%d" % i) for i in range(RE)]
-        eT = [keep.tile([P, 4 * NKEY], BF16, name="eT%d" % i) for i in range(NET)]
-        grp = keep.tile([P, 4 * NKEY], BF16, name="grp", align_bytes=64)
-        grd = [keep.tile([P, NKEY], BF16, name="grd%d" % i, align_bytes=64) for i in range(2)]
-        codes = [keep.tile([P, 1024], U32, name="codes%d" % i, align_bytes=64) for i in range(NC)]
-        scl = [keep.tile([P, 1024], U8, name="scl%d" % i, align_bytes=64) for i in range(NC)]
-        osb = [keep.tile([P, 512], F32, name="osb%d" % i) for i in range(NOS)]
+        key_rows = keep.tile([P, KEYS], BF16, name="key_rows")
+        keysT = keep.tile([P, KEYS], BF16, name="keysT")
+        key_sq = keep.tile([P, 8], F32, name="key_sq")
+        neg_key_sq = keep.tile([P, 8, P], F32, name="neg_key_sq")
+        src_rows = [keep.tile([P, 2048], BF16, name="src_rows%d" % g, tag="dist%d" % (DIST_SLOTS - 1 - g), align_bytes=64) for g in range(2)]
+        src_grouped = [keep.tile([P, 2048], BF16, name="src_grouped%d" % g, tag="dist%d" % (DIST_SLOTS - 3 - g), align_bytes=64) for g in range(2)]
+        src_codes = keep.tile([P, 1024], U32, name="src_codes", tag="dist%d" % (DIST_SLOTS - 5), align_bytes=64)
+        src_scales = keep.tile([P, 1024], U8, name="src_scales", align_bytes=64)
+        wf_rows = keep.tile([P, 512], BF16, name="wf_rows")
+        wf_grouped = keep.tile([P, 512], BF16, name="wf_grouped", align_bytes=64)
+        wf_codes = keep.tile([P, P], U32, name="wf_codes", align_bytes=64)
+        wf_scales = keep.tile([P, P], U8, name="wf_scales", align_bytes=64)
+        f_grouped = keep.tile([P, 1024], BF16, name="f_grouped", align_bytes=64)
+        f_codes = keep.tile([P, 256], U32, name="f_codes", align_bytes=64)
+        f_scales = keep.tile([P, 256], U8, name="f_scales", align_bytes=64)
+        scratch = keep.tile([P, P], F32, name="scratch")
+        tgt_sq = keep.tile([P, BLOCKS], F32, name="tgt_sq")
+        bank_max = keep.tile([P, 2 * BLOCKS], F32, name="bank_max")
+        row_max = keep.tile([P, BLOCKS], F32, name="row_max")
+        min_d2 = keep.tile([P, BLOCKS], F32, name="min_d2")
+        min_dist = keep.tile([P, BLOCKS], F32, name="min_dist")
+        exp_bias = keep.tile([P, BLOCKS], F32, name="exp_bias")
+        row_sum = keep.tile([P, BLOCKS], F32, name="row_sum")
+        inv_sum = keep.tile([P, BLOCKS], F32, name="inv_sum")
+        squares = [keep.tile([P, 1024], F32, name="squares%d" % i) for i in range(2)]
+        half_sums = keep.tile([P, 512], F32, name="half_sums")
+        tgt_rows = [keep.tile([P, 1024], BF16, name="tgt_rows%d" % i) for i in range(4)]
+        tgtT = [keep.tile([P, 1024], BF16, name="tgtT%d" % i) for i in range(3)]
+        dist = [keep.tile([P, KEYS], F32, name="dist%d" % i, align_bytes=64) for i in range(DIST_SLOTS - SRC_SLOTS)]
+        e = [keep.tile([P, KEYS], BF16, name="e%d" % i) for i in range(E_SLOTS)]
+        eT = [keep.tile([P, 4 * KEYS], BF16, name="eT%d" % i) for i in range(2)]
+        grouped = keep.tile([P, 4 * KEYS], BF16, name="grouped", align_bytes=64)
+        grouped_v = [keep.tile([P, KEYS], BF16, name="grouped_v%d" % i, align_bytes=64) for i in range(2)]
+        codes = [keep.tile([P, 1024], U32, name="codes%d" % i, align_bytes=64) for i in range(2)]
+        scales = [keep.tile([P, 1024], U8, name="scales%d" % i, align_bytes=64) for i in range(2)]
+        out_sb = [keep.tile([P, 512], F32, name="out_sb%d" % i) for i in range(2)]
         bank = {}
 
-        def load_octet(o):
-            nc.sync.dma_start(out=tn[o % NTN][:], in_=target[o * 1024:(o + 1) * 1024, :].rearrange("(p i) e -> p (i e)", i=8))
-
-        def transpose8(tag, src_tile):
+        def transpose8(tag, rows):
             pb = psum.tile([P, 1024], BF16, name="pb_" + tag, tag=tag)
             for i in range(8):
-                nc.tensor.transpose(pb[:, i * P:(i + 1) * P], src_tile[:, i * P:(i + 1) * P], ident_b[:])
+                nc.tensor.transpose(pb[:, i * P:(i + 1) * P], rows[:, i * P:(i + 1) * P], ident_b[:])
             return pb
 
-        def prep_pe(o):
-            bank["x", o] = transpose8("X", tn[o % NTN])
+        def load_octet(o):
+            nc.sync.dma_start(out=tgt_rows[o % 4][:], in_=target[o * 1024:(o + 1) * 1024, :].rearrange("(p i) e -> p (i e)", i=8))
 
-        def prep_cp(o):
-            if TT_ON_ACT and o > 1:
-                nc.scalar.copy(out=tT[o % NTT][:], in_=bank["x", o][:])
-            else:
-                nc.vector.tensor_copy(out=tT[o % NTT][:], in_=bank["x", o][:])
+        def octet_transpose(o):
+            bank["x", o] = transpose8("X", tgt_rows[o % 4])
 
-        def prep_sq(eng, o, lo, hi):
-            rows = tT[o % NTT] if T2PE else tn[o % NTN]
-            eng.tensor_tensor(out=sq[o % 2][:, lo:hi], in0=rows[:, lo:hi], in1=rows[:, lo:hi], op=ALU.mult)
+        def octet_copy(engine_copy, o):
+            engine_copy(out=tgtT[o % 3][:], in_=bank["x", o][:])
 
-        def prep_half(o):
-            v = sq[o % 2][:].rearrange("p (i h e) -> p i h e", i=8, h=2)
-            nc.gpsimd.tensor_tensor(out=sqh[:].rearrange("p (i e) -> p i e", i=8), in0=v[:, :, 0, :], in1=v[:, :, 1, :], op=ALU.add)
+        def octet_square(o, lo, hi):
+            rows = tgt_rows[o % 4]
+            nc.gpsimd.tensor_tensor(out=squares[o % 2][:, lo:hi], in0=rows[:, lo:hi], in1=rows[:, lo:hi], op=ALU.mult)
 
-        def prep_sum(o):
-            xs = psum.tile([P, 16], F32, name="xs", tag="X")
-            for i in range(8):
-                nc.tensor.matmul(xs[:, 2 * i:2 * i + 2], lhsT=sq[o % 2][:, i * P:(i + 1) * P], rhs=ones2[:], start=True, stop=True)
-            bank["xs", o] = xs
+        def octet_halve(o):
+            v = squares[o % 2][:].rearrange("p (i h e) -> p i h e", i=8, h=2)
+            nc.gpsimd.tensor_tensor(out=half_sums[:].rearrange("p (i e) -> p i e", i=8), in0=v[:, :, 0, :], in1=v[:, :, 1, :], op=ALU.add)
 
-        def prep_red(o):
-            if not T2PE:
-                if L1:
-                    nc.vector.tensor_reduce(out=t2s[:, 8 * o:8 * o + 8], in_=sqh[:].rearrange("p (i e) -> p i e", i=8), axis=AX.X, op=ALU.add)
-                else:
-                    nc.vector.tensor_reduce(out=t2s[:, 8 * o:8 * o + 8], in_=sq[o % 2][:].rearrange("p (i e) -> p i e", i=8), axis=AX.X, op=ALU.add)
-                return
-            nc.vector.tensor_copy(out=t2s[:, 8 * o:8 * o + 8], in_=bank["xs", o][:].rearrange("p (i w) -> p i w", w=2)[:, :, 0])
+        def octet_reduce(o):
+            nc.vector.tensor_reduce(out=tgt_sq[:, 8 * o:8 * o + 8], in_=half_sums[:].rearrange("p (i e) -> p i e", i=8), axis=AX.X, op=ALU.add)
 
-        def front_pe(a):
+        def front_tensor(a):
             o, i = divmod(a, 8)
             for g in range(2):
                 yb = psum.tile([P, 512], F32, name="yb", tag="Y%d" % (2 * (a % 2) + g))
                 for t in range(4):
-                    nc.tensor.matmul(yb[:, t * P:(t + 1) * P], lhsT=negk[:, 4 * g + t, :], rhs=ident_f[:], is_transpose=True, start=(t == 0), stop=False)
+                    nc.tensor.matmul(yb[:, t * P:(t + 1) * P], lhsT=neg_key_sq[:, 4 * g + t, :], rhs=ident_f[:], is_transpose=True, start=(t == 0), stop=False)
                 bank["y", a, g] = yb
             for g in range(2):
-                nc.tensor.matmul(bank["y", a, g][:], lhsT=tT[o % NTT][:, i * P:(i + 1) * P], rhs=kT[:, g * 512:(g + 1) * 512], start=False, stop=True)
+                nc.tensor.matmul(bank["y", a, g][:], lhsT=tgtT[o % 3][:, i * P:(i + 1) * P], rhs=keysT[:, g * 512:(g + 1) * 512], start=False, stop=True)
 
-        def front_v(a):
+        def front_vector(a):
             for g in (1, 0):
-                nc.vector.tensor_scalar(out=y[a % R][:, g * 512:(g + 1) * 512], in0=bank["y", a, g][:], scalar1=t2s[:, a:a + 1], scalar2=None,
-                                        op0=ALU.min, op1=ALU.max, accum_out=ymax2[:, 2 * a + g:2 * a + g + 1])
+                nc.vector.tensor_scalar(out=dist[a % DIST_SLOTS][:, g * 512:(g + 1) * 512], in0=bank["y", a, g][:], scalar1=tgt_sq[:, a:a + 1], scalar2=None,
+                                        op0=ALU.min, op1=ALU.max, accum_out=bank_max[:, 2 * a + g:2 * a + g + 1])
 
-        def v_tiny(a0, a1):
-            nc.vector.tensor_reduce(out=ymx[:, a0:a1], in_=ymax2[:, 2 * a0:2 * a1].rearrange("p (a h) -> p a h", h=2), axis=AX.X, op=ALU.max)
-            nc.gpsimd.tensor_tensor(out=arg[:, a0:a1], in0=t2s[:, a0:a1], in1=ymx[:, a0:a1], op=ALU.subtract)
+        def group_min_d2(a0, a1):
+            nc.vector.tensor_reduce(out=row_max[:, a0:a1], in_=bank_max[:, 2 * a0:2 * a1].rearrange("p (a h) -> p a h", h=2), axis=AX.X, op=ALU.max)
+            nc.gpsimd.tensor_tensor(out=min_d2[:, a0:a1], in0=tgt_sq[:, a0:a1], in1=row_max[:, a0:a1], op=ALU.subtract)
 
-        def act_sqrt(a):
-            nc.scalar.activation(out=y[a % R][:], in_=y[a % R][:], func=ACTF.Sqrt, bias=t2s[:, a:a + 1], scale=-1.0)
+        def scalar_sqrt(a):
+            nc.scalar.activation(out=dist[a % DIST_SLOTS][:], in_=dist[a % DIST_SLOTS][:], func=ACT.Sqrt, bias=tgt_sq[:, a:a + 1], scale=-1.0)
 
-        def act_tiny(a0, a1):
-            nc.scalar.activation(out=dmin[:, a0:a1], in_=arg[:, a0:a1], func=ACTF.Sqrt)
-            nc.scalar.activation(out=lmin[:, a0:a1], in_=dmin[:, a0:a1], func=ACTF.Copy, scale=CSC)
+        def scalar_group_bias(a0, a1):
+            nc.scalar.activation(out=min_dist[:, a0:a1], in_=min_d2[:, a0:a1], func=ACT.Sqrt)
+            nc.scalar.activation(out=exp_bias[:, a0:a1], in_=min_dist[:, a0:a1], func=ACT.Copy, scale=INV_ROOT)
 
-        def act_exp(a):
-            nc.scalar.activation(out=e[a % RE][:], in_=y[a % R][:], func=ACTF.Exp, bias=lmin[:, a:a + 1], scale=-CSC, accum_out=rs[:, a:a + 1])
+        def scalar_exp(a):
+            nc.scalar.activation(out=e[a % E_SLOTS][:], in_=dist[a % DIST_SLOTS][:], func=ACT.Exp, bias=exp_bias[:, a:a + 1], scale=-INV_ROOT, accum_out=row_sum[:, a:a + 1])
 
-        def back_pe(b):
-            bank["t", b] = transpose8("T%d" % (b % 2), e[b % RE])
+        def back_transpose(b):
+            bank["t", b] = transpose8("T%d" % (b % 2), e[b % E_SLOTS])
 
-        def back_cp(b):
+        def back_copy(b):
             q, i = divmod(b, 4)
-            nc.vector.tensor_copy(out=eT[q % NET][:, i * NKEY:(i + 1) * NKEY], in_=bank["t", b][:])
+            nc.vector.tensor_copy(out=eT[q % 2][:, i * KEYS:(i + 1) * KEYS], in_=bank["t", b][:])
 
-        def back_rg(q):
-            nc.gpsimd.tensor_scalar(out=grp[:].rearrange("p (g b t) -> p g b t", g=8, t=4),
-                                    in0=eT[q % NET][:].rearrange("p (g t b) -> p g b t", g=8, t=4),
+        def back_regroup(q):
+            nc.gpsimd.tensor_scalar(out=grouped[:].rearrange("p (g b t) -> p g b t", g=8, t=4),
+                                    in0=eT[q % 2][:].rearrange("p (g t b) -> p g b t", g=8, t=4),
                                     scalar1=1.0, scalar2=0.0, op0=ALU.mult, op1=ALU.add)
 
-        def back_cd(b):
-            if b % CDA == CDA - 1:
-                nc.scalar.copy(out=grd[b % 2][:].rearrange("p (g b t) -> p g b t", g=2, t=4),
-                               in_=bank["t", b][:].rearrange("p (g t b) -> p g b t", g=2, t=4))
-            else:
-                nc.vector.tensor_copy(out=grd[b % 2][:].rearrange("p (g b t) -> p g b t", g=2, t=4),
-                                      in_=bank["t", b][:].rearrange("p (g t b) -> p g b t", g=2, t=4))
+        def back_copy_regrouped(b):
+            nc.vector.tensor_copy(out=grouped_v[b % 2][:].rearrange("p (g b t) -> p g b t", g=2, t=4),
+                                  in_=bank["t", b][:].rearrange("p (g t b) -> p g b t", g=2, t=4))
 
-        def back_q4(q):
-            nc.vector.quantize_mx(out=codes[q % NC][:].bitcast(FP8X4), scales=scl[q % NC][:], in_=grp[:])
+        def quantise_quad(q):
+            nc.vector.quantize_mx(out=codes[q % 2][:].bitcast(FP8X4), scales=scales[q % 2][:], in_=grouped[:])
 
-        def back_q1(b):
+        def quantise_block(b):
             q, i = divmod(b, 4)
-            nc.vector.quantize_mx(out=codes[q % NC][:, i * 256:(i + 1) * 256].bitcast(FP8X4), scales=scl[q % NC][:, i * 256:(i + 1) * 256], in_=grd[b % 2][:])
+            nc.vector.quantize_mx(out=codes[q % 2][:, i * 256:(i + 1) * 256].bitcast(FP8X4), scales=scales[q % 2][:, i * 256:(i + 1) * 256], in_=grouped_v[b % 2][:])
 
-        def mx(q):
+        def quad_products(q):
             ob = psum.tile([P, 512], F32, name="ob", tag="O")
             for i in range(4):
                 for g in range(2):
                     c0 = i * 256 + g * P
-                    nc.tensor.matmul_mx(out=ob[:, i * P:(i + 1) * P], lhsT=codes[q % NC][:, c0:c0 + P].bitcast(FP8X4), lhsT_scale=scl[q % NC][:, c0:c0 + P],
-                                        rhs=f_c[:, g * P:(g + 1) * P].bitcast(FP8X4), rhs_scale=f_s[:, g * P:(g + 1) * P], start=(g == 0), stop=(g == 1))
+                    nc.tensor.matmul_mx(out=ob[:, i * P:(i + 1) * P], lhsT=codes[q % 2][:, c0:c0 + P].bitcast(FP8X4), lhsT_scale=scales[q % 2][:, c0:c0 + P],
+                                        rhs=f_codes[:, g * P:(g + 1) * P].bitcast(FP8X4), rhs_scale=f_scales[:, g * P:(g + 1) * P], start=(g == 0), stop=(g == 1))
             bank["o", q] = ob
 
-        def fin(q):
-            if st["rcp"] < 4 * q + 4:
-                hi = 4 * q + 4
-                while LAZY and hi + 4 <= NB and all(exp_old[hi:hi + 4]):
-                    hi += 4
-                nc.vector.reciprocal(out=rcp[:, st["rcp"]:hi], in_=rs[:, st["rcp"]:hi])
-                st["rcp"] = hi
-            nc.vector.tensor_tensor(out=osb[q % NOS][:].rearrange("p (i d) -> p i d", i=4), in0=bank["o", q][:].rearrange("p (i d) -> p i d", i=4),
-                                    in1=rcp[:, 4 * q:4 * q + 4].unsqueeze(2).to_broadcast([P, 4, P]), op=ALU.mult)
+        def quad_finish(q):
+            nc.vector.reciprocal(out=inv_sum[:, 4 * q:4 * q + 4], in_=row_sum[:, 4 * q:4 * q + 4])
+            nc.vector.tensor_tensor(out=out_sb[q % 2][:].rearrange("p (i d) -> p i d", i=4), in0=bank["o", q][:].rearrange("p (i d) -> p i d", i=4),
+                                    in1=inv_sum[:, 4 * q:4 * q + 4].unsqueeze(2).to_broadcast([P, 4, P]), op=ALU.mult)
             o, h = divmod(q, 2)
-            nc.sync.dma_start(out=out[o * 1024:(o + 1) * 1024, :].rearrange("(p i) d -> p (i d)", i=8)[:, h * 512:(h + 1) * 512], in_=osb[q % NOS][:])
+            nc.sync.dma_start(out=out[o * 1024:(o + 1) * 1024, :].rearrange("(p i) d -> p (i d)", i=8)[:, h * 512:(h + 1) * 512], in_=out_sb[q % 2][:])
 
-        def words_pe(tag, rows, nchunk):
-            pw = psum.tile([P, 2 * nchunk * P], F32, name="pw_" + tag, tag=tag)
-            for c in range(nchunk):
+        def words_transpose(tag, rows, chunks):
+            pw = psum.tile([P, 2 * chunks * P], F32, name="pw_" + tag, tag=tag)
+            for c in range(chunks):
                 for u in range(2):
                     nc.tensor.transpose(pw[:, (2 * c + u) * P:(2 * c + u + 1) * P], rows[:, c * 512:(c + 1) * 512].bitcast(F32)[:, u * P:(u + 1) * P], ident_f[:])
             return pw
 
-        def words_cp(pw, dst, nchunk):
-            nc.vector.tensor_copy(out=dst.bitcast(F32).rearrange("w (c n u) -> w c n u", c=nchunk, u=2), in_=pw[:].rearrange("w (c u n) -> w c n u", c=nchunk, u=2))
+        def words_copy(pw, dst, chunks):
+            nc.vector.tensor_copy(out=dst.bitcast(F32).rearrange("w (c n u) -> w c n u", c=chunks, u=2), in_=pw[:].rearrange("w (c u n) -> w c n u", c=chunks, u=2))
 
-        def src_pe(j):
-            bank["s", j] = words_pe(["O", "T1"][j % 2], src[j // 2][:, (j % 2) * 1024:(j % 2 + 1) * 1024], 2)
+        def src_transpose(j):
+            bank["s", j] = words_transpose(["O", "T1"][j % 2], src_rows[j // 2][:, (j % 2) * 1024:(j % 2 + 1) * 1024], 2)
 
-        def src_cp(j):
-            words_cp(bank["s", j], src_g[j // 2][:, (j % 2) * 1024:(j % 2 + 1) * 1024], 2)
+        def src_copy(j):
+            words_copy(bank["s", j], src_grouped[j // 2][:, (j % 2) * 1024:(j % 2 + 1) * 1024], 2)
 
-        def wf_pe():
-            bank["w"] = words_pe("T0", wf[:], 1)
+        def f_step0():
+            bank["w"] = words_transpose("T0", wf_rows[:], 1)
+            src_transpose(0)
 
-        def f_mx():
+        def f_step1():
+            words_copy(bank["w"], wf_grouped[:], 1)
+            src_transpose(1)
+
+        def f_step2():
+            src_copy(0)
+            src_transpose(2)
+
+        def f_step3():
+            src_copy(1)
+            src_transpose(3)
+
+        def f_step4():
+            src_copy(2)
+            nc.vector.quantize_mx(out=wf_codes[:].bitcast(FP8X4), scales=wf_scales[:], in_=wf_grouped[:])
+
+        def f_step5():
+            src_copy(3)
+
+        def f_step6():
+            for g in range(2):
+                nc.vector.quantize_mx(out=src_codes[:, g * 512:(g + 1) * 512].bitcast(FP8X4), scales=src_scales[:, g * 512:(g + 1) * 512], in_=src_grouped[g][:])
             for g in range(2):
                 fb = psum.tile([P, 512], F32, name="fb", tag=["O", "T1"][g])
                 for t in range(4):
                     c = 4 * g + t
-                    nc.tensor.matmul_mx(out=fb[:, t * P:(t + 1) * P], lhsT=src_c[:, c * P:(c + 1) * P].bitcast(FP8X4), lhsT_scale=src_s[:, c * P:(c + 1) * P],
-                                        rhs=wf_c[:].bitcast(FP8X4), rhs_scale=wf_s[:], start=True, stop=True)
+                    nc.tensor.matmul_mx(out=fb[:, t * P:(t + 1) * P], lhsT=src_codes[:, c * P:(c + 1) * P].bitcast(FP8X4), lhsT_scale=src_scales[:, c * P:(c + 1) * P],
+                                        rhs=wf_codes[:].bitcast(FP8X4), rhs_scale=wf_scales[:], start=True, stop=True)
                 bank["f", g] = fb
 
-        def f_cp(g):
-            nc.vector.tensor_copy(out=f_g[:, g * 512:(g + 1) * 512].rearrange("p (d t) -> p d t", t=4), in_=bank["f", g][:].rearrange("p (t d) -> p d t", t=4))
-
-        def x0():
-            wf_pe(); src_pe(0)
-        def x1():
-            words_cp(bank["w"], wf_g[:], 1); src_pe(1)
-        def x2():
-            src_cp(0); src_pe(2)
-        def x3():
-            src_cp(1); src_pe(3)
-        def x4():
-            src_cp(2)
-            nc.vector.quantize_mx(out=wf_c[:].bitcast(FP8X4), scales=wf_s[:], in_=wf_g[:])
-        def x5():
-            src_cp(3)
-        def x6():
+        def f_step7():
             for g in range(2):
-                nc.vector.quantize_mx(out=src_c[:, g * 512:(g + 1) * 512].bitcast(FP8X4), scales=src_s[:, g * 512:(g + 1) * 512], in_=src_g[g][:])
-            f_mx()
-        def x7():
-            f_cp(0); f_cp(1)
-        def x8():
-            nc.vector.quantize_mx(out=f_c[:].bitcast(FP8X4), scales=f_s[:], in_=f_g[:])
-        extra = [x0, x1, x2, x3, x4, x5, x6, x7, x8]
+                nc.vector.tensor_copy(out=f_grouped[:, g * 512:(g + 1) * 512].rearrange("p (d t) -> p d t", t=4), in_=bank["f", g][:].rearrange("p (t d) -> p d t", t=4))
 
-        nc.sync.dma_start(out=kr[:].rearrange("p (g x) -> p g x", g=2), in_=k_right.rearrange("(g p t) e -> p g (t e)", g=2, t=4))
+        def f_step8():
+            nc.vector.quantize_mx(out=f_codes[:].bitcast(FP8X4), scales=f_scales[:], in_=f_grouped[:])
+
+        f_steps = [f_step0, f_step1, f_step2, f_step3, f_step4, f_step5, f_step6, f_step7, f_step8]
+
+        def finish_f():
+            while f_steps:
+                f_steps.pop(0)()
+
+        nc.sync.dma_start(out=key_rows[:].rearrange("p (g x) -> p g x", g=2), in_=k_right.rearrange("(g p t) e -> p g (t e)", g=2, t=4))
         load_octet(0)
-        nc.sync.dma_start(out=wf[:], in_=WF_right)
+        nc.sync.dma_start(out=wf_rows[:], in_=WF_right)
         for g in range(2):
-            nc.sync.dma_start(out=src[g][:], in_=source[g * 512:(g + 1) * 512, :].rearrange("(p t) c -> p (t c)", t=4))
+            nc.sync.dma_start(out=src_rows[g][:], in_=source[g * 512:(g + 1) * 512, :].rearrange("(p t) c -> p (t c)", t=4))
         load_octet(1)
         load_octet(2)
         load_octet(3)
         make_identity(nc, ident_b[:])
         make_identity(nc, ident_f[:])
-        nc.gpsimd.memset(ones2[:], 1.0)
-        nc.vector.memset(junk[:, 0:1], 1.0)
-        nc.scalar.activation(out=junk[:, 1:2], in_=junk[:, 0:1], func=ACTF.Sqrt)
-        kb = transpose8("T0", kr)
-        prep_pe(0)
+        nc.vector.memset(scratch[:, 0:1], 1.0)
+        nc.scalar.activation(out=scratch[:, 1:2], in_=scratch[:, 0:1], func=ACT.Sqrt)
+        keys_bank = transpose8("T0", key_rows)
+        octet_transpose(0)
         for c in range(8):
-            nc.scalar.activation(out=junk[:], in_=kr[:, c * P:(c + 1) * P], func=ACTF.Square, accum_out=k2[:, c:c + 1])
+            nc.scalar.activation(out=scratch[:], in_=key_rows[:, c * P:(c + 1) * P], func=ACT.Square, accum_out=key_sq[:, c:c + 1])
         for c in range(8):
-            nc.scalar.activation(out=junk[:], in_=tn[0][:, c * P:(c + 1) * P], func=ACTF.Square, accum_out=t2s[:, c:c + 1])
-        nc.vector.tensor_scalar(out=kT[:], in0=kb[:], scalar1=2.0, scalar2=None, op0=ALU.mult)
-        prep_cp(0)
-        nc.vector.tensor_scalar(out=negk[:], in0=k2[:].unsqueeze(2).to_broadcast([P, 8, P]), scalar1=-1.0, scalar2=None, op0=ALU.mult)
-        front_pe(0)
+            nc.scalar.activation(out=scratch[:], in_=tgt_rows[0][:, c * P:(c + 1) * P], func=ACT.Square, accum_out=tgt_sq[:, c:c + 1])
+        nc.vector.tensor_scalar(out=keysT[:], in0=keys_bank[:], scalar1=2.0, scalar2=None, op0=ALU.mult)
+        octet_copy(nc.vector.tensor_copy, 0)
+        nc.vector.tensor_scalar(out=neg_key_sq[:], in0=key_sq[:].unsqueeze(2).to_broadcast([P, 8, P]), scalar1=-1.0, scalar2=None, op0=ALU.mult)
+        front_tensor(0)
 
-        bounds = []
-        a0 = 0
-        for gsz in GROUPS:
-            bounds.append((a0, a0 + gsz))
-            a0 += gsz
-        assert a0 == NB
-        acts = []
-        for (b0, b1) in bounds:
-            order = []
-            ab = AB1 if b0 == 0 else AB
-            for c0 in range(b0, b1, ab):
-                order += list(reversed(range(c0, min(c0 + ab, b1))))
-            acts += [("s", a) for a in order] + [("t", (b0, b1))] + [("e", a) for a in order]
-        need = [0.0] * (len(acts) + 1)
-        for s in range(len(acts) - 1, -1, -1):
-            need[s] = need[s + 1] - SLOPE
-            if acts[s][0] == "s":
-                need[s] = max(need[s], acts[s][1] + 1 + MARGIN)
-        last_of = dict((b1 - 1, (b0, b1)) for (b0, b1) in bounds)
-        st = {"F": 0, "B": 0, "E": 0, "last": "F", "rcp": 0}
-        exp_old = [False] * NB
-        recent = []
+        scalar_order = []
+        group_of_last = {}
+        first = 0
+        for size in GROUPS:
+            last = first + size
+            pair = 1 if first == 0 else 2
+            assert size % pair == 0
+            blocks = []
+            for c0 in range(first, last, pair):
+                blocks += list(reversed(range(c0, c0 + pair)))
+            scalar_order += [("sqrt", a) for a in blocks] + [("bias", (first, last))] + [("exp", a) for a in blocks]
+            group_of_last[last - 1] = (first, last)
+            first = last
+        assert first == BLOCKS
+        front_needed = [0.0] * (len(scalar_order) + 1)
+        for s in range(len(scalar_order) - 1, -1, -1):
+            front_needed[s] = front_needed[s + 1] - FRONT_PACE
+            if scalar_order[s][0] == "sqrt":
+                front_needed[s] = max(front_needed[s], scalar_order[s][1] + 1 + LEAD)
+        quantise_at = [4 * q + 7 for q in range(QUADS)]
+        products_at = [(4 * q + 8 if q < VECTOR_QUADS else 4 * q + 6) for q in range(QUADS)]
+        done = {"front": 0, "back": 0, "last": "front"}
+        exp_written = [False] * BLOCKS
 
-        def is_direct(q):
-            return q >= QD or (q >= QA and q % 2 == 1)
+        def front_possible():
+            a = done["front"]
+            return a < BLOCKS and (a < DIST_SLOTS or exp_written[a - DIST_SLOTS])
 
-        mx_at = [(4 * q + 6 if is_direct(q) else 4 * q + 4 + LQ + LM) for q in range(NQ)]
+        def back_possible():
+            return done["back"] < BLOCKS and exp_written[done["back"]]
 
-        exp_done = [False] * NB
-
-        def can_f():
-            return st["F"] < NB and (st["F"] < R or exp_done[st["F"] - R])
-
-        def can_b():
-            return st["B"] < NB and exp_done[st["B"]]
-
-        def unit_f():
-            a = st["F"]
-            oc, r = divmod(a, 8)
-            if len(y) <= a < R:
-                while extra:
-                    extra.pop(0)()
-                y.append(keep.tile([P, NKEY], F32, name="y%d" % a, align_bytes=64))
-            if oc == 0:
+        def front_unit():
+            a = done["front"]
+            o, r = divmod(a, 8)
+            if len(dist) <= a < DIST_SLOTS:
+                finish_f()
+                dist.append(keep.tile([P, KEYS], F32, name="dist%d" % a, align_bytes=64))
+            if o == 0:
                 if r == 0:
-                    prep_pe(1)
+                    octet_transpose(1)
                 if 1 <= r <= 4:
-                    prep_sq(nc.gpsimd, 1, (r - 1) * 256, r * 256)
-            if r == 4 and oc + 4 < NO:
-                load_octet(oc + 4)
-            if r >= 4 and oc + 2 < NO:
-                prep_sq(nc.gpsimd, oc + 2, (r - 4) * P, (r - 3) * P)
-            if r < 4 and 2 <= oc + 1 < NO:
-                prep_sq(nc.gpsimd, oc + 1, (r + 4) * P, (r + 5) * P)
-            if r == 2 and oc + 2 < NO:
-                prep_pe(oc + 2)
-            if r == 5 and oc + 1 < NO and T2PE:
-                prep_sum(oc + 1)
-            if r == 4 and oc + 1 < NO and L1:
-                prep_half(oc + 1)
-            if a + 1 < NB:
-                front_pe(a + 1)
-            front_v(a)
-            if r == 6 and oc + 1 < NO:
-                prep_red(oc + 1)
-            if oc == 0 and r == 0:
-                prep_cp(1)
-            if r == RCP and oc + 2 < NO:
-                prep_cp(oc + 2)
-            if a in last_of:
-                v_tiny(*last_of[a])
-            st["F"] += 1
-            st["last"] = "F"
+                    octet_square(1, (r - 1) * 256, r * 256)
+            if r == 4 and o + 4 < OCTETS:
+                load_octet(o + 4)
+            if r >= 4 and o + 2 < OCTETS:
+                octet_square(o + 2, (r - 4) * P, (r - 3) * P)
+            if r < 4 and 2 <= o + 1 < OCTETS:
+                octet_square(o + 1, (r + 4) * P, (r + 5) * P)
+            if r == 2 and o + 2 < OCTETS:
+                octet_transpose(o + 2)
+            if r == 4 and o + 1 < OCTETS:
+                octet_halve(o + 1)
+            if a + 1 < BLOCKS:
+                front_tensor(a + 1)
+            front_vector(a)
+            if r == 6 and o + 1 < OCTETS:
+                octet_reduce(o + 1)
+            if o == 0 and r == 0:
+                octet_copy(nc.vector.tensor_copy, 1)
+            if r == 5 and o + 2 < OCTETS:
+                octet_copy(nc.scalar.copy, o + 2)
+            if a in group_of_last:
+                group_min_d2(*group_of_last[a])
+            done["front"] += 1
+            done["last"] = "front"
 
-        def unit_b():
-            n = st["B"]
-            for q in range(NQ):
-                if n == mx_at[q]:
-                    while extra:
-                        extra.pop(0)()
-                    mx(q)
-            if n < NB:
-                back_pe(n)
+        def back_unit():
+            n = done["back"]
+            if n in products_at:
+                finish_f()
+                quad_products(products_at.index(n))
+            if n < BLOCKS:
+                back_transpose(n)
             b = n - 1
-            if 0 <= b < NB:
-                if not is_direct(b // 4):
-                    back_cp(b)
+            if 0 <= b < BLOCKS:
+                if b // 4 < VECTOR_QUADS:
+                    back_copy(b)
                     if b % 4 == 3:
-                        back_rg(b // 4)
+                        back_regroup(b // 4)
                 else:
-                    back_cd(b)
-            for q in range(NQ):
-                if not is_direct(q) and n == 4 * q + 4 + LQ:
-                    back_q4(q)
-            if 0 <= n - 2 < NB and is_direct((n - 2) // 4):
-                back_q1(n - 2)
-            for q in range(NQ):
-                if n == mx_at[q] + 1:
-                    fin(q)
-            st["B"] += 1
-            st["last"] = "B"
+                    back_copy_regrouped(b)
+            if n in quantise_at and quantise_at.index(n) < VECTOR_QUADS:
+                quantise_quad(quantise_at.index(n))
+            if 0 <= n - 2 < BLOCKS and (n - 2) // 4 >= VECTOR_QUADS:
+                quantise_block(n - 2)
+            if n - 1 in products_at:
+                quad_finish(products_at.index(n - 1))
+            done["back"] += 1
+            done["last"] = "back"
 
-        for s, (kind, x) in enumerate(acts):
-            if kind == "s":
-                while st["F"] <= x:
-                    unit_f()
-                act_sqrt(x)
-            elif kind == "t":
-                act_tiny(*x)
+        for s, (kind, x) in enumerate(scalar_order):
+            if kind == "sqrt":
+                while done["front"] <= x:
+                    front_unit()
+                scalar_sqrt(x)
+            elif kind == "bias":
+                scalar_group_bias(*x)
             else:
-                while st["B"] <= x - RE:
-                    unit_b()
-                act_exp(x)
-                exp_done[x] = True
-                recent.append(x)
-                if len(recent) > 6:
-                    exp_old[recent.pop(0)] = True
-            if can_f() and st["F"] < need[s + 1]:
-                unit_f()
-            elif extra:
-                extra.pop(0)()
-            elif can_b() and (st["last"] != "B" or not can_f() or not ALT):
-                unit_b()
-            elif can_f():
-                unit_f()
-        while st["B"] < NB + 8 + LQ + LM:
-            unit_b()
+                while done["back"] <= x - E_SLOTS:
+                    back_unit()
+                scalar_exp(x)
+                exp_written[x] = True
+            if front_possible() and done["front"] < front_needed[s + 1]:
+                front_unit()
+            elif f_steps:
+                f_steps.pop(0)()
+            elif back_possible() and (done["last"] != "back" or not front_possible()):
+                back_unit()
+            elif front_possible():
+                front_unit()
+        while done["back"] <= products_at[QUADS - 1] + 1:
+            back_unit()

@@ -21,7 +21,7 @@ OCTETS = BLOCKS // 8
 QUADS = BLOCKS // 4
 INV_ROOT = 128.0 ** -0.5
 
-GROUPS = [6, 10, 16, 24, 24, 24, 16, 8]
+GROUPS = [8, 24, 24, 24, 24, 24]
 DIST_SLOTS = 28
 E_SLOTS = 16
 LEAD = 2

@@ -24,8 +24,7 @@ INV_ROOT = 128.0 ** -0.5
 GROUPS = [8, 24, 24, 24, 24, 24]
 DIST_SLOTS = 28
 E_SLOTS = 16
-LEAD = 2
-FRONT_PACE = 0.55
+AHEAD = 29
 VECTOR_QUADS = 25
 SRC_SLOTS = 5
 
@@ -187,52 +186,31 @@ def tile_kanadjunction_pa_t_kernel(tc, source, target, k_right, WF_right, out):
         def src_copy(j):
             words_copy(bank["s", j], src_grouped[j // 2][:, (j % 2) * 1024:(j % 2 + 1) * 1024], 2)
 
-        def f_step0():
-            bank["w"] = words_transpose("T0", wf_rows[:], 1)
+        def prepare_f():
+            wf_bank = words_transpose("T0", wf_rows[:], 1)
             src_transpose(0)
-
-        def f_step1():
-            words_copy(bank["w"], wf_grouped[:], 1)
+            words_copy(wf_bank, wf_grouped[:], 1)
             src_transpose(1)
-
-        def f_step2():
             src_copy(0)
             src_transpose(2)
-
-        def f_step3():
             src_copy(1)
             src_transpose(3)
-
-        def f_step4():
             src_copy(2)
             nc.vector.quantize_mx(out=wf_codes[:].bitcast(FP8X4), scales=wf_scales[:], in_=wf_grouped[:])
-
-        def f_step5():
             src_copy(3)
-
-        def f_step6():
             for g in range(2):
                 nc.vector.quantize_mx(out=src_codes[:, g * 512:(g + 1) * 512].bitcast(FP8X4), scales=src_scales[:, g * 512:(g + 1) * 512], in_=src_grouped[g][:])
+            f_banks = []
             for g in range(2):
                 fb = psum.tile([P, 512], F32, name="fb", tag=["O", "T1"][g])
                 for t in range(4):
                     c = 4 * g + t
                     nc.tensor.matmul_mx(out=fb[:, t * P:(t + 1) * P], lhsT=src_codes[:, c * P:(c + 1) * P].bitcast(FP8X4), lhsT_scale=src_scales[:, c * P:(c + 1) * P],
                                         rhs=wf_codes[:].bitcast(FP8X4), rhs_scale=wf_scales[:], start=True, stop=True)
-                bank["f", g] = fb
-
-        def f_step7():
+                f_banks.append(fb)
             for g in range(2):
-                nc.vector.tensor_copy(out=f_grouped[:, g * 512:(g + 1) * 512].rearrange("p (d t) -> p d t", t=4), in_=bank["f", g][:].rearrange("p (t d) -> p d t", t=4))
-
-        def f_step8():
+                nc.vector.tensor_copy(out=f_grouped[:, g * 512:(g + 1) * 512].rearrange("p (d t) -> p d t", t=4), in_=f_banks[g][:].rearrange("p (t d) -> p d t", t=4))
             nc.vector.quantize_mx(out=f_codes[:].bitcast(FP8X4), scales=f_scales[:], in_=f_grouped[:])
-
-        f_steps = [f_step0, f_step1, f_step2, f_step3, f_step4, f_step5, f_step6, f_step7, f_step8]
-
-        def finish_f():
-            while f_steps:
-                f_steps.pop(0)()
 
         nc.sync.dma_start(out=key_rows[:].rearrange("p (g x) -> p g x", g=2), in_=k_right.rearrange("(g p t) e -> p g (t e)", g=2, t=4))
         load_octet(0)
@@ -271,29 +249,14 @@ def tile_kanadjunction_pa_t_kernel(tc, source, target, k_right, WF_right, out):
             group_of_last[last - 1] = (first, last)
             first = last
         assert first == BLOCKS
-        front_needed = [0.0] * (len(scalar_order) + 1)
-        for s in range(len(scalar_order) - 1, -1, -1):
-            front_needed[s] = front_needed[s + 1] - FRONT_PACE
-            if scalar_order[s][0] == "sqrt":
-                front_needed[s] = max(front_needed[s], scalar_order[s][1] + 1 + LEAD)
         quantise_at = [4 * q + 7 for q in range(QUADS)]
         products_at = [(4 * q + 8 if q < VECTOR_QUADS else 4 * q + 6) for q in range(QUADS)]
-        done = {"front": 0, "back": 0, "last": "front"}
+        written = {"front": 0, "back": 0, "scalar": 0}
         exp_written = [False] * BLOCKS
 
-        def front_possible():
-            a = done["front"]
-            return a < BLOCKS and (a < DIST_SLOTS or exp_written[a - DIST_SLOTS])
-
-        def back_possible():
-            return done["back"] < BLOCKS and exp_written[done["back"]]
-
-        def front_unit():
-            a = done["front"]
+        def front_unit(a):
+            assert a < DIST_SLOTS or exp_written[a - DIST_SLOTS]
             o, r = divmod(a, 8)
-            if len(dist) <= a < DIST_SLOTS:
-                finish_f()
-                dist.append(keep.tile([P, KEYS], F32, name="dist%d" % a, align_bytes=64))
             if o == 0:
                 if r == 0:
                     octet_transpose(1)
@@ -320,13 +283,11 @@ def tile_kanadjunction_pa_t_kernel(tc, source, target, k_right, WF_right, out):
                 octet_copy(nc.scalar.copy, o + 2)
             if a in group_of_last:
                 group_min_d2(*group_of_last[a])
-            done["front"] += 1
-            done["last"] = "front"
+            written["front"] = a + 1
 
-        def back_unit():
-            n = done["back"]
+        def back_unit(n):
+            assert n >= BLOCKS or exp_written[n]
             if n in products_at:
-                finish_f()
                 quad_products(products_at.index(n))
             if n < BLOCKS:
                 back_transpose(n)
@@ -344,28 +305,34 @@ def tile_kanadjunction_pa_t_kernel(tc, source, target, k_right, WF_right, out):
                 quantise_block(n - 2)
             if n - 1 in products_at:
                 quad_finish(products_at.index(n - 1))
-            done["back"] += 1
-            done["last"] = "back"
+            written["back"] = n + 1
 
-        for s, (kind, x) in enumerate(scalar_order):
-            if kind == "sqrt":
-                while done["front"] <= x:
-                    front_unit()
-                scalar_sqrt(x)
-            elif kind == "bias":
+        def scalar_unit():
+            while written["scalar"] < len(scalar_order):
+                kind, x = scalar_order[written["scalar"]]
+                written["scalar"] += 1
+                if kind == "sqrt":
+                    assert x < written["front"]
+                    scalar_sqrt(x)
+                    return
+                if kind == "exp":
+                    assert x - E_SLOTS < written["back"]
+                    scalar_exp(x)
+                    exp_written[x] = True
+                    return
                 scalar_group_bias(*x)
-            else:
-                while done["back"] <= x - E_SLOTS:
-                    back_unit()
-                scalar_exp(x)
-                exp_written[x] = True
-            if front_possible() and done["front"] < front_needed[s + 1]:
-                front_unit()
-            elif f_steps:
-                f_steps.pop(0)()
-            elif back_possible() and (done["last"] != "back" or not front_possible()):
-                back_unit()
-            elif front_possible():
-                front_unit()
-        while done["back"] <= products_at[QUADS - 1] + 1:
-            back_unit()
+
+        for a in range(AHEAD):
+            if a == DIST_SLOTS - SRC_SLOTS:
+                prepare_f()
+                dist += [keep.tile([P, KEYS], F32, name="dist%d" % i, align_bytes=64) for i in range(len(dist), DIST_SLOTS)]
+            front_unit(a)
+            scalar_unit()
+        for n in range(products_at[QUADS - 1] + 2):
+            while n < BLOCKS and not exp_written[n]:
+                scalar_unit()
+            back_unit(n)
+            scalar_unit()
+            if n + AHEAD < BLOCKS:
+                front_unit(n + AHEAD)
+                scalar_unit()

@@ -25,7 +25,6 @@ GROUPS = [8, 24, 24, 24, 24, 24]
 DIST_SLOTS = 28
 E_SLOTS = 16
 AHEAD = 29
-VECTOR_QUADS = 25
 SRC_SLOTS = 5
 
 
@@ -68,9 +67,7 @@ def tile_kanadjunction_pa_t_kernel(tc, source, target, k_right, WF_right, out):
         tgtT = [keep.tile([P, 1024], BF16, name="tgtT%d" % i) for i in range(3)]
         dist = [keep.tile([P, KEYS], F32, name="dist%d" % i, align_bytes=64) for i in range(DIST_SLOTS - SRC_SLOTS)]
         e = [keep.tile([P, KEYS], BF16, name="e%d" % i) for i in range(E_SLOTS)]
-        eT = [keep.tile([P, 4 * KEYS], BF16, name="eT%d" % i) for i in range(2)]
-        grouped = keep.tile([P, 4 * KEYS], BF16, name="grouped", align_bytes=64)
-        grouped_v = [keep.tile([P, KEYS], BF16, name="grouped_v%d" % i, align_bytes=64) for i in range(2)]
+        grouped = [keep.tile([P, KEYS], BF16, name="grouped%d" % i, align_bytes=64) for i in range(2)]
         codes = [keep.tile([P, 1024], U32, name="codes%d" % i, align_bytes=64) for i in range(2)]
         scales = [keep.tile([P, 1024], U8, name="scales%d" % i, align_bytes=64) for i in range(2)]
         out_sb = [keep.tile([P, 512], F32, name="out_sb%d" % i) for i in range(2)]
@@ -107,7 +104,8 @@ def tile_kanadjunction_pa_t_kernel(tc, source, target, k_right, WF_right, out):
             for g in range(2):
                 yb = psum.tile([P, 512], F32, name="yb", tag="Y%d" % (2 * (a % 2) + g))
                 for t in range(4):
-                    nc.tensor.matmul(yb[:, t * P:(t + 1) * P], lhsT=neg_key_sq[:, 4 * g + t, :], rhs=ident_f[:], is_transpose=True, start=(t == 0), stop=False)
+                    u, h = divmod(t, 2)
+                    nc.tensor.matmul(yb[:, t * P:(t + 1) * P], lhsT=neg_key_sq[:, 4 * u + 2 * g + h, :], rhs=ident_f[:], is_transpose=True, start=(t == 0), stop=False)
                 bank["y", a, g] = yb
             for g in range(2):
                 nc.tensor.matmul(bank["y", a, g][:], lhsT=tgtT[o % 3][:, i * P:(i + 1) * P], rhs=keysT[:, g * 512:(g + 1) * 512], start=False, stop=True)
@@ -132,27 +130,14 @@ def tile_kanadjunction_pa_t_kernel(tc, source, target, k_right, WF_right, out):
             nc.scalar.activation(out=e[a % E_SLOTS][:], in_=dist[a % DIST_SLOTS][:], func=ACT.Exp, bias=exp_bias[:, a:a + 1], scale=-INV_ROOT, accum_out=row_sum[:, a:a + 1])
 
         def back_transpose(b):
-            bank["t", b] = transpose8("T%d" % (b % 2), e[b % E_SLOTS])
+            bank["t", b] = words_transpose("T%d" % (b % 2), e[b % E_SLOTS], 2)
 
         def back_copy(b):
-            q, i = divmod(b, 4)
-            nc.vector.tensor_copy(out=eT[q % 2][:, i * KEYS:(i + 1) * KEYS], in_=bank["t", b][:])
-
-        def back_regroup(q):
-            nc.gpsimd.tensor_scalar(out=grouped[:].rearrange("p (g b t) -> p g b t", g=8, t=4),
-                                    in0=eT[q % 2][:].rearrange("p (g t b) -> p g b t", g=8, t=4),
-                                    scalar1=1.0, scalar2=0.0, op0=ALU.mult, op1=ALU.add)
-
-        def back_copy_regrouped(b):
-            nc.vector.tensor_copy(out=grouped_v[b % 2][:].rearrange("p (g b t) -> p g b t", g=2, t=4),
-                                  in_=bank["t", b][:].rearrange("p (g t b) -> p g b t", g=2, t=4))
-
-        def quantise_quad(q):
-            nc.vector.quantize_mx(out=codes[q % 2][:].bitcast(FP8X4), scales=scales[q % 2][:], in_=grouped[:])
+            words_copy(bank["t", b], grouped[b % 2][:], 2)
 
         def quantise_block(b):
             q, i = divmod(b, 4)
-            nc.vector.quantize_mx(out=codes[q % 2][:, i * 256:(i + 1) * 256].bitcast(FP8X4), scales=scales[q % 2][:, i * 256:(i + 1) * 256], in_=grouped_v[b % 2][:])
+            nc.vector.quantize_mx(out=codes[q % 2][:, i * 256:(i + 1) * 256].bitcast(FP8X4), scales=scales[q % 2][:, i * 256:(i + 1) * 256], in_=grouped[b % 2][:])
 
         def quad_products(q):
             ob = psum.tile([P, 512], F32, name="ob", tag="O")
@@ -212,7 +197,9 @@ def tile_kanadjunction_pa_t_kernel(tc, source, target, k_right, WF_right, out):
                 nc.vector.tensor_copy(out=f_grouped[:, g * 512:(g + 1) * 512].rearrange("p (d t) -> p d t", t=4), in_=f_banks[g][:].rearrange("p (t d) -> p d t", t=4))
             nc.vector.quantize_mx(out=f_codes[:].bitcast(FP8X4), scales=f_scales[:], in_=f_grouped[:])
 
-        nc.sync.dma_start(out=key_rows[:].rearrange("p (g x) -> p g x", g=2), in_=k_right.rearrange("(g p t) e -> p g (t e)", g=2, t=4))
+        for u in range(2):
+            for v in range(2):
+                nc.sync.dma_start(out=key_rows[v:P:2, u * 512:(u + 1) * 512].rearrange("p (s e) -> p s e", s=4), in_=k_right.rearrange("(s p w) e -> w p s e", s=4, w=4)[2 * u + v])
         load_octet(0)
         nc.sync.dma_start(out=wf_rows[:], in_=WF_right)
         for g in range(2):
@@ -224,7 +211,12 @@ def tile_kanadjunction_pa_t_kernel(tc, source, target, k_right, WF_right, out):
         make_identity(nc, ident_f[:])
         nc.vector.memset(scratch[:, 0:1], 1.0)
         nc.scalar.activation(out=scratch[:, 1:2], in_=scratch[:, 0:1], func=ACT.Sqrt)
-        keys_bank = transpose8("T0", key_rows)
+        keys_bank = psum.tile([P, 1024], BF16, name="keys_bank", tag="T0")
+        for g in range(2):
+            for u in range(2):
+                for h in range(2):
+                    c, s = 4 * g + 2 * u + h, 4 * u + 2 * g + h
+                    nc.tensor.transpose(keys_bank[:, c * P:(c + 1) * P], key_rows[:, s * P:(s + 1) * P], ident_b[:])
         octet_transpose(0)
         for c in range(8):
             nc.scalar.activation(out=scratch[:], in_=key_rows[:, c * P:(c + 1) * P], func=ACT.Square, accum_out=key_sq[:, c:c + 1])
@@ -249,8 +241,7 @@ def tile_kanadjunction_pa_t_kernel(tc, source, target, k_right, WF_right, out):
             group_of_last[last - 1] = (first, last)
             first = last
         assert first == BLOCKS
-        quantise_at = [4 * q + 7 for q in range(QUADS)]
-        products_at = [(4 * q + 8 if q < VECTOR_QUADS else 4 * q + 6) for q in range(QUADS)]
+        products_at = [4 * q + 6 for q in range(QUADS)]
         written = {"front": 0, "back": 0, "scalar": 0}
         exp_written = [False] * BLOCKS
 
@@ -293,15 +284,8 @@ def tile_kanadjunction_pa_t_kernel(tc, source, target, k_right, WF_right, out):
                 back_transpose(n)
             b = n - 1
             if 0 <= b < BLOCKS:
-                if b // 4 < VECTOR_QUADS:
-                    back_copy(b)
-                    if b % 4 == 3:
-                        back_regroup(b // 4)
-                else:
-                    back_copy_regrouped(b)
-            if n in quantise_at and quantise_at.index(n) < VECTOR_QUADS:
-                quantise_quad(quantise_at.index(n))
-            if 0 <= n - 2 < BLOCKS and (n - 2) // 4 >= VECTOR_QUADS:
+                back_copy(b)
+            if 0 <= n - 2 < BLOCKS:
                 quantise_block(n - 2)
             if n - 1 in products_at:
                 quad_finish(products_at.index(n - 1))

@@ -62,12 +62,11 @@ def tile_kanadjunction_pa_t_kernel(tc, source, target, k_right, WF_right, out):
         row_sum = keep.tile([P, BLOCKS], F32, name="row_sum")
         inv_sum = keep.tile([P, BLOCKS], F32, name="inv_sum")
         squares = [keep.tile([P, 1024], F32, name="squares%d" % i) for i in range(2)]
-        half_sums = keep.tile([P, 512], F32, name="half_sums")
         tgt_rows = [keep.tile([P, 1024], BF16, name="tgt_rows%d" % i) for i in range(4)]
         tgtT = [keep.tile([P, 1024], BF16, name="tgtT%d" % i) for i in range(3)]
         dist = [keep.tile([P, KEYS], F32, name="dist%d" % i, align_bytes=64) for i in range(DIST_SLOTS - SRC_SLOTS)]
         e = [keep.tile([P, KEYS], BF16, name="e%d" % i) for i in range(E_SLOTS)]
-        grouped = [keep.tile([P, KEYS], BF16, name="grouped%d" % i, align_bytes=64) for i in range(2)]
+        grouped = [keep.tile([P, 2 * KEYS], BF16, name="grouped%d" % i, align_bytes=64) for i in range(2)]
         codes = [keep.tile([P, 1024], U32, name="codes%d" % i, align_bytes=64) for i in range(2)]
         scales = [keep.tile([P, 1024], U8, name="scales%d" % i, align_bytes=64) for i in range(2)]
         out_sb = [keep.tile([P, 512], F32, name="out_sb%d" % i) for i in range(2)]
@@ -92,12 +91,10 @@ def tile_kanadjunction_pa_t_kernel(tc, source, target, k_right, WF_right, out):
             rows = tgt_rows[o % 4]
             nc.gpsimd.tensor_tensor(out=squares[o % 2][:, lo:hi], in0=rows[:, lo:hi], in1=rows[:, lo:hi], op=ALU.mult)
 
-        def octet_halve(o):
-            v = squares[o % 2][:].rearrange("p (i h e) -> p i h e", i=8, h=2)
-            nc.gpsimd.tensor_tensor(out=half_sums[:].rearrange("p (i e) -> p i e", i=8), in0=v[:, :, 0, :], in1=v[:, :, 1, :], op=ALU.add)
-
-        def octet_reduce(o):
-            nc.vector.tensor_reduce(out=tgt_sq[:, 8 * o:8 * o + 8], in_=half_sums[:].rearrange("p (i e) -> p i e", i=8), axis=AX.X, op=ALU.add)
+        def octet_fold(o, width):
+            v = squares[o % 2][:].rearrange("p (i e) -> p i e", i=8)
+            dst = v[:, :, 0:width] if width > 1 else tgt_sq[:, 8 * o:8 * o + 8].unsqueeze(2)
+            nc.gpsimd.tensor_tensor(out=dst, in0=v[:, :, 0:width], in1=v[:, :, width:2 * width], op=ALU.add)
 
         def front_tensor(a):
             o, i = divmod(a, 8)
@@ -133,11 +130,11 @@ def tile_kanadjunction_pa_t_kernel(tc, source, target, k_right, WF_right, out):
             bank["t", b] = words_transpose("T%d" % (b % 2), e[b % E_SLOTS], 2)
 
         def back_copy(b):
-            words_copy(bank["t", b], grouped[b % 2][:], 2)
+            words_copy(bank["t", b], grouped[b // 2 % 2][:, (b % 2) * KEYS:(b % 2 + 1) * KEYS], 2)
 
-        def quantise_block(b):
-            q, i = divmod(b, 4)
-            nc.vector.quantize_mx(out=codes[q % 2][:, i * 256:(i + 1) * 256].bitcast(FP8X4), scales=scales[q % 2][:, i * 256:(i + 1) * 256], in_=grouped[b % 2][:])
+        def quantise_pair(b):
+            q, i = divmod(b - 1, 4)
+            nc.vector.quantize_mx(out=codes[q % 2][:, i * 256:(i + 2) * 256].bitcast(FP8X4), scales=scales[q % 2][:, i * 256:(i + 2) * 256], in_=grouped[b // 2 % 2][:])
 
         def quad_products(q):
             ob = psum.tile([P, 512], F32, name="ob", tag="O")
@@ -261,13 +258,12 @@ def tile_kanadjunction_pa_t_kernel(tc, source, target, k_right, WF_right, out):
                 octet_square(o + 1, (r + 4) * P, (r + 5) * P)
             if r == 2 and o + 2 < OCTETS:
                 octet_transpose(o + 2)
-            if r == 4 and o + 1 < OCTETS:
-                octet_halve(o + 1)
+            if 4 <= r <= 6 and o + 1 < OCTETS:
+                for width in [[64], [32, 16], [8, 4, 2, 1]][r - 4]:
+                    octet_fold(o + 1, width)
             if a + 1 < BLOCKS:
                 front_tensor(a + 1)
             front_vector(a)
-            if r == 6 and o + 1 < OCTETS:
-                octet_reduce(o + 1)
             if o == 0 and r == 0:
                 octet_copy(nc.vector.tensor_copy, 1)
             if r == 5 and o + 2 < OCTETS:
@@ -285,8 +281,8 @@ def tile_kanadjunction_pa_t_kernel(tc, source, target, k_right, WF_right, out):
             b = n - 1
             if 0 <= b < BLOCKS:
                 back_copy(b)
-            if 0 <= n - 2 < BLOCKS:
-                quantise_block(n - 2)
+            if 0 <= n - 2 < BLOCKS and n % 2 == 1:
+                quantise_pair(n - 2)
             if n - 1 in products_at:
                 quad_finish(products_at.index(n - 1))
             written["back"] = n + 1

@@ -66,7 +66,7 @@ def tile_kanadjunction_pa_t_kernel(tc, source, target, k_right, WF_right, out):
         tgtT = [keep.tile([P, 1024], BF16, name="tgtT%d" % i) for i in range(3)]
         dist = [keep.tile([P, KEYS], F32, name="dist%d" % i, align_bytes=64) for i in range(DIST_SLOTS - SRC_SLOTS)]
         e = [keep.tile([P, KEYS], BF16, name="e%d" % i) for i in range(E_SLOTS)]
-        grouped = [keep.tile([P, 2 * KEYS], BF16, name="grouped%d" % i, align_bytes=64) for i in range(2)]
+        grouped = [keep.tile([P, 4 * KEYS], BF16, name="grouped%d" % i, align_bytes=64) for i in range(2)]
         codes = [keep.tile([P, 1024], U32, name="codes%d" % i, align_bytes=64) for i in range(2)]
         scales = [keep.tile([P, 1024], U8, name="scales%d" % i, align_bytes=64) for i in range(2)]
         out_sb = [keep.tile([P, 512], F32, name="out_sb%d" % i) for i in range(2)]
@@ -130,11 +130,10 @@ def tile_kanadjunction_pa_t_kernel(tc, source, target, k_right, WF_right, out):
             bank["t", b] = words_transpose("T%d" % (b % 2), e[b % E_SLOTS], 2)
 
         def back_copy(b):
-            words_copy(bank["t", b], grouped[b // 2 % 2][:, (b % 2) * KEYS:(b % 2 + 1) * KEYS], 2)
+            words_copy(bank["t", b], grouped[b // 4 % 2][:, (b % 4) * KEYS:(b % 4 + 1) * KEYS], 2)
 
-        def quantise_pair(b):
-            q, i = divmod(b - 1, 4)
-            nc.vector.quantize_mx(out=codes[q % 2][:, i * 256:(i + 2) * 256].bitcast(FP8X4), scales=scales[q % 2][:, i * 256:(i + 2) * 256], in_=grouped[b // 2 % 2][:])
+        def quantise_quad(q):
+            nc.vector.quantize_mx(out=codes[q % 2][:].bitcast(FP8X4), scales=scales[q % 2][:], in_=grouped[q % 2][:])
 
         def quad_products(q):
             ob = psum.tile([P, 512], F32, name="ob", tag="O")
@@ -145,8 +144,10 @@ def tile_kanadjunction_pa_t_kernel(tc, source, target, k_right, WF_right, out):
                                         rhs=f_codes[:, g * P:(g + 1) * P].bitcast(FP8X4), rhs_scale=f_scales[:, g * P:(g + 1) * P], start=(g == 0), stop=(g == 1))
             bank["o", q] = ob
 
-        def quad_finish(q):
+        def quad_reciprocal(q):
             nc.vector.reciprocal(out=inv_sum[:, 4 * q:4 * q + 4], in_=row_sum[:, 4 * q:4 * q + 4])
+
+        def quad_finish(q):
             nc.vector.tensor_tensor(out=out_sb[q % 2][:].rearrange("p (i d) -> p i d", i=4), in0=bank["o", q][:].rearrange("p (i d) -> p i d", i=4),
                                     in1=inv_sum[:, 4 * q:4 * q + 4].unsqueeze(2).to_broadcast([P, 4, P]), op=ALU.mult)
             o, h = divmod(q, 2)
@@ -238,6 +239,7 @@ def tile_kanadjunction_pa_t_kernel(tc, source, target, k_right, WF_right, out):
             group_of_last[last - 1] = (first, last)
             first = last
         assert first == BLOCKS
+        quantise_at = [4 * q + 5 for q in range(QUADS)]
         products_at = [4 * q + 6 for q in range(QUADS)]
         written = {"front": 0, "back": 0, "scalar": 0}
         exp_written = [False] * BLOCKS
@@ -274,15 +276,17 @@ def tile_kanadjunction_pa_t_kernel(tc, source, target, k_right, WF_right, out):
 
         def back_unit(n):
             assert n >= BLOCKS or exp_written[n]
-            if n in products_at:
-                quad_products(products_at.index(n))
             if n < BLOCKS:
                 back_transpose(n)
+            if n in products_at:
+                quad_products(products_at.index(n))
+            if n in quantise_at:
+                quad_reciprocal(quantise_at.index(n))
             b = n - 1
             if 0 <= b < BLOCKS:
                 back_copy(b)
-            if 0 <= n - 2 < BLOCKS and n % 2 == 1:
-                quantise_pair(n - 2)
+            if n in quantise_at:
+                quantise_quad(quantise_at.index(n))
             if n - 1 in products_at:
                 quad_finish(products_at.index(n - 1))
             written["back"] = n + 1

@@ -21,11 +21,12 @@ OCTETS = BLOCKS // 8
 QUADS = BLOCKS // 4
 INV_ROOT = 128.0 ** -0.5
 
-GROUPS = [8, 24, 24, 24, 24, 24]
-DIST_SLOTS = 28
-E_SLOTS = 16
-AHEAD = 29
-SRC_SLOTS = 5
+GROUPS = [8, 24, 32, 32, 32]
+DIST_SLOTS = 35
+E_SLOTS = 18
+LEAD = 4
+KEEP = 2
+SRC_SLOTS = 7
 
 
 def tile_kanadjunction_pa_t_kernel(tc, source, target, k_right, WF_right, out):
@@ -37,19 +38,22 @@ def tile_kanadjunction_pa_t_kernel(tc, source, target, k_right, WF_right, out):
 
         ident_f = keep.tile([P, P], F32, name="ident_f")
         ident_b = keep.tile([P, P], BF16, name="ident_b")
-        key_rows = keep.tile([P, KEYS], BF16, name="key_rows")
         keysT = keep.tile([P, KEYS], BF16, name="keysT")
         key_sq = keep.tile([P, 8], F32, name="key_sq")
         neg_key_sq = keep.tile([P, 8, P], F32, name="neg_key_sq")
-        src_rows = [keep.tile([P, 2048], BF16, name="src_rows%d" % g, tag="dist%d" % (DIST_SLOTS - 1 - g), align_bytes=64) for g in range(2)]
-        src_grouped = [keep.tile([P, 2048], BF16, name="src_grouped%d" % g, tag="dist%d" % (DIST_SLOTS - 3 - g), align_bytes=64) for g in range(2)]
-        src_codes = keep.tile([P, 1024], U32, name="src_codes", tag="dist%d" % (DIST_SLOTS - 5), align_bytes=64)
+
+        def early_tile(j, dtype, name):
+            return keep.tile([P, 4096 // (2 if dtype == BF16 else 4)], dtype, name=name, tag="dist%d" % (DIST_SLOTS - 1 - j), align_bytes=64)
+
+        src_rows = [early_tile(g, BF16, "src_rows%d" % g) for g in range(2)]
+        src_grouped = [early_tile(2 + g, BF16, "src_grouped%d" % g) for g in range(2)]
+        src_codes = early_tile(4, U32, "src_codes")
+        wf_tile = early_tile(5, BF16, "wf_tile")
+        wf_rows, wf_grouped, f_grouped = wf_tile[:, 0:512], wf_tile[:, 512:1024], wf_tile[:, 1024:2048]
+        key_rows = early_tile(6, BF16, "key_rows")
         src_scales = keep.tile([P, 1024], U8, name="src_scales", align_bytes=64)
-        wf_rows = keep.tile([P, 512], BF16, name="wf_rows")
-        wf_grouped = keep.tile([P, 512], BF16, name="wf_grouped", align_bytes=64)
         wf_codes = keep.tile([P, P], U32, name="wf_codes", align_bytes=64)
         wf_scales = keep.tile([P, P], U8, name="wf_scales", align_bytes=64)
-        f_grouped = keep.tile([P, 1024], BF16, name="f_grouped", align_bytes=64)
         f_codes = keep.tile([P, 256], U32, name="f_codes", align_bytes=64)
         f_scales = keep.tile([P, 256], U8, name="f_scales", align_bytes=64)
         scratch = keep.tile([P, P], F32, name="scratch")
@@ -61,8 +65,8 @@ def tile_kanadjunction_pa_t_kernel(tc, source, target, k_right, WF_right, out):
         exp_bias = keep.tile([P, BLOCKS], F32, name="exp_bias")
         row_sum = keep.tile([P, BLOCKS], F32, name="row_sum")
         inv_sum = keep.tile([P, BLOCKS], F32, name="inv_sum")
-        squares = [keep.tile([P, 1024], F32, name="squares%d" % i) for i in range(2)]
-        tgt_rows = [keep.tile([P, 1024], BF16, name="tgt_rows%d" % i) for i in range(4)]
+        squares = keep.tile([P, 1024], F32, name="squares")
+        tgt_rows = [keep.tile([P, 1024], BF16, name="tgt_rows%d" % i) for i in range(3)]
         tgtT = [keep.tile([P, 1024], BF16, name="tgtT%d" % i) for i in range(3)]
         dist = [keep.tile([P, KEYS], F32, name="dist%d" % i, align_bytes=64) for i in range(DIST_SLOTS - SRC_SLOTS)]
         e = [keep.tile([P, KEYS], BF16, name="e%d" % i) for i in range(E_SLOTS)]
@@ -79,20 +83,20 @@ def tile_kanadjunction_pa_t_kernel(tc, source, target, k_right, WF_right, out):
             return pb
 
         def load_octet(o):
-            nc.sync.dma_start(out=tgt_rows[o % 4][:], in_=target[o * 1024:(o + 1) * 1024, :].rearrange("(p i) e -> p (i e)", i=8))
+            nc.sync.dma_start(out=tgt_rows[o % 3][:], in_=target[o * 1024:(o + 1) * 1024, :].rearrange("(p i) e -> p (i e)", i=8))
 
         def octet_transpose(o):
-            bank["x", o] = transpose8("X", tgt_rows[o % 4])
+            bank["x", o] = transpose8("X", tgt_rows[o % 3])
 
         def octet_copy(engine_copy, o):
             engine_copy(out=tgtT[o % 3][:], in_=bank["x", o][:])
 
         def octet_square(o, lo, hi):
-            rows = tgt_rows[o % 4]
-            nc.gpsimd.tensor_tensor(out=squares[o % 2][:, lo:hi], in0=rows[:, lo:hi], in1=rows[:, lo:hi], op=ALU.mult)
+            rows = tgt_rows[o % 3]
+            nc.gpsimd.tensor_tensor(out=squares[:, lo:hi], in0=rows[:, lo:hi], in1=rows[:, lo:hi], op=ALU.mult)
 
         def octet_fold(o, width):
-            v = squares[o % 2][:].rearrange("p (i e) -> p i e", i=8)
+            v = squares[:].rearrange("p (i e) -> p i e", i=8)
             dst = v[:, :, 0:width] if width > 1 else tgt_sq[:, 8 * o:8 * o + 8].unsqueeze(2)
             nc.gpsimd.tensor_tensor(out=dst, in0=v[:, :, 0:width], in1=v[:, :, width:2 * width], op=ALU.add)
 
@@ -130,7 +134,7 @@ def tile_kanadjunction_pa_t_kernel(tc, source, target, k_right, WF_right, out):
             bank["t", b] = words_transpose("T%d" % (b % 2), e[b % E_SLOTS], 2)
 
         def back_copy(b):
-            words_copy(bank["t", b], grouped[b // 4 % 2][:, (b % 4) * KEYS:(b % 4 + 1) * KEYS], 2)
+            words_copy(nc.vector.tensor_copy, bank["t", b], grouped[b // 4 % 2][:, (b % 4) * KEYS:(b % 4 + 1) * KEYS], 2)
 
         def quantise_quad(q):
             nc.vector.quantize_mx(out=codes[q % 2][:].bitcast(FP8X4), scales=scales[q % 2][:], in_=grouped[q % 2][:])
@@ -160,51 +164,50 @@ def tile_kanadjunction_pa_t_kernel(tc, source, target, k_right, WF_right, out):
                     nc.tensor.transpose(pw[:, (2 * c + u) * P:(2 * c + u + 1) * P], rows[:, c * 512:(c + 1) * 512].bitcast(F32)[:, u * P:(u + 1) * P], ident_f[:])
             return pw
 
-        def words_copy(pw, dst, chunks):
-            nc.vector.tensor_copy(out=dst.bitcast(F32).rearrange("w (c n u) -> w c n u", c=chunks, u=2), in_=pw[:].rearrange("w (c u n) -> w c n u", c=chunks, u=2))
+        def words_copy(copy, pw, dst, chunks):
+            copy(out=dst.bitcast(F32).rearrange("w (c n u) -> w c n u", c=chunks, u=2), in_=pw[:].rearrange("w (c u n) -> w c n u", c=chunks, u=2))
+
+        def wf_transpose():
+            bank["wf"] = words_transpose("T0", wf_rows, 1)
 
         def src_transpose(j):
             bank["s", j] = words_transpose(["O", "T1"][j % 2], src_rows[j // 2][:, (j % 2) * 1024:(j % 2 + 1) * 1024], 2)
 
-        def src_copy(j):
-            words_copy(bank["s", j], src_grouped[j // 2][:, (j % 2) * 1024:(j % 2 + 1) * 1024], 2)
+        def wf_copy():
+            words_copy(nc.scalar.copy, bank["wf"], wf_grouped, 1)
 
-        def prepare_f():
-            wf_bank = words_transpose("T0", wf_rows[:], 1)
-            src_transpose(0)
-            words_copy(wf_bank, wf_grouped[:], 1)
-            src_transpose(1)
-            src_copy(0)
-            src_transpose(2)
-            src_copy(1)
-            src_transpose(3)
-            src_copy(2)
-            nc.vector.quantize_mx(out=wf_codes[:].bitcast(FP8X4), scales=wf_scales[:], in_=wf_grouped[:])
-            src_copy(3)
-            for g in range(2):
-                nc.vector.quantize_mx(out=src_codes[:, g * 512:(g + 1) * 512].bitcast(FP8X4), scales=src_scales[:, g * 512:(g + 1) * 512], in_=src_grouped[g][:])
-            f_banks = []
-            for g in range(2):
-                fb = psum.tile([P, 512], F32, name="fb", tag=["O", "T1"][g])
-                for t in range(4):
-                    c = 4 * g + t
-                    nc.tensor.matmul_mx(out=fb[:, t * P:(t + 1) * P], lhsT=src_codes[:, c * P:(c + 1) * P].bitcast(FP8X4), lhsT_scale=src_scales[:, c * P:(c + 1) * P],
-                                        rhs=wf_codes[:].bitcast(FP8X4), rhs_scale=wf_scales[:], start=True, stop=True)
-                f_banks.append(fb)
-            for g in range(2):
-                nc.vector.tensor_copy(out=f_grouped[:, g * 512:(g + 1) * 512].rearrange("p (d t) -> p d t", t=4), in_=f_banks[g][:].rearrange("p (t d) -> p d t", t=4))
-            nc.vector.quantize_mx(out=f_codes[:].bitcast(FP8X4), scales=f_scales[:], in_=f_grouped[:])
+        def src_copy(j):
+            words_copy(nc.scalar.copy, bank["s", j], src_grouped[j // 2][:, (j % 2) * 1024:(j % 2 + 1) * 1024], 2)
+
+        def wf_quantise():
+            nc.vector.quantize_mx(out=wf_codes[:].bitcast(FP8X4), scales=wf_scales[:], in_=wf_grouped)
+
+        def src_quantise(g):
+            nc.vector.quantize_mx(out=src_codes[:, g * 512:(g + 1) * 512].bitcast(FP8X4), scales=src_scales[:, g * 512:(g + 1) * 512], in_=src_grouped[g][:])
+
+        def f_products(g):
+            fb = psum.tile([P, 512], F32, name="fb", tag=["O", "T1"][g])
+            for t in range(4):
+                c = 4 * g + t
+                nc.tensor.matmul_mx(out=fb[:, t * P:(t + 1) * P], lhsT=src_codes[:, c * P:(c + 1) * P].bitcast(FP8X4), lhsT_scale=src_scales[:, c * P:(c + 1) * P],
+                                    rhs=wf_codes[:].bitcast(FP8X4), rhs_scale=wf_scales[:], start=True, stop=True)
+            bank["f", g] = fb
+
+        def f_copy(g):
+            nc.vector.tensor_copy(out=f_grouped[:, g * 512:(g + 1) * 512].rearrange("p (d t) -> p d t", t=4), in_=bank["f", g][:].rearrange("p (t d) -> p d t", t=4))
+
+        def f_quantise():
+            nc.vector.quantize_mx(out=f_codes[:].bitcast(FP8X4), scales=f_scales[:], in_=f_grouped)
 
         for u in range(2):
             for v in range(2):
                 nc.sync.dma_start(out=key_rows[v:P:2, u * 512:(u + 1) * 512].rearrange("p (s e) -> p s e", s=4), in_=k_right.rearrange("(s p w) e -> w p s e", s=4, w=4)[2 * u + v])
         load_octet(0)
-        nc.sync.dma_start(out=wf_rows[:], in_=WF_right)
+        nc.sync.dma_start(out=wf_rows, in_=WF_right)
         for g in range(2):
             nc.sync.dma_start(out=src_rows[g][:], in_=source[g * 512:(g + 1) * 512, :].rearrange("(p t) c -> p (t c)", t=4))
         load_octet(1)
         load_octet(2)
-        load_octet(3)
         make_identity(nc, ident_b[:])
         make_identity(nc, ident_f[:])
         nc.vector.memset(scratch[:, 0:1], 1.0)
@@ -225,44 +228,46 @@ def tile_kanadjunction_pa_t_kernel(tc, source, target, k_right, WF_right, out):
         nc.vector.tensor_scalar(out=neg_key_sq[:], in0=key_sq[:].unsqueeze(2).to_broadcast([P, 8, P]), scalar1=-1.0, scalar2=None, op0=ALU.mult)
         front_tensor(0)
 
-        scalar_order = []
-        group_of_last = {}
-        first = 0
-        for size in GROUPS:
-            last = first + size
-            pair = 1 if first == 0 else 2
-            assert size % pair == 0
-            blocks = []
-            for c0 in range(first, last, pair):
-                blocks += list(reversed(range(c0, c0 + pair)))
-            scalar_order += [("sqrt", a) for a in blocks] + [("bias", (first, last))] + [("exp", a) for a in blocks]
-            group_of_last[last - 1] = (first, last)
-            first = last
-        assert first == BLOCKS
         quantise_at = [4 * q + 5 for q in range(QUADS)]
         products_at = [4 * q + 6 for q in range(QUADS)]
-        written = {"front": 0, "back": 0, "scalar": 0}
-        exp_written = [False] * BLOCKS
+        back_units = products_at[QUADS - 1] + 2
+        written = {"front": 0, "back": 0, "exp": 0}
+        group_ends = {}
+        first = 0
+        for size in GROUPS:
+            group_ends[first + size - 1] = (first, first + size)
+            first += size
+        assert first == BLOCKS
+
+        before = {1: [wf_transpose], 2: [lambda: src_transpose(0)], 3: [lambda: src_transpose(1)], 4: [lambda: src_transpose(2)], 5: [lambda: src_transpose(3)],
+                  7: [wf_quantise, lambda: src_quantise(0)], 8: [lambda: src_quantise(1), lambda: f_products(0)], 9: [lambda: f_products(1), lambda: f_copy(0)],
+                  10: [lambda: f_copy(1)], 11: [f_quantise]}
+        after_sqrt = {2: [wf_copy], 3: [lambda: src_copy(0)], 4: [lambda: src_copy(1)], 5: [lambda: src_copy(2)], 6: [lambda: src_copy(3)]}
 
         def front_unit(a):
-            assert a < DIST_SLOTS or exp_written[a - DIST_SLOTS]
+            assert a - DIST_SLOTS < written["exp"]
+            for step in before.get(a, []):
+                step()
+            if a == DIST_SLOTS - SRC_SLOTS:
+                dist.extend([keep.tile([P, KEYS], F32, name="dist%d" % i, align_bytes=64) for i in range(len(dist), DIST_SLOTS)])
             o, r = divmod(a, 8)
             if o == 0:
                 if r == 0:
                     octet_transpose(1)
-                if 1 <= r <= 4:
-                    octet_square(1, (r - 1) * 256, r * 256)
-            if r == 4 and o + 4 < OCTETS:
-                load_octet(o + 4)
+                if r < 4:
+                    octet_square(1, r * 256, (r + 1) * 256)
+                if r == 3:
+                    for width in [64, 32, 16, 8, 4, 2, 1]:
+                        octet_fold(1, width)
+            elif r < 3 and o + 1 < OCTETS:
+                for width in [[64], [32, 16], [8, 4, 2, 1]][r]:
+                    octet_fold(o + 1, width)
             if r >= 4 and o + 2 < OCTETS:
-                octet_square(o + 2, (r - 4) * P, (r - 3) * P)
-            if r < 4 and 2 <= o + 1 < OCTETS:
-                octet_square(o + 1, (r + 4) * P, (r + 5) * P)
+                octet_square(o + 2, (r - 4) * 256, (r - 3) * 256)
+            if r == 4 and o + 3 < OCTETS:
+                load_octet(o + 3)
             if r == 2 and o + 2 < OCTETS:
                 octet_transpose(o + 2)
-            if 4 <= r <= 6 and o + 1 < OCTETS:
-                for width in [[64], [32, 16], [8, 4, 2, 1]][r - 4]:
-                    octet_fold(o + 1, width)
             if a + 1 < BLOCKS:
                 front_tensor(a + 1)
             front_vector(a)
@@ -270,53 +275,52 @@ def tile_kanadjunction_pa_t_kernel(tc, source, target, k_right, WF_right, out):
                 octet_copy(nc.vector.tensor_copy, 1)
             if r == 5 and o + 2 < OCTETS:
                 octet_copy(nc.scalar.copy, o + 2)
-            if a in group_of_last:
-                group_min_d2(*group_of_last[a])
+            if a in group_ends:
+                group_min_d2(*group_ends[a])
             written["front"] = a + 1
 
         def back_unit(n):
-            assert n >= BLOCKS or exp_written[n]
+            assert n >= BLOCKS or n < written["exp"]
             if n < BLOCKS:
                 back_transpose(n)
             if n in products_at:
                 quad_products(products_at.index(n))
             if n in quantise_at:
                 quad_reciprocal(quantise_at.index(n))
-            b = n - 1
-            if 0 <= b < BLOCKS:
-                back_copy(b)
+            if 0 <= n - 1 < BLOCKS:
+                back_copy(n - 1)
             if n in quantise_at:
                 quantise_quad(quantise_at.index(n))
             if n - 1 in products_at:
                 quad_finish(products_at.index(n - 1))
             written["back"] = n + 1
 
-        def scalar_unit():
-            while written["scalar"] < len(scalar_order):
-                kind, x = scalar_order[written["scalar"]]
-                written["scalar"] += 1
-                if kind == "sqrt":
-                    assert x < written["front"]
-                    scalar_sqrt(x)
-                    return
-                if kind == "exp":
-                    assert x - E_SLOTS < written["back"]
-                    scalar_exp(x)
-                    exp_written[x] = True
-                    return
-                scalar_group_bias(*x)
+        def units_up_to(front, back):
+            front, back = min(front, BLOCKS), min(back, written["exp"])
+            while written["front"] < front or written["back"] < back:
+                if written["back"] < back:
+                    back_unit(written["back"])
+                if written["front"] < front:
+                    front_unit(written["front"])
 
-        for a in range(AHEAD):
-            if a == DIST_SLOTS - SRC_SLOTS:
-                prepare_f()
-                dist += [keep.tile([P, KEYS], F32, name="dist%d" % i, align_bytes=64) for i in range(len(dist), DIST_SLOTS)]
-            front_unit(a)
-            scalar_unit()
-        for n in range(products_at[QUADS - 1] + 2):
-            while n < BLOCKS and not exp_written[n]:
-                scalar_unit()
+        first = 0
+        for k, size in enumerate(GROUPS):
+            last = first + size
+            lead = size // LEAD if k > 0 else 0
+            kept = GROUPS[k - 1] // KEEP if k > 0 else 0
+            next_lead = GROUPS[k + 1] // LEAD if k + 1 < len(GROUPS) else 0
+            next_kept = size // KEEP if k + 1 < len(GROUPS) else 0
+            for i in range(size):
+                units_up_to(first + lead + ((size - lead) * (i + 1) + size - 1) // size + 1, first - kept + kept * (i + 1) // size)
+                scalar_sqrt(first + i)
+                for step in after_sqrt.get(first + i, []):
+                    step()
+            scalar_group_bias(first, last)
+            for i in range(size):
+                assert first + i - E_SLOTS < written["back"]
+                scalar_exp(first + i)
+                written["exp"] = first + i + 1
+                units_up_to(last + next_lead * (i + 1) // size + 1, first + (size - next_kept) * (i + 1) // size)
+            first = last
+        for n in range(written["back"], back_units):
             back_unit(n)
-            scalar_unit()
-            if n + AHEAD < BLOCKS:
-                front_unit(n + AHEAD)
-                scalar_unit()

@@ -274,7 +274,7 @@ def tile_kanadjunction_pa_t_kernel(tc, source, target, k_right, WF_right, out):
             if o == 0 and r == 0:
                 octet_copy(nc.vector.tensor_copy, 1)
             if r == 5 and o + 2 < OCTETS:
-                octet_copy(nc.scalar.copy, o + 2)
+                octet_copy(nc.vector.tensor_copy, o + 2)
             if a in group_ends:
                 group_min_d2(*group_ends[a])
             written["front"] = a + 1

@@ -24,7 +24,7 @@ INV_ROOT = 128.0 ** -0.5
 GROUPS = [8, 24, 32, 32, 32]
 DIST_SLOTS = 35
 E_SLOTS = 18
-LEAD = 4
+LEAD = 2
 KEEP = 2
 SRC_SLOTS = 7
 
@@ -112,7 +112,7 @@ def tile_kanadjunction_pa_t_kernel(tc, source, target, k_right, WF_right, out):
                 nc.tensor.matmul(bank["y", a, g][:], lhsT=tgtT[o % 3][:, i * P:(i + 1) * P], rhs=keysT[:, g * 512:(g + 1) * 512], start=False, stop=True)
 
         def front_vector(a):
-            for g in (1, 0):
+            for g in range(2):
                 nc.vector.tensor_scalar(out=dist[a % DIST_SLOTS][:, g * 512:(g + 1) * 512], in0=bank["y", a, g][:], scalar1=tgt_sq[:, a:a + 1], scalar2=None,
                                         op0=ALU.min, op1=ALU.max, accum_out=bank_max[:, 2 * a + g:2 * a + g + 1])
 

@@ -19,6 +19,7 @@ KEYS = 1024
 BLOCKS = 128
 OCTETS = BLOCKS // 8
 QUADS = BLOCKS // 4
+LAST_QUAD = QUADS - 1
 INV_ROOT = 128.0 ** -0.5
 
 GROUPS = [8, 24, 32, 32, 32]
@@ -26,6 +27,7 @@ DIST_SLOTS = 35
 E_SLOTS = 18
 LEAD = 2
 KEEP = 2
+RING = 5
 SRC_SLOTS = 7
 
 
@@ -75,9 +77,14 @@ def tile_kanadjunction_pa_t_kernel(tc, source, target, k_right, WF_right, out):
         scales = [keep.tile([P, 1024], U8, name="scales%d" % i, align_bytes=64) for i in range(2)]
         out_sb = [keep.tile([P, 512], F32, name="out_sb%d" % i) for i in range(2)]
         bank = {}
+        turns = []
 
-        def transpose8(tag, rows):
-            pb = psum.tile([P, 1024], BF16, name="pb_" + tag, tag=tag)
+        def next_bank():
+            turns.append(len(turns) % RING)
+            return "R%d" % turns[-1]
+
+        def transpose8(rows):
+            pb = psum.tile([P, 1024], BF16, name="pb", tag=next_bank())
             for i in range(8):
                 nc.tensor.transpose(pb[:, i * P:(i + 1) * P], rows[:, i * P:(i + 1) * P], ident_b[:])
             return pb
@@ -86,7 +93,7 @@ def tile_kanadjunction_pa_t_kernel(tc, source, target, k_right, WF_right, out):
             nc.sync.dma_start(out=tgt_rows[o % 3][:], in_=target[o * 1024:(o + 1) * 1024, :].rearrange("(p i) e -> p (i e)", i=8))
 
         def octet_transpose(o):
-            bank["x", o] = transpose8("X", tgt_rows[o % 3])
+            bank["x", o] = transpose8(tgt_rows[o % 3])
 
         def octet_copy(engine_copy, o):
             engine_copy(out=tgtT[o % 3][:], in_=bank["x", o][:])
@@ -103,10 +110,9 @@ def tile_kanadjunction_pa_t_kernel(tc, source, target, k_right, WF_right, out):
         def front_tensor(a):
             o, i = divmod(a, 8)
             for g in range(2):
-                yb = psum.tile([P, 512], F32, name="yb", tag="Y%d" % (2 * (a % 2) + g))
+                yb = psum.tile([P, 512], F32, name="yb", tag=next_bank())
                 for t in range(4):
-                    u, h = divmod(t, 2)
-                    nc.tensor.matmul(yb[:, t * P:(t + 1) * P], lhsT=neg_key_sq[:, 4 * u + 2 * g + h, :], rhs=ident_f[:], is_transpose=True, start=(t == 0), stop=False)
+                    nc.tensor.matmul(yb[:, t * P:(t + 1) * P], lhsT=neg_key_sq[:, 4 * g + t, :], rhs=ident_f[:], is_transpose=True, start=(t == 0), stop=False)
                 bank["y", a, g] = yb
             for g in range(2):
                 nc.tensor.matmul(bank["y", a, g][:], lhsT=tgtT[o % 3][:, i * P:(i + 1) * P], rhs=keysT[:, g * 512:(g + 1) * 512], start=False, stop=True)
@@ -136,17 +142,19 @@ def tile_kanadjunction_pa_t_kernel(tc, source, target, k_right, WF_right, out):
         def back_copy(b):
             words_copy(nc.vector.tensor_copy, bank["t", b], grouped[b // 4 % 2][:, (b % 4) * KEYS:(b % 4 + 1) * KEYS], 2)
 
-        def quantise_quad(q):
-            nc.vector.quantize_mx(out=codes[q % 2][:].bitcast(FP8X4), scales=scales[q % 2][:], in_=grouped[q % 2][:])
+        def quantise(q, i0=0, i1=4):
+            nc.vector.quantize_mx(out=codes[q % 2][:, i0 * 256:i1 * 256].bitcast(FP8X4), scales=scales[q % 2][:, i0 * 256:i1 * 256],
+                                  in_=grouped[q % 2][:, i0 * KEYS:i1 * KEYS])
 
-        def quad_products(q):
-            ob = psum.tile([P, 512], F32, name="ob", tag="O")
-            for i in range(4):
+        def products(q, i0=0, i1=4):
+            if i0 == 0:
+                bank["o", q] = psum.tile([P, 512], F32, name="ob", tag="O" if q < LAST_QUAD else next_bank())
+            ob = bank["o", q]
+            for i in range(i0, i1):
                 for g in range(2):
                     c0 = i * 256 + g * P
                     nc.tensor.matmul_mx(out=ob[:, i * P:(i + 1) * P], lhsT=codes[q % 2][:, c0:c0 + P].bitcast(FP8X4), lhsT_scale=scales[q % 2][:, c0:c0 + P],
                                         rhs=f_codes[:, g * P:(g + 1) * P].bitcast(FP8X4), rhs_scale=f_scales[:, g * P:(g + 1) * P], start=(g == 0), stop=(g == 1))
-            bank["o", q] = ob
 
         def quad_reciprocal(q):
             nc.vector.reciprocal(out=inv_sum[:, 4 * q:4 * q + 4], in_=row_sum[:, 4 * q:4 * q + 4])
@@ -158,7 +166,7 @@ def tile_kanadjunction_pa_t_kernel(tc, source, target, k_right, WF_right, out):
             nc.sync.dma_start(out=out[o * 1024:(o + 1) * 1024, :].rearrange("(p i) d -> p (i d)", i=8)[:, h * 512:(h + 1) * 512], in_=out_sb[q % 2][:])
 
         def words_transpose(tag, rows, chunks):
-            pw = psum.tile([P, 2 * chunks * P], F32, name="pw_" + tag, tag=tag)
+            pw = psum.tile([P, 2 * chunks * P], F32, name="pw", tag=tag)
             for c in range(chunks):
                 for u in range(2):
                     nc.tensor.transpose(pw[:, (2 * c + u) * P:(2 * c + u + 1) * P], rows[:, c * 512:(c + 1) * 512].bitcast(F32)[:, u * P:(u + 1) * P], ident_f[:])
@@ -168,10 +176,10 @@ def tile_kanadjunction_pa_t_kernel(tc, source, target, k_right, WF_right, out):
             copy(out=dst.bitcast(F32).rearrange("w (c n u) -> w c n u", c=chunks, u=2), in_=pw[:].rearrange("w (c u n) -> w c n u", c=chunks, u=2))
 
         def wf_transpose():
-            bank["wf"] = words_transpose("T0", wf_rows, 1)
+            bank["wf"] = words_transpose(next_bank(), wf_rows, 1)
 
         def src_transpose(j):
-            bank["s", j] = words_transpose(["O", "T1"][j % 2], src_rows[j // 2][:, (j % 2) * 1024:(j % 2 + 1) * 1024], 2)
+            bank["s", j] = words_transpose(next_bank(), src_rows[j // 2][:, (j % 2) * 1024:(j % 2 + 1) * 1024], 2)
 
         def wf_copy():
             words_copy(nc.scalar.copy, bank["wf"], wf_grouped, 1)
@@ -186,7 +194,7 @@ def tile_kanadjunction_pa_t_kernel(tc, source, target, k_right, WF_right, out):
             nc.vector.quantize_mx(out=src_codes[:, g * 512:(g + 1) * 512].bitcast(FP8X4), scales=src_scales[:, g * 512:(g + 1) * 512], in_=src_grouped[g][:])
 
         def f_products(g):
-            fb = psum.tile([P, 512], F32, name="fb", tag=["O", "T1"][g])
+            fb = psum.tile([P, 512], F32, name="fb", tag=next_bank())
             for t in range(4):
                 c = 4 * g + t
                 nc.tensor.matmul_mx(out=fb[:, t * P:(t + 1) * P], lhsT=src_codes[:, c * P:(c + 1) * P].bitcast(FP8X4), lhsT_scale=src_scales[:, c * P:(c + 1) * P],
@@ -194,7 +202,7 @@ def tile_kanadjunction_pa_t_kernel(tc, source, target, k_right, WF_right, out):
             bank["f", g] = fb
 
         def f_copy(g):
-            nc.vector.tensor_copy(out=f_grouped[:, g * 512:(g + 1) * 512].rearrange("p (d t) -> p d t", t=4), in_=bank["f", g][:].rearrange("p (t d) -> p d t", t=4))
+            nc.scalar.copy(out=f_grouped[:, g * 512:(g + 1) * 512].rearrange("p (d t) -> p d t", t=4), in_=bank["f", g][:].rearrange("p (t d) -> p d t", t=4))
 
         def f_quantise():
             nc.vector.quantize_mx(out=f_codes[:].bitcast(FP8X4), scales=f_scales[:], in_=f_grouped)
@@ -212,25 +220,39 @@ def tile_kanadjunction_pa_t_kernel(tc, source, target, k_right, WF_right, out):
         make_identity(nc, ident_f[:])
         nc.vector.memset(scratch[:, 0:1], 1.0)
         nc.scalar.activation(out=scratch[:, 1:2], in_=scratch[:, 0:1], func=ACT.Sqrt)
-        keys_bank = psum.tile([P, 1024], BF16, name="keys_bank", tag="T0")
+        keys_bank = psum.tile([P, 1024], BF16, name="keys_bank", tag=next_bank())
         for g in range(2):
             for u in range(2):
                 for h in range(2):
                     c, s = 4 * g + 2 * u + h, 4 * u + 2 * g + h
                     nc.tensor.transpose(keys_bank[:, c * P:(c + 1) * P], key_rows[:, s * P:(s + 1) * P], ident_b[:])
         octet_transpose(0)
-        for c in range(8):
-            nc.scalar.activation(out=scratch[:], in_=key_rows[:, c * P:(c + 1) * P], func=ACT.Square, accum_out=key_sq[:, c:c + 1])
-        for c in range(8):
+        def key_squares(g):
+            for t in range(4):
+                u, h = divmod(t, 2)
+                s = 4 * u + 2 * g + h
+                nc.scalar.activation(out=scratch[:], in_=key_rows[:, s * P:(s + 1) * P], func=ACT.Square, accum_out=key_sq[:, 4 * g + t:4 * g + t + 1])
+
+        def target_squares(c):
             nc.scalar.activation(out=scratch[:], in_=tgt_rows[0][:, c * P:(c + 1) * P], func=ACT.Square, accum_out=tgt_sq[:, c:c + 1])
+
+        def key_spread(g):
+            nc.vector.tensor_scalar(out=neg_key_sq[:, 4 * g:4 * g + 4, :], in0=key_sq[:, 4 * g:4 * g + 4].unsqueeze(2).to_broadcast([P, 4, P]), scalar1=-1.0, scalar2=None, op0=ALU.mult)
+
+        key_squares(0)
+        target_squares(0)
+        key_squares(1)
+        for c in range(1, 8):
+            target_squares(c)
         nc.vector.tensor_scalar(out=keysT[:], in0=keys_bank[:], scalar1=2.0, scalar2=None, op0=ALU.mult)
+        key_spread(0)
         octet_copy(nc.vector.tensor_copy, 0)
-        nc.vector.tensor_scalar(out=neg_key_sq[:], in0=key_sq[:].unsqueeze(2).to_broadcast([P, 8, P]), scalar1=-1.0, scalar2=None, op0=ALU.mult)
+        key_spread(1)
         front_tensor(0)
 
-        quantise_at = [4 * q + 5 for q in range(QUADS)]
-        products_at = [4 * q + 6 for q in range(QUADS)]
-        back_units = products_at[QUADS - 1] + 2
+        quantise_at = [4 * q + 5 for q in range(QUADS - 1)]
+        products_at = [4 * q + 6 for q in range(QUADS - 1)]
+        back_units = BLOCKS + 2
         written = {"front": 0, "back": 0, "exp": 0}
         group_ends = {}
         first = 0
@@ -240,9 +262,10 @@ def tile_kanadjunction_pa_t_kernel(tc, source, target, k_right, WF_right, out):
         assert first == BLOCKS
 
         before = {1: [wf_transpose], 2: [lambda: src_transpose(0)], 3: [lambda: src_transpose(1)], 4: [lambda: src_transpose(2)], 5: [lambda: src_transpose(3)],
-                  7: [wf_quantise, lambda: src_quantise(0)], 8: [lambda: src_quantise(1), lambda: f_products(0)], 9: [lambda: f_products(1), lambda: f_copy(0)],
-                  10: [lambda: f_copy(1)], 11: [f_quantise]}
-        after_sqrt = {2: [wf_copy], 3: [lambda: src_copy(0)], 4: [lambda: src_copy(1)], 5: [lambda: src_copy(2)], 6: [lambda: src_copy(3)]}
+                  7: [wf_quantise, lambda: src_quantise(0)], 8: [lambda: src_quantise(1), lambda: f_products(0)], 9: [lambda: f_products(1)],
+                  14: [f_quantise]}
+        after_sqrt = {0: [wf_copy], 1: [lambda: src_copy(0)], 2: [lambda: src_copy(1)], 3: [lambda: src_copy(2)], 4: [lambda: src_copy(3)]}
+        after_exp = {0: [lambda: f_copy(0)], 1: [lambda: f_copy(1)]}
 
         def front_unit(a):
             assert a - DIST_SLOTS < written["exp"]
@@ -255,7 +278,8 @@ def tile_kanadjunction_pa_t_kernel(tc, source, target, k_right, WF_right, out):
                 if r == 0:
                     octet_transpose(1)
                 if r < 4:
-                    octet_square(1, r * 256, (r + 1) * 256)
+                    for lo in (r * 256, r * 256 + P):
+                        octet_square(1, lo, lo + P)
                 if r == 3:
                     for width in [64, 32, 16, 8, 4, 2, 1]:
                         octet_fold(1, width)
@@ -263,17 +287,18 @@ def tile_kanadjunction_pa_t_kernel(tc, source, target, k_right, WF_right, out):
                 for width in [[64], [32, 16], [8, 4, 2, 1]][r]:
                     octet_fold(o + 1, width)
             if r >= 4 and o + 2 < OCTETS:
-                octet_square(o + 2, (r - 4) * 256, (r - 3) * 256)
+                for lo in ((r - 4) * 256, (r - 4) * 256 + P):
+                    octet_square(o + 2, lo, lo + P)
             if r == 4 and o + 3 < OCTETS:
                 load_octet(o + 3)
-            if r == 2 and o + 2 < OCTETS:
+            if r == 4 and o + 2 < OCTETS:
                 octet_transpose(o + 2)
             if a + 1 < BLOCKS:
                 front_tensor(a + 1)
             front_vector(a)
             if o == 0 and r == 0:
                 octet_copy(nc.vector.tensor_copy, 1)
-            if r == 5 and o + 2 < OCTETS:
+            if r == 4 and o + 2 < OCTETS:
                 octet_copy(nc.vector.tensor_copy, o + 2)
             if a in group_ends:
                 group_min_d2(*group_ends[a])
@@ -284,15 +309,24 @@ def tile_kanadjunction_pa_t_kernel(tc, source, target, k_right, WF_right, out):
             if n < BLOCKS:
                 back_transpose(n)
             if n in products_at:
-                quad_products(products_at.index(n))
+                products(products_at.index(n))
             if n in quantise_at:
                 quad_reciprocal(quantise_at.index(n))
             if 0 <= n - 1 < BLOCKS:
                 back_copy(n - 1)
             if n in quantise_at:
-                quantise_quad(quantise_at.index(n))
+                quantise(quantise_at.index(n))
             if n - 1 in products_at:
                 quad_finish(products_at.index(n - 1))
+            i = n - 1 - 4 * LAST_QUAD
+            if 1 <= i <= 4:
+                products(LAST_QUAD, i - 1, i)
+            if 0 <= i < 4:
+                quantise(LAST_QUAD, i, i + 1)
+            if n == BLOCKS:
+                quad_reciprocal(LAST_QUAD)
+            if n == BLOCKS + 1:
+                quad_finish(LAST_QUAD)
             written["back"] = n + 1
 
         def units_up_to(front, back):
@@ -320,6 +354,8 @@ def tile_kanadjunction_pa_t_kernel(tc, source, target, k_right, WF_right, out):
                 assert first + i - E_SLOTS < written["back"]
                 scalar_exp(first + i)
                 written["exp"] = first + i + 1
+                for step in after_exp.get(first + i, []):
+                    step()
                 units_up_to(last + next_lead * (i + 1) // size + 1, first + (size - next_kept) * (i + 1) // size)
             first = last
         for n in range(written["back"], back_units):

@@ -24,11 +24,11 @@ INV_ROOT = 128.0 ** -0.5
 
 GROUPS = [8, 24, 32, 32, 32]
 DIST_SLOTS = 35
-E_SLOTS = 18
-LEAD = 2
-KEEP = 2
+E_SLOTS = 21
+LEAD = (1, 2)
+KEEP = (3, 5)
 RING = 5
-SRC_SLOTS = 7
+SRC_SLOTS = 9
 
 
 def tile_kanadjunction_pa_t_kernel(tc, source, target, k_right, WF_right, out):
@@ -45,7 +45,7 @@ def tile_kanadjunction_pa_t_kernel(tc, source, target, k_right, WF_right, out):
         neg_key_sq = keep.tile([P, 8, P], F32, name="neg_key_sq")
 
         def early_tile(j, dtype, name):
-            return keep.tile([P, 4096 // (2 if dtype == BF16 else 4)], dtype, name=name, tag="dist%d" % (DIST_SLOTS - 1 - j), align_bytes=64)
+            return keep.tile([P, 4096 // {BF16: 2, U32: 4, U8: 1}[dtype]], dtype, name=name, tag="dist%d" % (DIST_SLOTS - 1 - j), align_bytes=64)
 
         src_rows = [early_tile(g, BF16, "src_rows%d" % g) for g in range(2)]
         src_grouped = [early_tile(2 + g, BF16, "src_grouped%d" % g) for g in range(2)]
@@ -53,12 +53,13 @@ def tile_kanadjunction_pa_t_kernel(tc, source, target, k_right, WF_right, out):
         wf_tile = early_tile(5, BF16, "wf_tile")
         wf_rows, wf_grouped, f_grouped = wf_tile[:, 0:512], wf_tile[:, 512:1024], wf_tile[:, 1024:2048]
         key_rows = early_tile(6, BF16, "key_rows")
-        src_scales = keep.tile([P, 1024], U8, name="src_scales", align_bytes=64)
-        wf_codes = keep.tile([P, P], U32, name="wf_codes", align_bytes=64)
-        wf_scales = keep.tile([P, P], U8, name="wf_scales", align_bytes=64)
+        wf_codes = early_tile(7, U32, "wf_codes")[:, 0:P]
+        scales_tile = early_tile(8, U8, "scales_tile")
+        src_scales, wf_scales = scales_tile[:, 0:1024], scales_tile[:, 1024:1024 + P]
         f_codes = keep.tile([P, 256], U32, name="f_codes", align_bytes=64)
         f_scales = keep.tile([P, 256], U8, name="f_scales", align_bytes=64)
         scratch = keep.tile([P, P], F32, name="scratch")
+        minus_one = keep.tile([P, 1], F32, name="minus_one")
         tgt_sq = keep.tile([P, BLOCKS], F32, name="tgt_sq")
         bank_max = keep.tile([P, 2 * BLOCKS], F32, name="bank_max")
         row_max = keep.tile([P, BLOCKS], F32, name="row_max")
@@ -69,13 +70,13 @@ def tile_kanadjunction_pa_t_kernel(tc, source, target, k_right, WF_right, out):
         inv_sum = keep.tile([P, BLOCKS], F32, name="inv_sum")
         squares = keep.tile([P, 1024], F32, name="squares")
         tgt_rows = [keep.tile([P, 1024], BF16, name="tgt_rows%d" % i) for i in range(3)]
-        tgtT = [keep.tile([P, 1024], BF16, name="tgtT%d" % i) for i in range(3)]
+        tgtT = [keep.tile([P, 1024], BF16, name="tgtT%d" % i) for i in range(2)]
         dist = [keep.tile([P, KEYS], F32, name="dist%d" % i, align_bytes=64) for i in range(DIST_SLOTS - SRC_SLOTS)]
         e = [keep.tile([P, KEYS], BF16, name="e%d" % i) for i in range(E_SLOTS)]
         grouped = [keep.tile([P, 4 * KEYS], BF16, name="grouped%d" % i, align_bytes=64) for i in range(2)]
         codes = [keep.tile([P, 1024], U32, name="codes%d" % i, align_bytes=64) for i in range(2)]
         scales = [keep.tile([P, 1024], U8, name="scales%d" % i, align_bytes=64) for i in range(2)]
-        out_sb = [keep.tile([P, 512], F32, name="out_sb%d" % i) for i in range(2)]
+        out_sb = keep.tile([P, 512], F32, name="out_sb")
         bank = {}
         turns = []
 
@@ -96,7 +97,7 @@ def tile_kanadjunction_pa_t_kernel(tc, source, target, k_right, WF_right, out):
             bank["x", o] = transpose8(tgt_rows[o % 3])
 
         def octet_copy(engine_copy, o):
-            engine_copy(out=tgtT[o % 3][:], in_=bank["x", o][:])
+            engine_copy(out=tgtT[o % 2][:], in_=bank["x", o][:])
 
         def octet_square(o, lo, hi):
             rows = tgt_rows[o % 3]
@@ -115,7 +116,7 @@ def tile_kanadjunction_pa_t_kernel(tc, source, target, k_right, WF_right, out):
                     nc.tensor.matmul(yb[:, t * P:(t + 1) * P], lhsT=neg_key_sq[:, 4 * g + t, :], rhs=ident_f[:], is_transpose=True, start=(t == 0), stop=False)
                 bank["y", a, g] = yb
             for g in range(2):
-                nc.tensor.matmul(bank["y", a, g][:], lhsT=tgtT[o % 3][:, i * P:(i + 1) * P], rhs=keysT[:, g * 512:(g + 1) * 512], start=False, stop=True)
+                nc.tensor.matmul(bank["y", a, g][:], lhsT=tgtT[o % 2][:, i * P:(i + 1) * P], rhs=keysT[:, g * 512:(g + 1) * 512], start=False, stop=True)
 
         def front_vector(a):
             for g in range(2):
@@ -131,7 +132,7 @@ def tile_kanadjunction_pa_t_kernel(tc, source, target, k_right, WF_right, out):
 
         def scalar_group_bias(a0, a1):
             nc.scalar.activation(out=min_dist[:, a0:a1], in_=min_d2[:, a0:a1], func=ACT.Sqrt)
-            nc.scalar.activation(out=exp_bias[:, a0:a1], in_=min_dist[:, a0:a1], func=ACT.Copy, scale=INV_ROOT)
+            nc.gpsimd.tensor_scalar(out=exp_bias[:, a0:a1], in0=min_dist[:, a0:a1], scalar1=INV_ROOT, scalar2=0.0, op0=ALU.mult, op1=ALU.add)
 
         def scalar_exp(a):
             nc.scalar.activation(out=e[a % E_SLOTS][:], in_=dist[a % DIST_SLOTS][:], func=ACT.Exp, bias=exp_bias[:, a:a + 1], scale=-INV_ROOT, accum_out=row_sum[:, a:a + 1])
@@ -157,13 +158,13 @@ def tile_kanadjunction_pa_t_kernel(tc, source, target, k_right, WF_right, out):
                                         rhs=f_codes[:, g * P:(g + 1) * P].bitcast(FP8X4), rhs_scale=f_scales[:, g * P:(g + 1) * P], start=(g == 0), stop=(g == 1))
 
         def quad_reciprocal(q):
-            nc.vector.reciprocal(out=inv_sum[:, 4 * q:4 * q + 4], in_=row_sum[:, 4 * q:4 * q + 4])
+            nc.gpsimd.tensor_tensor(out=inv_sum[:, 4 * q:4 * q + 4], in0=row_sum[:, 4 * q:4 * q + 4], in1=minus_one[:].to_broadcast([P, 4]), op=ALU.pow)
 
         def quad_finish(q):
-            nc.vector.tensor_tensor(out=out_sb[q % 2][:].rearrange("p (i d) -> p i d", i=4), in0=bank["o", q][:].rearrange("p (i d) -> p i d", i=4),
+            nc.vector.tensor_tensor(out=out_sb[:].rearrange("p (i d) -> p i d", i=4), in0=bank["o", q][:].rearrange("p (i d) -> p i d", i=4),
                                     in1=inv_sum[:, 4 * q:4 * q + 4].unsqueeze(2).to_broadcast([P, 4, P]), op=ALU.mult)
             o, h = divmod(q, 2)
-            nc.sync.dma_start(out=out[o * 1024:(o + 1) * 1024, :].rearrange("(p i) d -> p (i d)", i=8)[:, h * 512:(h + 1) * 512], in_=out_sb[q % 2][:])
+            nc.sync.dma_start(out=out[o * 1024:(o + 1) * 1024, :].rearrange("(p i) d -> p (i d)", i=8)[:, h * 512:(h + 1) * 512], in_=out_sb[:])
 
         def words_transpose(tag, rows, chunks):
             pw = psum.tile([P, 2 * chunks * P], F32, name="pw", tag=tag)
@@ -188,7 +189,7 @@ def tile_kanadjunction_pa_t_kernel(tc, source, target, k_right, WF_right, out):
             words_copy(nc.scalar.copy, bank["s", j], src_grouped[j // 2][:, (j % 2) * 1024:(j % 2 + 1) * 1024], 2)
 
         def wf_quantise():
-            nc.vector.quantize_mx(out=wf_codes[:].bitcast(FP8X4), scales=wf_scales[:], in_=wf_grouped)
+            nc.vector.quantize_mx(out=wf_codes.bitcast(FP8X4), scales=wf_scales, in_=wf_grouped)
 
         def src_quantise(g):
             nc.vector.quantize_mx(out=src_codes[:, g * 512:(g + 1) * 512].bitcast(FP8X4), scales=src_scales[:, g * 512:(g + 1) * 512], in_=src_grouped[g][:])
@@ -198,7 +199,7 @@ def tile_kanadjunction_pa_t_kernel(tc, source, target, k_right, WF_right, out):
             for t in range(4):
                 c = 4 * g + t
                 nc.tensor.matmul_mx(out=fb[:, t * P:(t + 1) * P], lhsT=src_codes[:, c * P:(c + 1) * P].bitcast(FP8X4), lhsT_scale=src_scales[:, c * P:(c + 1) * P],
-                                    rhs=wf_codes[:].bitcast(FP8X4), rhs_scale=wf_scales[:], start=True, stop=True)
+                                    rhs=wf_codes.bitcast(FP8X4), rhs_scale=wf_scales, start=True, stop=True)
             bank["f", g] = fb
 
         def f_copy(g):
@@ -218,6 +219,7 @@ def tile_kanadjunction_pa_t_kernel(tc, source, target, k_right, WF_right, out):
         load_octet(2)
         make_identity(nc, ident_b[:])
         make_identity(nc, ident_f[:])
+        nc.vector.memset(minus_one[:], -1.0)
         nc.vector.memset(scratch[:, 0:1], 1.0)
         nc.scalar.activation(out=scratch[:, 1:2], in_=scratch[:, 0:1], func=ACT.Sqrt)
         keys_bank = psum.tile([P, 1024], BF16, name="keys_bank", tag=next_bank())
@@ -275,8 +277,6 @@ def tile_kanadjunction_pa_t_kernel(tc, source, target, k_right, WF_right, out):
                 dist.extend([keep.tile([P, KEYS], F32, name="dist%d" % i, align_bytes=64) for i in range(len(dist), DIST_SLOTS)])
             o, r = divmod(a, 8)
             if o == 0:
-                if r == 0:
-                    octet_transpose(1)
                 if r < 4:
                     for lo in (r * 256, r * 256 + P):
                         octet_square(1, lo, lo + P)
@@ -289,17 +289,15 @@ def tile_kanadjunction_pa_t_kernel(tc, source, target, k_right, WF_right, out):
             if r >= 4 and o + 2 < OCTETS:
                 for lo in ((r - 4) * 256, (r - 4) * 256 + P):
                     octet_square(o + 2, lo, lo + P)
-            if r == 4 and o + 3 < OCTETS:
+            if r == 0 and o + 3 < OCTETS:
                 load_octet(o + 3)
-            if r == 4 and o + 2 < OCTETS:
-                octet_transpose(o + 2)
+            if r == 4 and o + 1 < OCTETS:
+                octet_transpose(o + 1)
             if a + 1 < BLOCKS:
                 front_tensor(a + 1)
             front_vector(a)
-            if o == 0 and r == 0:
-                octet_copy(nc.vector.tensor_copy, 1)
-            if r == 4 and o + 2 < OCTETS:
-                octet_copy(nc.vector.tensor_copy, o + 2)
+            if r == 4 and o + 1 < OCTETS:
+                octet_copy(nc.vector.tensor_copy, o + 1)
             if a in group_ends:
                 group_min_d2(*group_ends[a])
             written["front"] = a + 1
@@ -337,13 +335,16 @@ def tile_kanadjunction_pa_t_kernel(tc, source, target, k_right, WF_right, out):
                 if written["front"] < front:
                     front_unit(written["front"])
 
+        def share(size, part):
+            return size * part[0] // part[1]
+
         first = 0
         for k, size in enumerate(GROUPS):
             last = first + size
-            lead = size // LEAD if k > 0 else 0
-            kept = GROUPS[k - 1] // KEEP if k > 0 else 0
-            next_lead = GROUPS[k + 1] // LEAD if k + 1 < len(GROUPS) else 0
-            next_kept = size // KEEP if k + 1 < len(GROUPS) else 0
+            lead = share(size, LEAD) if k > 0 else 0
+            kept = share(GROUPS[k - 1], KEEP) if k > 0 else 0
+            next_lead = share(GROUPS[k + 1], LEAD) if k + 1 < len(GROUPS) else 0
+            next_kept = share(size, KEEP) if k + 1 < len(GROUPS) else 0
             for i in range(size):
                 units_up_to(first + lead + ((size - lead) * (i + 1) + size - 1) // size + 1, first - kept + kept * (i + 1) // size)
                 scalar_sqrt(first + i)

@@ -22,11 +22,10 @@ QUADS = BLOCKS // 4
 LAST_QUAD = QUADS - 1
 INV_ROOT = 128.0 ** -0.5
 
-GROUPS = [8, 24, 32, 32, 32]
-DIST_SLOTS = 35
-E_SLOTS = 21
+GROUPS = [8, 40, 40, 40]
+DIST_SLOTS = 45
 LEAD = (1, 2)
-KEEP = (3, 5)
+KEEP = (1, 2)
 RING = 5
 SRC_SLOTS = 9
 
@@ -72,11 +71,10 @@ def tile_kanadjunction_pa_t_kernel(tc, source, target, k_right, WF_right, out):
         tgt_rows = [keep.tile([P, 1024], BF16, name="tgt_rows%d" % i) for i in range(3)]
         tgtT = [keep.tile([P, 1024], BF16, name="tgtT%d" % i) for i in range(2)]
         dist = [keep.tile([P, KEYS], F32, name="dist%d" % i, align_bytes=64) for i in range(DIST_SLOTS - SRC_SLOTS)]
-        e = [keep.tile([P, KEYS], BF16, name="e%d" % i) for i in range(E_SLOTS)]
         grouped = [keep.tile([P, 4 * KEYS], BF16, name="grouped%d" % i, align_bytes=64) for i in range(2)]
         codes = [keep.tile([P, 1024], U32, name="codes%d" % i, align_bytes=64) for i in range(2)]
         scales = [keep.tile([P, 1024], U8, name="scales%d" % i, align_bytes=64) for i in range(2)]
-        out_sb = keep.tile([P, 512], F32, name="out_sb")
+        out_sb = [keep.tile([P, 512], F32, name="out_sb%d" % i) for i in range(2)]
         bank = {}
         turns = []
 
@@ -134,11 +132,14 @@ def tile_kanadjunction_pa_t_kernel(tc, source, target, k_right, WF_right, out):
             nc.scalar.activation(out=min_dist[:, a0:a1], in_=min_d2[:, a0:a1], func=ACT.Sqrt)
             nc.gpsimd.tensor_scalar(out=exp_bias[:, a0:a1], in0=min_dist[:, a0:a1], scalar1=INV_ROOT, scalar2=0.0, op0=ALU.mult, op1=ALU.add)
 
+        def e_rows(a):
+            return dist[a % DIST_SLOTS][:].bitcast(BF16)[:, 0:KEYS]
+
         def scalar_exp(a):
-            nc.scalar.activation(out=e[a % E_SLOTS][:], in_=dist[a % DIST_SLOTS][:], func=ACT.Exp, bias=exp_bias[:, a:a + 1], scale=-INV_ROOT, accum_out=row_sum[:, a:a + 1])
+            nc.scalar.activation(out=e_rows(a), in_=dist[a % DIST_SLOTS][:], func=ACT.Exp, bias=exp_bias[:, a:a + 1], scale=-INV_ROOT, accum_out=row_sum[:, a:a + 1])
 
         def back_transpose(b):
-            bank["t", b] = words_transpose("T%d" % (b % 2), e[b % E_SLOTS], 2)
+            bank["t", b] = words_transpose("T%d" % (b % 2), e_rows(b), 2)
 
         def back_copy(b):
             words_copy(nc.vector.tensor_copy, bank["t", b], grouped[b // 4 % 2][:, (b % 4) * KEYS:(b % 4 + 1) * KEYS], 2)
@@ -161,10 +162,10 @@ def tile_kanadjunction_pa_t_kernel(tc, source, target, k_right, WF_right, out):
             nc.gpsimd.tensor_tensor(out=inv_sum[:, 4 * q:4 * q + 4], in0=row_sum[:, 4 * q:4 * q + 4], in1=minus_one[:].to_broadcast([P, 4]), op=ALU.pow)
 
         def quad_finish(q):
-            nc.vector.tensor_tensor(out=out_sb[:].rearrange("p (i d) -> p i d", i=4), in0=bank["o", q][:].rearrange("p (i d) -> p i d", i=4),
+            nc.vector.tensor_tensor(out=out_sb[q % 2][:].rearrange("p (i d) -> p i d", i=4), in0=bank["o", q][:].rearrange("p (i d) -> p i d", i=4),
                                     in1=inv_sum[:, 4 * q:4 * q + 4].unsqueeze(2).to_broadcast([P, 4, P]), op=ALU.mult)
             o, h = divmod(q, 2)
-            nc.sync.dma_start(out=out[o * 1024:(o + 1) * 1024, :].rearrange("(p i) d -> p (i d)", i=8)[:, h * 512:(h + 1) * 512], in_=out_sb[:])
+            nc.sync.dma_start(out=out[o * 1024:(o + 1) * 1024, :].rearrange("(p i) d -> p (i d)", i=8)[:, h * 512:(h + 1) * 512], in_=out_sb[q % 2][:])
 
         def words_transpose(tag, rows, chunks):
             pw = psum.tile([P, 2 * chunks * P], F32, name="pw", tag=tag)
@@ -270,7 +271,7 @@ def tile_kanadjunction_pa_t_kernel(tc, source, target, k_right, WF_right, out):
         after_exp = {0: [lambda: f_copy(0)], 1: [lambda: f_copy(1)]}
 
         def front_unit(a):
-            assert a - DIST_SLOTS < written["exp"]
+            assert a - DIST_SLOTS < written["back"]
             for step in before.get(a, []):
                 step()
             if a == DIST_SLOTS - SRC_SLOTS:
@@ -352,7 +353,6 @@ def tile_kanadjunction_pa_t_kernel(tc, source, target, k_right, WF_right, out):
                     step()
             scalar_group_bias(first, last)
             for i in range(size):
-                assert first + i - E_SLOTS < written["back"]
                 scalar_exp(first + i)
                 written["exp"] = first + i + 1
                 for step in after_exp.get(first + i, []):

@@ -22,8 +22,9 @@ QUADS = BLOCKS // 4
 LAST_QUAD = QUADS - 1
 INV_ROOT = 128.0 ** -0.5
 
-GROUPS = [8, 40, 40, 40]
+GROUPS = [10, 38, 40, 40]
 DIST_SLOTS = 45
+BACKLOG = 3
 LEAD = (1, 2)
 KEEP = (1, 2)
 RING = 5
@@ -82,8 +83,8 @@ def tile_kanadjunction_pa_t_kernel(tc, source, target, k_right, WF_right, out):
             turns.append(len(turns) % RING)
             return "R%d" % turns[-1]
 
-        def transpose8(rows):
-            pb = psum.tile([P, 1024], BF16, name="pb", tag=next_bank())
+        def transpose8(rows, tag):
+            pb = psum.tile([P, 1024], BF16, name="pb", tag=tag)
             for i in range(8):
                 nc.tensor.transpose(pb[:, i * P:(i + 1) * P], rows[:, i * P:(i + 1) * P], ident_b[:])
             return pb
@@ -92,10 +93,10 @@ def tile_kanadjunction_pa_t_kernel(tc, source, target, k_right, WF_right, out):
             nc.sync.dma_start(out=tgt_rows[o % 3][:], in_=target[o * 1024:(o + 1) * 1024, :].rearrange("(p i) e -> p (i e)", i=8))
 
         def octet_transpose(o):
-            bank["x", o] = transpose8(tgt_rows[o % 3])
+            bank["x", o] = transpose8(tgt_rows[o % 3], "T%d" % (written["back"] % 2) if o > 0 else next_bank())
 
-        def octet_copy(engine_copy, o):
-            engine_copy(out=tgtT[o % 2][:], in_=bank["x", o][:])
+        def octet_copy(o):
+            nc.vector.tensor_copy(out=tgtT[o % 2][:], in_=bank["x", o][:])
 
         def octet_square(o, lo, hi):
             rows = tgt_rows[o % 3]
@@ -249,7 +250,7 @@ def tile_kanadjunction_pa_t_kernel(tc, source, target, k_right, WF_right, out):
             target_squares(c)
         nc.vector.tensor_scalar(out=keysT[:], in0=keys_bank[:], scalar1=2.0, scalar2=None, op0=ALU.mult)
         key_spread(0)
-        octet_copy(nc.vector.tensor_copy, 0)
+        octet_copy(0)
         key_spread(1)
         front_tensor(0)
 
@@ -264,11 +265,13 @@ def tile_kanadjunction_pa_t_kernel(tc, source, target, k_right, WF_right, out):
             first += size
         assert first == BLOCKS
 
-        before = {1: [wf_transpose], 2: [lambda: src_transpose(0)], 3: [lambda: src_transpose(1)], 4: [lambda: src_transpose(2)], 5: [lambda: src_transpose(3)],
-                  7: [wf_quantise, lambda: src_quantise(0)], 8: [lambda: src_quantise(1), lambda: f_products(0)], 9: [lambda: f_products(1)],
-                  14: [f_quantise]}
-        after_sqrt = {0: [wf_copy], 1: [lambda: src_copy(0)], 2: [lambda: src_copy(1)], 3: [lambda: src_copy(2)], 4: [lambda: src_copy(3)]}
-        after_exp = {0: [lambda: f_copy(0)], 1: [lambda: f_copy(1)]}
+        f0 = 1
+        before = {f0: [wf_transpose], f0 + 6: [wf_quantise, lambda: src_quantise(0)], f0 + 7: [lambda: src_quantise(1), lambda: f_products(0)],
+                  f0 + 8: [lambda: f_products(1)], f0 + 12: [f_quantise]}
+        after = {f0: [wf_copy], f0 + 8: [lambda: f_copy(0)], f0 + 9: [lambda: f_copy(1)]}
+        for j in range(4):
+            before[f0 + 1 + j] = [lambda j=j: src_transpose(j)]
+            after[f0 + 1 + j] = [lambda j=j: src_copy(j)]
 
         def front_unit(a):
             assert a - DIST_SLOTS < written["back"]
@@ -292,15 +295,17 @@ def tile_kanadjunction_pa_t_kernel(tc, source, target, k_right, WF_right, out):
                     octet_square(o + 2, lo, lo + P)
             if r == 0 and o + 3 < OCTETS:
                 load_octet(o + 3)
-            if r == 4 and o + 1 < OCTETS:
+            if r == (0 if o > 0 else 4) and o + 1 < OCTETS:
                 octet_transpose(o + 1)
             if a + 1 < BLOCKS:
                 front_tensor(a + 1)
             front_vector(a)
-            if r == 4 and o + 1 < OCTETS:
-                octet_copy(nc.vector.tensor_copy, o + 1)
+            if r == (0 if o > 0 else 4) and o + 1 < OCTETS:
+                octet_copy(o + 1)
             if a in group_ends:
                 group_min_d2(*group_ends[a])
+            for step in after.get(a, []):
+                step()
             written["front"] = a + 1
 
         def back_unit(n):
@@ -329,7 +334,7 @@ def tile_kanadjunction_pa_t_kernel(tc, source, target, k_right, WF_right, out):
             written["back"] = n + 1
 
         def units_up_to(front, back):
-            front, back = min(front, BLOCKS), min(back, written["exp"])
+            front, back = min(front, BLOCKS), min(back - BACKLOG, written["exp"])
             while written["front"] < front or written["back"] < back:
                 if written["back"] < back:
                     back_unit(written["back"])
@@ -349,15 +354,12 @@ def tile_kanadjunction_pa_t_kernel(tc, source, target, k_right, WF_right, out):
             for i in range(size):
                 units_up_to(first + lead + ((size - lead) * (i + 1) + size - 1) // size + 1, first - kept + kept * (i + 1) // size)
                 scalar_sqrt(first + i)
-                for step in after_sqrt.get(first + i, []):
-                    step()
             scalar_group_bias(first, last)
+            caught_up = BACKLOG if k + 1 == len(GROUPS) else 0
             for i in range(size):
                 scalar_exp(first + i)
                 written["exp"] = first + i + 1
-                for step in after_exp.get(first + i, []):
-                    step()
-                units_up_to(last + next_lead * (i + 1) // size + 1, first + (size - next_kept) * (i + 1) // size)
+                units_up_to(last + next_lead * (i + 1) // size + 1, first + (size - next_kept) * (i + 1) // size + caught_up * (i + 1) // size)
             first = last
         for n in range(written["back"], back_units):
             back_unit(n)

@@ -22,11 +22,12 @@ QUADS = BLOCKS // 4
 LAST_QUAD = QUADS - 1
 INV_ROOT = 128.0 ** -0.5
 
-GROUPS = [10, 38, 40, 40]
+GROUPS = [14, 38, 38, 38]
 DIST_SLOTS = 45
-BACKLOG = 3
+BACKLOG = 5
 LEAD = (1, 2)
 KEEP = (1, 2)
+BACK_RING = 3
 RING = 5
 SRC_SLOTS = 9
 
@@ -78,10 +79,15 @@ def tile_kanadjunction_pa_t_kernel(tc, source, target, k_right, WF_right, out):
         out_sb = [keep.tile([P, 512], F32, name="out_sb%d" % i) for i in range(2)]
         bank = {}
         turns = []
+        back_turns = []
 
         def next_bank():
             turns.append(len(turns) % RING)
             return "R%d" % turns[-1]
+
+        def next_back_bank():
+            back_turns.append(len(back_turns) % BACK_RING)
+            return "B%d" % back_turns[-1]
 
         def transpose8(rows, tag):
             pb = psum.tile([P, 1024], BF16, name="pb", tag=tag)
@@ -93,7 +99,7 @@ def tile_kanadjunction_pa_t_kernel(tc, source, target, k_right, WF_right, out):
             nc.sync.dma_start(out=tgt_rows[o % 3][:], in_=target[o * 1024:(o + 1) * 1024, :].rearrange("(p i) e -> p (i e)", i=8))
 
         def octet_transpose(o):
-            bank["x", o] = transpose8(tgt_rows[o % 3], "T%d" % (written["back"] % 2) if o > 0 else next_bank())
+            bank["x", o] = transpose8(tgt_rows[o % 3], next_back_bank() if o > 0 else next_bank())
 
         def octet_copy(o):
             nc.vector.tensor_copy(out=tgtT[o % 2][:], in_=bank["x", o][:])
@@ -140,7 +146,7 @@ def tile_kanadjunction_pa_t_kernel(tc, source, target, k_right, WF_right, out):
             nc.scalar.activation(out=e_rows(a), in_=dist[a % DIST_SLOTS][:], func=ACT.Exp, bias=exp_bias[:, a:a + 1], scale=-INV_ROOT, accum_out=row_sum[:, a:a + 1])
 
         def back_transpose(b):
-            bank["t", b] = words_transpose("T%d" % (b % 2), e_rows(b), 2)
+            bank["t", b] = words_transpose(next_back_bank(), e_rows(b), 2)
 
         def back_copy(b):
             words_copy(nc.vector.tensor_copy, bank["t", b], grouped[b // 4 % 2][:, (b % 4) * KEYS:(b % 4 + 1) * KEYS], 2)
@@ -151,7 +157,7 @@ def tile_kanadjunction_pa_t_kernel(tc, source, target, k_right, WF_right, out):
 
         def products(q, i0=0, i1=4):
             if i0 == 0:
-                bank["o", q] = psum.tile([P, 512], F32, name="ob", tag="O" if q < LAST_QUAD else next_bank())
+                bank["o", q] = psum.tile([P, 512], F32, name="ob", tag=next_back_bank() if q < LAST_QUAD else next_bank())
             ob = bank["o", q]
             for i in range(i0, i1):
                 for g in range(2):

@@ -43,7 +43,7 @@ def tile_kanadjunction_pa_t_kernel(tc, source, target, k_right, WF_right, out):
         ident_b = keep.tile([P, P], BF16, name="ident_b")
         keysT = keep.tile([P, KEYS], BF16, name="keysT")
         key_sq = keep.tile([P, 8], F32, name="key_sq")
-        neg_key_sq = keep.tile([P, 8, P], F32, name="neg_key_sq")
+        neg_key_sq = keep.tile([P, 8], F32, name="neg_key_sq")
 
         def early_tile(j, dtype, name):
             return keep.tile([P, 4096 // {BF16: 2, U32: 4, U8: 1}[dtype]], dtype, name=name, tag="dist%d" % (DIST_SLOTS - 1 - j), align_bytes=64)
@@ -118,7 +118,7 @@ def tile_kanadjunction_pa_t_kernel(tc, source, target, k_right, WF_right, out):
             for g in range(2):
                 yb = psum.tile([P, 512], F32, name="yb", tag=next_bank())
                 for t in range(4):
-                    nc.tensor.matmul(yb[:, t * P:(t + 1) * P], lhsT=neg_key_sq[:, 4 * g + t, :], rhs=ident_f[:], is_transpose=True, start=(t == 0), stop=False)
+                    nc.tensor.matmul(yb[:, t * P:(t + 1) * P], lhsT=neg_key_sq[:, 4 * g + t:4 * g + t + 1].to_broadcast([P, P]), rhs=ident_f[:], is_transpose=True, start=(t == 0), stop=False)
                 bank["y", a, g] = yb
             for g in range(2):
                 nc.tensor.matmul(bank["y", a, g][:], lhsT=tgtT[o % 2][:, i * P:(i + 1) * P], rhs=keysT[:, g * 512:(g + 1) * 512], start=False, stop=True)
@@ -246,8 +246,8 @@ def tile_kanadjunction_pa_t_kernel(tc, source, target, k_right, WF_right, out):
         def target_squares(c):
             nc.scalar.activation(out=scratch[:], in_=tgt_rows[0][:, c * P:(c + 1) * P], func=ACT.Square, accum_out=tgt_sq[:, c:c + 1])
 
-        def key_spread(g):
-            nc.vector.tensor_scalar(out=neg_key_sq[:, 4 * g:4 * g + 4, :], in0=key_sq[:, 4 * g:4 * g + 4].unsqueeze(2).to_broadcast([P, 4, P]), scalar1=-1.0, scalar2=None, op0=ALU.mult)
+        def key_negate(g):
+            nc.vector.tensor_scalar(out=neg_key_sq[:, 4 * g:4 * g + 4], in0=key_sq[:, 4 * g:4 * g + 4], scalar1=-1.0, scalar2=None, op0=ALU.mult)
 
         key_squares(0)
         target_squares(0)
@@ -255,9 +255,9 @@ def tile_kanadjunction_pa_t_kernel(tc, source, target, k_right, WF_right, out):
         for c in range(1, 8):
             target_squares(c)
         nc.vector.tensor_scalar(out=keysT[:], in0=keys_bank[:], scalar1=2.0, scalar2=None, op0=ALU.mult)
-        key_spread(0)
+        key_negate(0)
         octet_copy(0)
-        key_spread(1)
+        key_negate(1)
         front_tensor(0)
 
         quantise_at = [4 * q + 5 for q in range(QUADS - 1)]

@@ -19,12 +19,12 @@ KEYS = 1024
 BLOCKS = 128
 OCTETS = BLOCKS // 8
 QUADS = BLOCKS // 4
-LAST_QUAD = QUADS - 1
+WHOLE_QUADS = QUADS - 2
 INV_ROOT = 128.0 ** -0.5
 
-GROUPS = [14, 38, 38, 38]
+GROUPS = [10, 38, 40, 40]
 DIST_SLOTS = 45
-BACKLOG = 5
+BACKLOG = 3
 LEAD = (1, 2)
 KEEP = (1, 2)
 BACK_RING = 3
@@ -157,7 +157,7 @@ def tile_kanadjunction_pa_t_kernel(tc, source, target, k_right, WF_right, out):
 
         def products(q, i0=0, i1=4):
             if i0 == 0:
-                bank["o", q] = psum.tile([P, 512], F32, name="ob", tag=next_back_bank() if q < LAST_QUAD else next_bank())
+                bank["o", q] = psum.tile([P, 512], F32, name="ob", tag=next_back_bank() if q < WHOLE_QUADS else next_bank())
             ob = bank["o", q]
             for i in range(i0, i1):
                 for g in range(2):
@@ -165,14 +165,16 @@ def tile_kanadjunction_pa_t_kernel(tc, source, target, k_right, WF_right, out):
                     nc.tensor.matmul_mx(out=ob[:, i * P:(i + 1) * P], lhsT=codes[q % 2][:, c0:c0 + P].bitcast(FP8X4), lhsT_scale=scales[q % 2][:, c0:c0 + P],
                                         rhs=f_codes[:, g * P:(g + 1) * P].bitcast(FP8X4), rhs_scale=f_scales[:, g * P:(g + 1) * P], start=(g == 0), stop=(g == 1))
 
-        def quad_reciprocal(q):
-            nc.gpsimd.tensor_tensor(out=inv_sum[:, 4 * q:4 * q + 4], in0=row_sum[:, 4 * q:4 * q + 4], in1=minus_one[:].to_broadcast([P, 4]), op=ALU.pow)
+        def reciprocals(q, i0=0, i1=4):
+            b0, b1 = 4 * q + i0, 4 * q + i1
+            nc.gpsimd.tensor_tensor(out=inv_sum[:, b0:b1], in0=row_sum[:, b0:b1], in1=minus_one[:].to_broadcast([P, b1 - b0]), op=ALU.pow)
 
-        def quad_finish(q):
-            nc.vector.tensor_tensor(out=out_sb[q % 2][:].rearrange("p (i d) -> p i d", i=4), in0=bank["o", q][:].rearrange("p (i d) -> p i d", i=4),
-                                    in1=inv_sum[:, 4 * q:4 * q + 4].unsqueeze(2).to_broadcast([P, 4, P]), op=ALU.mult)
+        def finish(q, i0=0, i1=4):
+            cols = slice(i0 * P, i1 * P)
+            nc.vector.tensor_tensor(out=out_sb[q % 2][:, cols].rearrange("p (i d) -> p i d", d=P), in0=bank["o", q][:, cols].rearrange("p (i d) -> p i d", d=P),
+                                    in1=inv_sum[:, 4 * q + i0:4 * q + i1].unsqueeze(2).to_broadcast([P, i1 - i0, P]), op=ALU.mult)
             o, h = divmod(q, 2)
-            nc.sync.dma_start(out=out[o * 1024:(o + 1) * 1024, :].rearrange("(p i) d -> p (i d)", i=8)[:, h * 512:(h + 1) * 512], in_=out_sb[q % 2][:])
+            nc.sync.dma_start(out=out[o * 1024:(o + 1) * 1024, :].rearrange("(p i) d -> p (i d)", i=8)[:, h * 512 + i0 * P:h * 512 + i1 * P], in_=out_sb[q % 2][:, cols])
 
         def words_transpose(tag, rows, chunks):
             pw = psum.tile([P, 2 * chunks * P], F32, name="pw", tag=tag)
@@ -260,8 +262,8 @@ def tile_kanadjunction_pa_t_kernel(tc, source, target, k_right, WF_right, out):
         key_negate(1)
         front_tensor(0)
 
-        quantise_at = [4 * q + 5 for q in range(QUADS - 1)]
-        products_at = [4 * q + 6 for q in range(QUADS - 1)]
+        quantise_at = [4 * q + 5 for q in range(WHOLE_QUADS)]
+        products_at = [4 * q + 6 for q in range(WHOLE_QUADS)]
         back_units = BLOCKS + 2
         written = {"front": 0, "back": 0, "exp": 0}
         group_ends = {}
@@ -321,22 +323,30 @@ def tile_kanadjunction_pa_t_kernel(tc, source, target, k_right, WF_right, out):
             if n in products_at:
                 products(products_at.index(n))
             if n in quantise_at:
-                quad_reciprocal(quantise_at.index(n))
+                reciprocals(quantise_at.index(n))
             if 0 <= n - 1 < BLOCKS:
                 back_copy(n - 1)
             if n in quantise_at:
                 quantise(quantise_at.index(n))
             if n - 1 in products_at:
-                quad_finish(products_at.index(n - 1))
-            i = n - 1 - 4 * LAST_QUAD
-            if 1 <= i <= 4:
-                products(LAST_QUAD, i - 1, i)
-            if 0 <= i < 4:
-                quantise(LAST_QUAD, i, i + 1)
+                finish(products_at.index(n - 1))
+            q, i = divmod(n - 2, 4)
+            if WHOLE_QUADS <= q < QUADS:
+                products(q, i, i + 1)
+            q, i = divmod(n - 1, 4)
+            if WHOLE_QUADS <= q < QUADS:
+                quantise(q, i, i + 1)
+            if n == BLOCKS - 3:
+                reciprocals(QUADS - 2)
+            if n == BLOCKS - 2:
+                finish(QUADS - 2)
+            if n == BLOCKS - 1:
+                reciprocals(QUADS - 1, 0, 3)
             if n == BLOCKS:
-                quad_reciprocal(LAST_QUAD)
+                reciprocals(QUADS - 1, 3, 4)
             if n == BLOCKS + 1:
-                quad_finish(LAST_QUAD)
+                finish(QUADS - 1, 0, 3)
+                finish(QUADS - 1, 3, 4)
             written["back"] = n + 1
 
         def units_up_to(front, back):

from contextlib import ExitStack

import concourse.mybir as mybir
from concourse.masks import make_identity

FLOPS = 2 * 1024 * 512 * 128 + 2 * 2 * 16384 * 1024 * 128

BF16 = mybir.dt.bfloat16
F32 = mybir.dt.float32
U32 = mybir.dt.uint32
U8 = mybir.dt.uint8
FP8X4 = mybir.dt.float8_e4m3fn_x4
ALU = mybir.AluOpType
ACT = mybir.ActivationFunctionType
AX = mybir.AxisListType

P = 128
KEYS = 1024
BLOCKS = 128
OCTETS = BLOCKS // 8
QUADS = BLOCKS // 4
WHOLE_QUADS = QUADS - 2
INV_ROOT = 128.0 ** -0.5

GROUPS = [10, 38, 40, 40]
DIST_SLOTS = 45
BACKLOG = 3
LEAD = (1, 2)
KEEP = (1, 2)
BACK_RING = 3
RING = 5
SRC_SLOTS = 9


def tile_kanadjunction_pa_t_kernel(tc, source, target, k_right, WF_right, out):
    nc = tc.nc
    with ExitStack() as ctx:
        keep = ctx.enter_context(tc.tile_pool(name="keep", bufs=1))
        psum = ctx.enter_context(tc.psum_pool(name="psum", bufs=1))
        ctx.enter_context(tc.manual_schedule())

        ident_f = keep.tile([P, P], F32, name="ident_f")
        ident_b = keep.tile([P, P], BF16, name="ident_b")
        keysT = keep.tile([P, KEYS], BF16, name="keysT")
        key_sq = keep.tile([P, 8], F32, name="key_sq")
        neg_key_sq = keep.tile([P, 8], F32, name="neg_key_sq")

        def early_tile(j, dtype, name):
            return keep.tile([P, 4096 // {BF16: 2, U32: 4, U8: 1}[dtype]], dtype, name=name, tag="dist%d" % (DIST_SLOTS - 1 - j), align_bytes=64)

        src_rows = [early_tile(g, BF16, "src_rows%d" % g) for g in range(2)]
        src_grouped = [early_tile(2 + g, BF16, "src_grouped%d" % g) for g in range(2)]
        src_codes = early_tile(4, U32, "src_codes")
        wf_tile = early_tile(5, BF16, "wf_tile")
        wf_rows, wf_grouped, f_grouped = wf_tile[:, 0:512], wf_tile[:, 512:1024], wf_tile[:, 1024:2048]
        key_rows = early_tile(6, BF16, "key_rows")
        wf_codes = early_tile(7, U32, "wf_codes")[:, 0:P]
        scales_tile = early_tile(8, U8, "scales_tile")
        src_scales, wf_scales = scales_tile[:, 0:1024], scales_tile[:, 1024:1024 + P]
        f_codes = keep.tile([P, 256], U32, name="f_codes", align_bytes=64)
        f_scales = keep.tile([P, 256], U8, name="f_scales", align_bytes=64)
        scratch = keep.tile([P, P], F32, name="scratch")
        minus_one = keep.tile([P, 1], F32, name="minus_one")
        tgt_sq = keep.tile([P, BLOCKS], F32, name="tgt_sq")
        bank_max = keep.tile([P, 2 * BLOCKS], F32, name="bank_max")
        row_max = keep.tile([P, BLOCKS], F32, name="row_max")
        min_d2 = keep.tile([P, BLOCKS], F32, name="min_d2")
        min_dist = keep.tile([P, BLOCKS], F32, name="min_dist")
        exp_bias = keep.tile([P, BLOCKS], F32, name="exp_bias")
        row_sum = keep.tile([P, BLOCKS], F32, name="row_sum")
        inv_sum = keep.tile([P, BLOCKS], F32, name="inv_sum")
        squares = keep.tile([P, 1024], F32, name="squares")
        tgt_rows = [keep.tile([P, 1024], BF16, name="tgt_rows%d" % i) for i in range(3)]
        tgtT = [keep.tile([P, 1024], BF16, name="tgtT%d" % i) for i in range(2)]
        dist = [keep.tile([P, KEYS], F32, name="dist%d" % i, align_bytes=64) for i in range(DIST_SLOTS - SRC_SLOTS)]
        grouped = [keep.tile([P, 4 * KEYS], BF16, name="grouped%d" % i, align_bytes=64) for i in range(2)]
        codes = [keep.tile([P, 1024], U32, name="codes%d" % i, align_bytes=64) for i in range(2)]
        scales = [keep.tile([P, 1024], U8, name="scales%d" % i, align_bytes=64) for i in range(2)]
        out_sb = [keep.tile([P, 512], F32, name="out_sb%d" % i) for i in range(2)]
        bank = {}
        turns = []
        back_turns = []

        def next_bank():
            turns.append(len(turns) % RING)
            return "R%d" % turns[-1]

        def next_back_bank():
            back_turns.append(len(back_turns) % BACK_RING)
            return "B%d" % back_turns[-1]

        def transpose8(rows, tag):
            pb = psum.tile([P, 1024], BF16, name="pb", tag=tag)
            for i in range(8):
                nc.tensor.transpose(pb[:, i * P:(i + 1) * P], rows[:, i * P:(i + 1) * P], ident_b[:])
            return pb

        def load_octet(o):
            nc.sync.dma_start(out=tgt_rows[o % 3][:], in_=target[o * 1024:(o + 1) * 1024, :].rearrange("(p i) e -> p (i e)", i=8))

        def octet_transpose(o):
            bank["x", o] = transpose8(tgt_rows[o % 3], next_back_bank() if o > 0 else next_bank())

        def octet_copy(o):
            nc.vector.tensor_copy(out=tgtT[o % 2][:], in_=bank["x", o][:])

        def octet_square(o, lo, hi):
            rows = tgt_rows[o % 3]
            nc.gpsimd.tensor_tensor(out=squares[:, lo:hi], in0=rows[:, lo:hi], in1=rows[:, lo:hi], op=ALU.mult)

        def octet_fold(o, width):
            v = squares[:].rearrange("p (i e) -> p i e", i=8)
            dst = v[:, :, 0:width] if width > 1 else tgt_sq[:, 8 * o:8 * o + 8].unsqueeze(2)
            nc.gpsimd.tensor_tensor(out=dst, in0=v[:, :, 0:width], in1=v[:, :, width:2 * width], op=ALU.add)

        def front_tensor(a):
            o, i = divmod(a, 8)
            for g in range(2):
                yb = psum.tile([P, 512], F32, name="yb", tag=next_bank())
                for t in range(4):
                    nc.tensor.matmul(yb[:, t * P:(t + 1) * P], lhsT=neg_key_sq[:, 4 * g + t:4 * g + t + 1].to_broadcast([P, P]), rhs=ident_f[:], is_transpose=True, start=(t == 0), stop=False)
                bank["y", a, g] = yb
            for g in range(2):
                nc.tensor.matmul(bank["y", a, g][:], lhsT=tgtT[o % 2][:, i * P:(i + 1) * P], rhs=keysT[:, g * 512:(g + 1) * 512], start=False, stop=True)

        def front_vector(a):
            for g in range(2):
                nc.vector.tensor_scalar(out=dist[a % DIST_SLOTS][:, g * 512:(g + 1) * 512], in0=bank["y", a, g][:], scalar1=tgt_sq[:, a:a + 1], scalar2=None,
                                        op0=ALU.min, op1=ALU.max, accum_out=bank_max[:, 2 * a + g:2 * a + g + 1])

        def group_min_d2(a0, a1):
            nc.vector.tensor_reduce(out=row_max[:, a0:a1], in_=bank_max[:, 2 * a0:2 * a1].rearrange("p (a h) -> p a h", h=2), axis=AX.X, op=ALU.max)
            nc.gpsimd.tensor_tensor(out=min_d2[:, a0:a1], in0=tgt_sq[:, a0:a1], in1=row_max[:, a0:a1], op=ALU.subtract)

        def scalar_sqrt(a):
            nc.scalar.activation(out=dist[a % DIST_SLOTS][:], in_=dist[a % DIST_SLOTS][:], func=ACT.Sqrt, bias=tgt_sq[:, a:a + 1], scale=-1.0)

        def scalar_group_bias(a0, a1):
            nc.scalar.activation(out=min_dist[:, a0:a1], in_=min_d2[:, a0:a1], func=ACT.Sqrt)
            nc.gpsimd.tensor_scalar(out=exp_bias[:, a0:a1], in0=min_dist[:, a0:a1], scalar1=INV_ROOT, scalar2=0.0, op0=ALU.mult, op1=ALU.add)

        def e_rows(a):
            return dist[a % DIST_SLOTS][:].bitcast(BF16)[:, 0:KEYS]

        def scalar_exp(a):
            nc.scalar.activation(out=e_rows(a), in_=dist[a % DIST_SLOTS][:], func=ACT.Exp, bias=exp_bias[:, a:a + 1], scale=-INV_ROOT, accum_out=row_sum[:, a:a + 1])

        def back_transpose(b):
            bank["t", b] = words_transpose(next_back_bank(), e_rows(b), 2)

        def back_copy(b):
            words_copy(nc.vector.tensor_copy, bank["t", b], grouped[b // 4 % 2][:, (b % 4) * KEYS:(b % 4 + 1) * KEYS], 2)

        def quantise(q, i0=0, i1=4):
            nc.vector.quantize_mx(out=codes[q % 2][:, i0 * 256:i1 * 256].bitcast(FP8X4), scales=scales[q % 2][:, i0 * 256:i1 * 256],
                                  in_=grouped[q % 2][:, i0 * KEYS:i1 * KEYS])

        def products(q, i0=0, i1=4):
            if i0 == 0:
                bank["o", q] = psum.tile([P, 512], F32, name="ob", tag=next_back_bank() if q < WHOLE_QUADS else next_bank())
            ob = bank["o", q]
            for i in range(i0, i1):
                for g in range(2):
                    c0 = i * 256 + g * P
                    nc.tensor.matmul_mx(out=ob[:, i * P:(i + 1) * P], lhsT=codes[q % 2][:, c0:c0 + P].bitcast(FP8X4), lhsT_scale=scales[q % 2][:, c0:c0 + P],
                                        rhs=f_codes[:, g * P:(g + 1) * P].bitcast(FP8X4), rhs_scale=f_scales[:, g * P:(g + 1) * P], start=(g == 0), stop=(g == 1))

        def reciprocals(q, i0=0, i1=4):
            b0, b1 = 4 * q + i0, 4 * q + i1
            nc.gpsimd.tensor_tensor(out=inv_sum[:, b0:b1], in0=row_sum[:, b0:b1], in1=minus_one[:].to_broadcast([P, b1 - b0]), op=ALU.pow)

        def finish(q, i0=0, i1=4):
            cols = slice(i0 * P, i1 * P)
            nc.vector.tensor_tensor(out=out_sb[q % 2][:, cols].rearrange("p (i d) -> p i d", d=P), in0=bank["o", q][:, cols].rearrange("p (i d) -> p i d", d=P),
                                    in1=inv_sum[:, 4 * q + i0:4 * q + i1].unsqueeze(2).to_broadcast([P, i1 - i0, P]), op=ALU.mult)
            o, h = divmod(q, 2)
            nc.sync.dma_start(out=out[o * 1024:(o + 1) * 1024, :].rearrange("(p i) d -> p (i d)", i=8)[:, h * 512 + i0 * P:h * 512 + i1 * P], in_=out_sb[q % 2][:, cols])

        def words_transpose(tag, rows, chunks):
            pw = psum.tile([P, 2 * chunks * P], F32, name="pw", tag=tag)
            for c in range(chunks):
                for u in range(2):
                    nc.tensor.transpose(pw[:, (2 * c + u) * P:(2 * c + u + 1) * P], rows[:, c * 512:(c + 1) * 512].bitcast(F32)[:, u * P:(u + 1) * P], ident_f[:])
            return pw

        def words_copy(copy, pw, dst, chunks):
            copy(out=dst.bitcast(F32).rearrange("w (c n u) -> w c n u", c=chunks, u=2), in_=pw[:].rearrange("w (c u n) -> w c n u", c=chunks, u=2))

        def wf_transpose():
            bank["wf"] = words_transpose(next_bank(), wf_rows, 1)

        def src_transpose(j):
            bank["s", j] = words_transpose(next_bank(), src_rows[j // 2][:, (j % 2) * 1024:(j % 2 + 1) * 1024], 2)

        def wf_copy():
            words_copy(nc.scalar.copy, bank["wf"], wf_grouped, 1)

        def src_copy(j):
            words_copy(nc.scalar.copy, bank["s", j], src_grouped[j // 2][:, (j % 2) * 1024:(j % 2 + 1) * 1024], 2)

        def wf_quantise():
            nc.vector.quantize_mx(out=wf_codes.bitcast(FP8X4), scales=wf_scales, in_=wf_grouped)

        def src_quantise(g):
            nc.vector.quantize_mx(out=src_codes[:, g * 512:(g + 1) * 512].bitcast(FP8X4), scales=src_scales[:, g * 512:(g + 1) * 512], in_=src_grouped[g][:])

        def f_products(g):
            fb = psum.tile([P, 512], F32, name="fb", tag=next_bank())
            for t in range(4):
                c = 4 * g + t
                nc.tensor.matmul_mx(out=fb[:, t * P:(t + 1) * P], lhsT=src_codes[:, c * P:(c + 1) * P].bitcast(FP8X4), lhsT_scale=src_scales[:, c * P:(c + 1) * P],
                                    rhs=wf_codes.bitcast(FP8X4), rhs_scale=wf_scales, start=True, stop=True)
            bank["f", g] = fb

        def f_copy(g):
            nc.scalar.copy(out=f_grouped[:, g * 512:(g + 1) * 512].rearrange("p (d t) -> p d t", t=4), in_=bank["f", g][:].rearrange("p (t d) -> p d t", t=4))

        def f_quantise():
            nc.vector.quantize_mx(out=f_codes[:].bitcast(FP8X4), scales=f_scales[:], in_=f_grouped)

        for u in range(2):
            for v in range(2):
                nc.sync.dma_start(out=key_rows[v:P:2, u * 512:(u + 1) * 512].rearrange("p (s e) -> p s e", s=4), in_=k_right.rearrange("(s p w) e -> w p s e", s=4, w=4)[2 * u + v])
        load_octet(0)
        nc.sync.dma_start(out=wf_rows, in_=WF_right)
        for g in range(2):
            nc.sync.dma_start(out=src_rows[g][:], in_=source[g * 512:(g + 1) * 512, :].rearrange("(p t) c -> p (t c)", t=4))
        load_octet(1)
        load_octet(2)
        make_identity(nc, ident_b[:])
        make_identity(nc, ident_f[:])
        nc.vector.memset(minus_one[:], -1.0)
        nc.vector.memset(scratch[:, 0:1], 1.0)
        nc.scalar.activation(out=scratch[:, 1:2], in_=scratch[:, 0:1], func=ACT.Sqrt)
        keys_bank = psum.tile([P, 1024], BF16, name="keys_bank", tag=next_bank())
        for g in range(2):
            for u in range(2):
                for h in range(2):
                    c, s = 4 * g + 2 * u + h, 4 * u + 2 * g + h
                    nc.tensor.transpose(keys_bank[:, c * P:(c + 1) * P], key_rows[:, s * P:(s + 1) * P], ident_b[:])
        octet_transpose(0)
        def key_squares(g):
            for t in range(4):
                u, h = divmod(t, 2)
                s = 4 * u + 2 * g + h
                nc.scalar.activation(out=scratch[:], in_=key_rows[:, s * P:(s + 1) * P], func=ACT.Square, accum_out=key_sq[:, 4 * g + t:4 * g + t + 1])

        def target_squares(c):
            nc.scalar.activation(out=scratch[:], in_=tgt_rows[0][:, c * P:(c + 1) * P], func=ACT.Square, accum_out=tgt_sq[:, c:c + 1])

        def key_negate(g):
            nc.vector.tensor_scalar(out=neg_key_sq[:, 4 * g:4 * g + 4], in0=key_sq[:, 4 * g:4 * g + 4], scalar1=-1.0, scalar2=None, op0=ALU.mult)

        key_squares(0)
        target_squares(0)
        key_squares(1)
        for c in range(1, 8):
            target_squares(c)
        nc.vector.tensor_scalar(out=keysT[:], in0=keys_bank[:], scalar1=2.0, scalar2=None, op0=ALU.mult)
        key_negate(0)
        octet_copy(0)
        key_negate(1)
        front_tensor(0)

        quantise_at = [4 * q + 5 for q in range(WHOLE_QUADS)]
        products_at = [4 * q + 6 for q in range(WHOLE_QUADS)]
        back_units = BLOCKS + 2
        written = {"front": 0, "back": 0, "exp": 0}
        group_ends = {}
        first = 0
        for size in GROUPS:
            group_ends[first + size - 1] = (first, first + size)
            first += size
        assert first == BLOCKS

        f0 = 1
        before = {f0: [wf_transpose], f0 + 6: [wf_quantise, lambda: src_quantise(0)], f0 + 7: [lambda: src_quantise(1), lambda: f_products(0)],
                  f0 + 8: [lambda: f_products(1)], f0 + 12: [f_quantise]}
        after = {f0: [wf_copy], f0 + 8: [lambda: f_copy(0)], f0 + 9: [lambda: f_copy(1)]}
        for j in range(4):
            before[f0 + 1 + j] = [lambda j=j: src_transpose(j)]
            after[f0 + 1 + j] = [lambda j=j: src_copy(j)]

        def front_unit(a):
            assert a - DIST_SLOTS < written["back"]
            for step in before.get(a, []):
                step()
            if a == DIST_SLOTS - SRC_SLOTS:
                dist.extend([keep.tile([P, KEYS], F32, name="dist%d" % i, align_bytes=64) for i in range(len(dist), DIST_SLOTS)])
            o, r = divmod(a, 8)
            if o == 0:
                if r < 4:
                    for lo in (r * 256, r * 256 + P):
                        octet_square(1, lo, lo + P)
                if r == 3:
                    for width in [64, 32, 16, 8, 4, 2, 1]:
                        octet_fold(1, width)
            elif r < 3 and o + 1 < OCTETS:
                for width in [[64], [32, 16], [8, 4, 2, 1]][r]:
                    octet_fold(o + 1, width)
            if r >= 4 and o + 2 < OCTETS:
                for lo in ((r - 4) * 256, (r - 4) * 256 + P):
                    octet_square(o + 2, lo, lo + P)
            if r == 0 and o + 3 < OCTETS:
                load_octet(o + 3)
            if r == (0 if o > 0 else 4) and o + 1 < OCTETS:
                octet_transpose(o + 1)
            if a + 1 < BLOCKS:
                front_tensor(a + 1)
            front_vector(a)
            if r == (0 if o > 0 else 4) and o + 1 < OCTETS:
                octet_copy(o + 1)
            if a in group_ends:
                group_min_d2(*group_ends[a])
            for step in after.get(a, []):
                step()
            written["front"] = a + 1

        def back_unit(n):
            assert n >= BLOCKS or n < written["exp"]
            if n < BLOCKS:
                back_transpose(n)
            if n in products_at:
                products(products_at.index(n))
            if n in quantise_at:
                reciprocals(quantise_at.index(n))
            if 0 <= n - 1 < BLOCKS:
                back_copy(n - 1)
            if n in quantise_at:
                quantise(quantise_at.index(n))
            if n - 1 in products_at:
                finish(products_at.index(n - 1))
            q, i = divmod(n - 2, 4)
            if WHOLE_QUADS <= q < QUADS:
                products(q, i, i + 1)
            q, i = divmod(n - 1, 4)
            if WHOLE_QUADS <= q < QUADS:
                quantise(q, i, i + 1)
            if n == BLOCKS - 3:
                reciprocals(QUADS - 2)
            if n == BLOCKS - 2:
                finish(QUADS - 2)
            if n == BLOCKS - 1:
                reciprocals(QUADS - 1, 0, 3)
            if n == BLOCKS:
                reciprocals(QUADS - 1, 3, 4)
            if n == BLOCKS + 1:
                finish(QUADS - 1, 0, 3)
                finish(QUADS - 1, 3, 4)
            written["back"] = n + 1

        def units_up_to(front, back):
            front, back = min(front, BLOCKS), min(back - BACKLOG, written["exp"])
            while written["front"] < front or written["back"] < back:
                if written["back"] < back:
                    back_unit(written["back"])
                if written["front"] < front:
                    front_unit(written["front"])

        def share(size, part):
            return size * part[0] // part[1]

        first = 0
        for k, size in enumerate(GROUPS):
            last = first + size
            lead = share(size, LEAD) if k > 0 else 0
            kept = share(GROUPS[k - 1], KEEP) if k > 0 else 0
            next_lead = share(GROUPS[k + 1], LEAD) if k + 1 < len(GROUPS) else 0
            next_kept = share(size, KEEP) if k + 1 < len(GROUPS) else 0
            for i in range(size):
                units_up_to(first + lead + ((size - lead) * (i + 1) + size - 1) // size + 1, first - kept + kept * (i + 1) // size)
                scalar_sqrt(first + i)
            scalar_group_bias(first, last)
            caught_up = BACKLOG if k + 1 == len(GROUPS) else 0
            for i in range(size):
                scalar_exp(first + i)
                written["exp"] = first + i + 1
                units_up_to(last + next_lead * (i + 1) // size + 1, first + (size - next_kept) * (i + 1) // size + caught_up * (i + 1) // size)
            first = last
        for n in range(written["back"], back_units):
            back_unit(n)
